import numpy as np
import ml_dtypes


def mxq(x, axis, fmt="e4m3"):
    dtype, down = {"e4m3": (ml_dtypes.float8_e4m3fn, 7), "e5m2": (ml_dtypes.float8_e5m2, 14)}[fmt]
    v = np.moveaxis(np.asarray(x, np.float32).astype(ml_dtypes.bfloat16).astype(np.float64), axis, -1)
    blocks = v.reshape(v.shape[:-1] + (-1, 32))
    amax = np.abs(blocks).max(-1, keepdims=True)
    byte = np.maximum(np.where(amax > 0, np.frexp(amax)[1] - 1 + 127, 0) - down, 1)
    scale = np.exp2(byte - 127.0)
    codes = (blocks / scale).astype(np.float32).astype(dtype).astype(np.float64)
    return np.moveaxis((codes * scale).reshape(v.shape), -1, axis)


WIDE = False


def mx_kscale(k):
    if not WIDE:
        return np.ones(k)
    levels = np.array([10, -10, 5, -5, 0])
    a = np.random.permutation(np.resize(levels, k // 512 * 4)).reshape(k // 512, 4)
    idx = np.arange(k)
    return np.exp2(a[idx // 512, idx % 128 // 32])


BF16 = ml_dtypes.bfloat16


def bf(x):
    return np.asarray(x, np.float32).astype(BF16)


def f64(x):
    return np.asarray(x).astype(np.float64)


B, N = 4096, 512
EPS = 1e-5
DECAY = 0.9
SLOPE = 0.01


def layer_norm(v, g, b):
    mu = v.mean(-1, keepdims=True)
    var = ((v - mu) ** 2).mean(-1, keepdims=True)
    return (v - mu) / np.sqrt(var + EPS) * g + b


def sigmoid(v):
    return 1.0 / (1.0 + np.exp(-v))


def setup_inputs():
    s = mx_kscale(N)
    rest = np.random.standard_normal(N) * 2.8 - 1.7
    return {"inputs": bf(np.random.standard_normal((B, N)) * (0.5 + np.random.random((B, 1))) + 0.3 * np.random.standard_normal((B, 1))),
            "prev_potential": bf(np.random.standard_normal((B, N)) + rest),
            "syn_weights": bf(np.random.standard_normal((N, N)) * 2.0 / np.sqrt(N) / s[:, None]),
            "gate_W": bf(np.random.standard_normal((N, N)) / np.sqrt(N)),
            "gate_b": bf(np.random.standard_normal(N) * 0.3),
            "pre_gamma": bf((1.0 + 0.1 * np.random.standard_normal(N)) * s),
            "pre_beta": bf(0.1 * np.random.standard_normal(N) * s),
            "ln_gamma": bf(1.0 + 0.1 * np.random.standard_normal(N)),
            "ln_beta": bf(0.1 * np.random.standard_normal(N))}


def reference(inputs, prev_potential, syn_weights, gate_W, gate_b, pre_gamma, pre_beta, ln_gamma, ln_beta):
    x = f64(inputs)
    x_norm = layer_norm(x, f64(pre_gamma), f64(pre_beta))
    pre = mxq(x_norm, 1, "e4m3") @ mxq(f64(syn_weights), 0, "e4m3")
    potential = DECAY * f64(prev_potential) + pre
    activation = np.where(potential >= 0, potential, SLOPE * potential)
    gate = sigmoid((mxq(x, 1, "e4m3") @ mxq(f64(gate_W), 1, "e4m3").T) + f64(gate_b))
    residual = gate * activation + (1.0 - gate) * x
    output = layer_norm(residual, f64(ln_gamma), f64(ln_beta))
    return (output, potential)

@@ -1,0 +1,241 @@
+from contextlib import ExitStack
+
+import concourse.bass as bass
+import concourse.mybir as mybir
+import concourse.tile as tile
+from concourse.masks import make_identity
+
+F32 = mybir.dt.float32
+BF16 = mybir.dt.bfloat16
+U32 = mybir.dt.uint32
+U8 = mybir.dt.uint8
+FP8X4 = mybir.dt.float8_e4m3fn_x4
+ALU = mybir.AluOpType
+ACT = mybir.ActivationFunctionType
+
+P = 128
+B = 4096
+N = 512
+NT = B // P
+GT = 4
+NG = NT // GT
+EPS = 1e-5
+DECAY = 0.9
+SLOPE = 0.01
+
+FLOPS = 2 * 2 * B * N * N
+
+
+def tile_mnelayer_pa_t_kernel(
+    tc, inputs, prev_potential, syn_weights, gate_W, gate_b, pre_gamma, pre_beta, ln_gamma, ln_beta, out_0, out_1
+):
+    nc = tc.nc
+    with ExitStack() as ctx:
+        const = ctx.enter_context(tc.tile_pool(name="const", bufs=1))
+        p2 = ctx.enter_context(tc.tile_pool(name="p2", bufs=2))
+        p3 = ctx.enter_context(tc.tile_pool(name="p3", bufs=3))
+        small = ctx.enter_context(tc.tile_pool(name="small", bufs=4))
+        psum = ctx.enter_context(tc.psum_pool(name="psum", bufs=2))
+
+        x_v = inputs.rearrange("(p i) k -> p i k", i=NT)
+        prev_v = prev_potential.rearrange("(p i) k -> p i k", i=NT)
+        out_v = out_0.rearrange("(p i) k -> p i k", i=NT)
+        pot_v = out_1.rearrange("(p i) k -> p i k", i=NT)
+
+        x_all = const.tile([P, NT, N], BF16, name="x_all")
+        prev_all = const.tile([P, NT, N], BF16, name="prev_all")
+        wg_raw = const.tile([P, GT, N], BF16, name="wg_raw")
+        ws_raw = const.tile([P, GT, N], BF16, name="ws_raw")
+        vt = const.tile([P, P], BF16, name="vt")
+        g_b = const.tile([P, N], BF16, name="g_b")
+        b_b = const.tile([P, N], BF16, name="b_b")
+        cols = const.tile([P, 12], F32, name="cols")
+        mhalf = const.tile([P, GT], F32, name="mhalf")
+        ident = const.tile([P, P], F32, name="ident")
+        identb = const.tile([P, P], BF16, name="identb")
+        junk = const.tile([P, N], BF16, name="junk")
+        ws_c = const.tile([P, N], U32, name="ws_c", align_bytes=64)
+        ws_p = const.tile([P, N], U8, name="ws_p", align_bytes=64)
+        wg_c = const.tile([P, N], U32, name="wg_c", align_bytes=64)
+        wg_p = const.tile([P, N], U8, name="wg_p", align_bytes=64)
+
+        nc.vector.memset(vt[:], 0.0)
+        nc.vector.memset(mhalf[:], -0.5)
+        make_identity(nc, ident[:])
+        make_identity(nc, identb[:])
+
+        def gsl(g):
+            return slice(g * GT, (g + 1) * GT)
+
+        nc.sync.dma_start(out=wg_raw[:], in_=gate_W.rearrange("(c m) k -> m c k", m=P))
+        nc.sync.dma_start(out=x_all[:, gsl(0), :], in_=x_v[:, gsl(0), :])
+        nc.sync.dma_start(out=vt[0:4, :], in_=pre_gamma.rearrange("(j p) -> j p", p=P))
+        nc.sync.dma_start(out=vt[4:8, :], in_=pre_beta.rearrange("(j p) -> j p", p=P))
+        nc.sync.dma_start(out=vt[8:12, :], in_=gate_b.rearrange("(j p) -> j p", p=P))
+        nc.sync.dma_start(out=ws_raw[:], in_=syn_weights.rearrange("(j p) n -> p j n", p=P))
+        nc.sync.dma_start(out=prev_all[:, gsl(0), :], in_=prev_v[:, gsl(0), :])
+        nc.sync.dma_start(out=x_all[:, gsl(1), :], in_=x_v[:, gsl(1), :])
+        nc.sync.dma_start(out=g_b[:], in_=ln_gamma.partition_broadcast(P))
+        nc.sync.dma_start(out=b_b[:], in_=ln_beta.partition_broadcast(P))
+        nc.sync.dma_start(out=prev_all[:, gsl(1), :], in_=prev_v[:, gsl(1), :])
+        for g in range(2, NG):
+            nc.sync.dma_start(out=x_all[:, gsl(g), :], in_=x_v[:, gsl(g), :])
+            nc.sync.dma_start(out=prev_all[:, gsl(g), :], in_=prev_v[:, gsl(g), :])
+
+        pv = psum.tile([P, P], BF16, name="pv", tag="tin")
+        nc.tensor.transpose(pv[:], vt[:], identb[:])
+        nc.vector.tensor_copy(out=cols[:], in_=pv[:, 0:12])
+
+        def words_to_codes(src, codes, plane):
+            grx = p2.tile([P, 4 * N], BF16, name="grx", tag="grx", align_bytes=64)
+            grx_w = grx[:].bitcast(F32).rearrange("p (c u) -> p c u", u=2)
+            for h in range(2):
+                bank = psum.tile([P, 2, 256], F32, name="xwb", tag="tin")
+                for t2 in range(2):
+                    w = src[:, 2 * h + t2, :].bitcast(F32)
+                    for u in range(2):
+                        nc.tensor.transpose(bank[:, u, t2 * P : (t2 + 1) * P], w[:, u * P : (u + 1) * P], ident[:])
+                nc.scalar.copy(out=grx_w[:, h * 256 : (h + 1) * 256, :], in_=bank[:].rearrange("p u c -> p c u"))
+            nc.vector.quantize_mx(out=codes.bitcast(FP8X4), scales=plane, in_=grx[:])
+
+        def regroup_quant(src, codes, plane):
+            grn = p2.tile([P, N, 4], BF16, name="grn", tag="grn", align_bytes=64)
+            nc.vector.tensor_copy(
+                out=grn[:].rearrange("p (c i) j -> p c j i", i=4),
+                in_=src.rearrange("p j (c i) -> p c j i", i=4),
+            )
+            nc.vector.quantize_mx(out=codes.bitcast(FP8X4), scales=plane, in_=grn[:].rearrange("p c j -> p (c j)"))
+
+        words_to_codes(wg_raw[:], wg_c[:], wg_p[:])
+        regroup_quant(ws_raw[:], ws_c[:], ws_p[:])
+
+        st = {}
+
+        def stage_a(g):
+            xs = x_all[:, gsl(g), :]
+            sx = small.tile([P, GT], F32, name="sx", tag="sx")
+            nm1 = small.tile([P, GT], F32, name="nm1", tag="nm1")
+            ss1 = small.tile([P, GT], F32, name="ss1", tag="ss1")
+            ve1 = small.tile([P, GT], F32, name="ve1", tag="ve1")
+            rstd1 = small.tile([P, GT], F32, name="rstd1", tag="rstd1")
+            nmr1 = small.tile([P, GT], F32, name="nmr1", tag="nmr1")
+            for t in range(GT):
+                nc.scalar.activation(out=junk[:], in_=xs[:, t, :], func=ACT.Identity, accum_out=sx[:, t : t + 1])
+            nc.gpsimd.tensor_scalar(out=nm1[:], in0=sx[:], scalar1=-1.0 / N, scalar2=0.0, op0=ALU.mult, op1=ALU.add)
+            for t in range(GT):
+                nc.scalar.activation(
+                    out=junk[:], in_=xs[:, t, :], func=ACT.Square, bias=nm1[:, t : t + 1], accum_out=ss1[:, t : t + 1]
+                )
+            nc.gpsimd.tensor_scalar(out=ve1[:], in0=ss1[:], scalar1=1.0 / N, scalar2=EPS, op0=ALU.mult, op1=ALU.add)
+            nc.gpsimd.tensor_tensor(out=rstd1[:], in0=ve1[:], in1=mhalf[:], op=ALU.pow)
+            nc.gpsimd.tensor_tensor(out=nmr1[:], in0=nm1[:], in1=rstd1[:], op=ALU.mult)
+            xh = p2.tile([P, GT, N], F32, name="xh", tag="xh")
+            for t in range(GT):
+                nc.scalar.activation(
+                    out=xh[:, t, :], in_=xs[:, t, :], func=ACT.Identity,
+                    scale=rstd1[:, t : t + 1], bias=nmr1[:, t : t + 1],
+                )
+            xnt = p2.tile([P, 4, N], BF16, name="xnt", tag="xnt")
+            for j in range(4):
+                bank = psum.tile([P, N], F32, name="xhb", tag="tin")
+                for t in range(GT):
+                    nc.tensor.transpose(bank[:, t * P : (t + 1) * P], xh[:, t, j * P : (j + 1) * P], ident[:])
+                nc.scalar.activation(
+                    out=xnt[:, j, :], in_=bank[:], func=ACT.Identity,
+                    scale=cols[:, j : j + 1], bias=cols[:, 4 + j : 5 + j],
+                )
+            cn = p2.tile([P, N], U32, name="cn", tag="cn", align_bytes=64)
+            pn = p2.tile([P, N], U8, name="pn", tag="pn", align_bytes=64)
+            cx = p2.tile([P, N], U32, name="cx", tag="cx", align_bytes=64)
+            px = p2.tile([P, N], U8, name="px", tag="px", align_bytes=64)
+            words_to_codes(xs, cx[:], px[:])
+            regroup_quant(xnt[:], cn[:], pn[:])
+            st[g] = {"nm1": nm1, "cn": cn, "pn": pn, "cx": cx, "px": px}
+
+        def stage_b1(g):
+            s = st[g]
+            xs = x_all[:, gsl(g), :]
+            gate_t = p2.tile([P, 4, N], F32, name="gate_t", tag="gate_t")
+            for c in range(4):
+                bank = psum.tile([P, N], F32, name="gtb", tag="gT")
+                nc.tensor.matmul_mx(
+                    out=bank[:],
+                    lhsT=wg_c[:, c * P : (c + 1) * P].bitcast(FP8X4),
+                    lhsT_scale=wg_p[:, c * P : (c + 1) * P],
+                    rhs=s["cx"][:].bitcast(FP8X4),
+                    rhs_scale=s["px"][:],
+                    start=True,
+                    stop=True,
+                )
+                nc.scalar.activation(
+                    out=gate_t[:, c, :], in_=bank[:], func=ACT.Sigmoid, bias=cols[:, 8 + c : 9 + c]
+                )
+            pot = p3.tile([P, GT, N], F32, name="pot", tag="pot")
+            wk = p3.tile([P, GT, N], F32, name="wk", tag="wk")
+            for t in range(GT):
+                bank = psum.tile([P, N], F32, name="preb", tag="pre")
+                nc.tensor.matmul_mx(
+                    out=bank[:],
+                    lhsT=s["cn"][:, t * P : (t + 1) * P].bitcast(FP8X4),
+                    lhsT_scale=s["pn"][:, t * P : (t + 1) * P],
+                    rhs=ws_c[:].bitcast(FP8X4),
+                    rhs_scale=ws_p[:],
+                    start=True,
+                    stop=True,
+                )
+                nc.vector.scalar_tensor_tensor(
+                    out=pot[:, t, :], in0=prev_all[:, g * GT + t, :], scalar=DECAY, in1=bank[:],
+                    op0=ALU.mult, op1=ALU.add,
+                )
+            nc.sync.dma_start(out=pot_v[:, gsl(g), :], in_=pot[:])
+            potf = pot[:].rearrange("p t n -> p (t n)")
+            wkf = wk[:].rearrange("p t n -> p (t n)")
+            nc.vector.scalar_tensor_tensor(out=wkf, in0=potf, scalar=SLOPE, in1=potf, op0=ALU.mult, op1=ALU.max)
+            nc.vector.tensor_tensor(out=wk[:], in0=wk[:], in1=xs, op=ALU.subtract)
+            sm = small.tile([P, GT], F32, name="sm", tag="sm")
+            mu2 = small.tile([P, GT], F32, name="mu2", tag="mu2")
+            ss2 = small.tile([P, GT], F32, name="ss2", tag="ss2")
+            ve2 = small.tile([P, GT], F32, name="ve2", tag="ve2")
+            rstd2 = small.tile([P, GT], F32, name="rstd2", tag="rstd2")
+            for t in range(GT):
+                bank = psum.tile([P, N], F32, name="gbb", tag="gb")
+                for c in range(4):
+                    nc.tensor.transpose(bank[:, c * P : (c + 1) * P], gate_t[:, c, t * P : (t + 1) * P], ident[:])
+                nc.vector.scalar_tensor_tensor(
+                    out=wk[:, t, :], in0=wk[:, t, :], scalar=1.0, in1=bank[:],
+                    op0=ALU.mult, op1=ALU.mult, accum_out=sm[:, t : t + 1],
+                )
+            nc.vector.scalar_tensor_tensor(
+                out=mu2[:], in0=sm[:], scalar=1.0 / N, in1=s["nm1"][:], op0=ALU.mult, op1=ALU.subtract
+            )
+            for t in range(GT):
+                nc.vector.scalar_tensor_tensor(
+                    out=wk[:, t, :], in0=wk[:, t, :], scalar=mu2[:, t : t + 1], in1=xs[:, t, :],
+                    op0=ALU.subtract, op1=ALU.add,
+                )
+                nc.scalar.activation(out=junk[:], in_=wk[:, t, :], func=ACT.Square, accum_out=ss2[:, t : t + 1])
+            nc.gpsimd.tensor_scalar(out=ve2[:], in0=ss2[:], scalar1=1.0 / N, scalar2=EPS, op0=ALU.mult, op1=ALU.add)
+            nc.gpsimd.tensor_tensor(out=rstd2[:], in0=ve2[:], in1=mhalf[:], op=ALU.pow)
+            s["wk"] = wk
+            s["rstd2"] = rstd2
+
+        def stage_b2(g):
+            s = st[g]
+            wk = s["wk"]
+            for t in range(GT):
+                nc.vector.scalar_tensor_tensor(
+                    out=wk[:, t, :], in0=wk[:, t, :], scalar=s["rstd2"][:, t : t + 1], in1=g_b[:],
+                    op0=ALU.mult, op1=ALU.mult,
+                )
+            nc.vector.tensor_tensor(
+                out=wk[:], in0=wk[:], in1=b_b[:].unsqueeze(1).to_broadcast([P, GT, N]), op=ALU.add
+            )
+            nc.sync.dma_start(out=out_v[:, gsl(g), :], in_=wk[:])
+
+        stage_a(0)
+        stage_a(1)
+        for g in range(NG):
+            stage_b1(g)
+            if g + 2 < NG:
+                stage_a(g + 2)
+            stage_b2(g)

@@ -1,8 +1,6 @@
 from contextlib import ExitStack
 
-import concourse.bass as bass
 import concourse.mybir as mybir
-import concourse.tile as tile
 from concourse.masks import make_identity
 
 F32 = mybir.dt.float32
@@ -31,10 +29,10 @@ def tile_mnelayer_pa_t_kernel(
 ):
     nc = tc.nc
     with ExitStack() as ctx:
+        ctx.enter_context(tc.manual_schedule())
         const = ctx.enter_context(tc.tile_pool(name="const", bufs=1))
         p2 = ctx.enter_context(tc.tile_pool(name="p2", bufs=2))
         p3 = ctx.enter_context(tc.tile_pool(name="p3", bufs=3))
-        small = ctx.enter_context(tc.tile_pool(name="small", bufs=4))
         psum = ctx.enter_context(tc.psum_pool(name="psum", bufs=2))
 
         x_v = inputs.rearrange("(p i) k -> p i k", i=NT)
@@ -51,6 +49,7 @@ def tile_mnelayer_pa_t_kernel(
         b_b = const.tile([P, N], BF16, name="b_b")
         cols = const.tile([P, 12], F32, name="cols")
         mhalf = const.tile([P, GT], F32, name="mhalf")
+        epst = const.tile([P, 1], F32, name="epst")
         ident = const.tile([P, P], F32, name="ident")
         identb = const.tile([P, P], BF16, name="identb")
         junk = const.tile([P, N], BF16, name="junk")
@@ -58,184 +57,350 @@ def tile_mnelayer_pa_t_kernel(
         ws_p = const.tile([P, N], U8, name="ws_p", align_bytes=64)
         wg_c = const.tile([P, N], U32, name="wg_c", align_bytes=64)
         wg_p = const.tile([P, N], U8, name="wg_p", align_bytes=64)
-
-        nc.vector.memset(vt[:], 0.0)
-        nc.vector.memset(mhalf[:], -0.5)
-        make_identity(nc, ident[:])
-        make_identity(nc, identb[:])
+        bst = const.tile([P, NT, 6], F32, name="bst")
+        mv = const.tile([P, NT, 2], F32, name="mv")
+        sx = const.tile([P, NT], F32, name="sx")
+        nm1 = const.tile([P, NT], F32, name="nm1")
+        ss1 = const.tile([P, NT], F32, name="ss1")
+        ve1 = const.tile([P, NT], F32, name="ve1")
+        rstd1 = const.tile([P, NT], F32, name="rstd1")
+        nmr1 = const.tile([P, NT], F32, name="nmr1")
+        sres = const.tile([P, NT], F32, name="sres")
+        nmu2 = const.tile([P, NT], F32, name="nmu2")
+        ss2 = const.tile([P, NT], F32, name="ss2")
+        ve2 = const.tile([P, NT], F32, name="ve2")
+        rstd2 = const.tile([P, NT], F32, name="rstd2")
 
         def gsl(g):
             return slice(g * GT, (g + 1) * GT)
 
-        nc.sync.dma_start(out=wg_raw[:], in_=gate_W.rearrange("(c m) k -> m c k", m=P))
+        def ok(g):
+            return 0 <= g < NG
+
+        nc.vector.memset(vt[:], 0.0)
+        nc.vector.memset(mhalf[:], -0.5)
+        nc.vector.memset(epst[:], EPS)
+        make_identity(nc, ident[:])
+        make_identity(nc, identb[:])
+
         nc.sync.dma_start(out=x_all[:, gsl(0), :], in_=x_v[:, gsl(0), :])
         nc.sync.dma_start(out=vt[0:4, :], in_=pre_gamma.rearrange("(j p) -> j p", p=P))
         nc.sync.dma_start(out=vt[4:8, :], in_=pre_beta.rearrange("(j p) -> j p", p=P))
         nc.sync.dma_start(out=vt[8:12, :], in_=gate_b.rearrange("(j p) -> j p", p=P))
-        nc.sync.dma_start(out=ws_raw[:], in_=syn_weights.rearrange("(j p) n -> p j n", p=P))
-        nc.sync.dma_start(out=prev_all[:, gsl(0), :], in_=prev_v[:, gsl(0), :])
         nc.sync.dma_start(out=x_all[:, gsl(1), :], in_=x_v[:, gsl(1), :])
+        nc.sync.dma_start(out=wg_raw[:], in_=gate_W.rearrange("(c m) k -> m c k", m=P))
+        nc.sync.dma_start(out=ws_raw[:], in_=syn_weights.rearrange("(j p) n -> p j n", p=P))
+        nc.sync.dma_start(out=x_all[:, gsl(2), :], in_=x_v[:, gsl(2), :])
+        nc.sync.dma_start(out=prev_all[:, gsl(0), :], in_=prev_v[:, gsl(0), :])
         nc.sync.dma_start(out=g_b[:], in_=ln_gamma.partition_broadcast(P))
         nc.sync.dma_start(out=b_b[:], in_=ln_beta.partition_broadcast(P))
+        nc.sync.dma_start(out=x_all[:, gsl(3), :], in_=x_v[:, gsl(3), :])
         nc.sync.dma_start(out=prev_all[:, gsl(1), :], in_=prev_v[:, gsl(1), :])
-        for g in range(2, NG):
+        for g in range(4, NG):
             nc.sync.dma_start(out=x_all[:, gsl(g), :], in_=x_v[:, gsl(g), :])
+            nc.sync.dma_start(out=prev_all[:, gsl(g - 2), :], in_=prev_v[:, gsl(g - 2), :])
+        for g in range(NG - 2, NG):
             nc.sync.dma_start(out=prev_all[:, gsl(g), :], in_=prev_v[:, gsl(g), :])
 
-        pv = psum.tile([P, P], BF16, name="pv", tag="tin")
-        nc.tensor.transpose(pv[:], vt[:], identb[:])
-        nc.vector.tensor_copy(out=cols[:], in_=pv[:, 0:12])
+        st = {}
 
-        def words_to_codes(src, codes, plane):
-            grx = p2.tile([P, 4 * N], BF16, name="grx", tag="grx", align_bytes=64)
-            grx_w = grx[:].bitcast(F32).rearrange("p (c u) -> p c u", u=2)
-            for h in range(2):
-                bank = psum.tile([P, 2, 256], F32, name="xwb", tag="tin")
-                for t2 in range(2):
-                    w = src[:, 2 * h + t2, :].bitcast(F32)
-                    for u in range(2):
-                        nc.tensor.transpose(bank[:, u, t2 * P : (t2 + 1) * P], w[:, u * P : (u + 1) * P], ident[:])
-                nc.scalar.copy(out=grx_w[:, h * 256 : (h + 1) * 256, :], in_=bank[:].rearrange("p u c -> p c u"))
-            nc.vector.quantize_mx(out=codes.bitcast(FP8X4), scales=plane, in_=grx[:])
+        def tiles(g):
+            if g not in st:
+                st[g] = {}
+            return st[g]
 
-        def regroup_quant(src, codes, plane):
+        def st_v(g):
+            for t in range(GT):
+                i = g * GT + t
+                nc.vector.bn_stats(out=bst[:, i, :], in_=x_all[:, i, :])
+                nc.vector.bn_aggr(out=mv[:, i, :], in_=bst[:, i, :])
+            nc.gpsimd.tensor_scalar(
+                out=ve1[:, gsl(g)], in0=mv[:, gsl(g), 1], scalar1=EPS, scalar2=1.0, op0=ALU.add, op1=ALU.mult
+            )
+            nc.gpsimd.tensor_tensor(out=rstd1[:, gsl(g)], in0=ve1[:, gsl(g)], in1=mhalf[:], op=ALU.pow)
+
+        def xh_v(g):
+            xh = p2.tile([P, GT, N], F32, name="xh", tag="xh")
+            tiles(g)["xh"] = xh
+            for t in range(GT):
+                i = g * GT + t
+                nc.vector.tensor_scalar(
+                    out=xh[:, t, :], in0=x_all[:, i, :], scalar1=mv[:, i, 0:1], scalar2=rstd1[:, i : i + 1],
+                    op0=ALU.subtract, op1=ALU.mult,
+                )
+
+        def st_sum(g):
+            for t in range(GT):
+                i = g * GT + t
+                nc.scalar.activation(out=junk[:], in_=x_all[:, i, :], func=ACT.Identity, accum_out=sx[:, i : i + 1])
+            nc.scalar.mul(out=nm1[:, gsl(g)], in_=sx[:, gsl(g)], mul=-1.0 / N)
+
+        def st_sq(g):
+            for t in range(GT):
+                i = g * GT + t
+                nc.scalar.activation(
+                    out=junk[:], in_=x_all[:, i, :], func=ACT.Square, bias=nm1[:, i : i + 1],
+                    accum_out=ss1[:, i : i + 1],
+                )
+            nc.scalar.activation(
+                out=ve1[:, gsl(g)], in_=ss1[:, gsl(g)], func=ACT.Identity, scale=1.0 / N, bias=epst[:, 0:1]
+            )
+            nc.gpsimd.tensor_tensor(out=rstd1[:, gsl(g)], in0=ve1[:, gsl(g)], in1=mhalf[:], op=ALU.pow)
+            nc.gpsimd.tensor_tensor(out=nmr1[:, gsl(g)], in0=nm1[:, gsl(g)], in1=rstd1[:, gsl(g)], op=ALU.mult)
+
+        def xh_s(g):
+            xh = p2.tile([P, GT, N], F32, name="xh", tag="xh")
+            tiles(g)["xh"] = xh
+            for t in range(GT):
+                i = g * GT + t
+                nc.scalar.activation(
+                    out=xh[:, t, :], in_=x_all[:, i, :], func=ACT.Identity,
+                    scale=rstd1[:, i : i + 1], bias=nmr1[:, i : i + 1],
+                )
+
+        def words_tx(src, h):
+            bank = psum.tile([P, 2, 256], F32, name="xwb", tag="tin")
+            for t2 in range(2):
+                w = src[:, 2 * h + t2, :].bitcast(F32)
+                for u in range(2):
+                    nc.tensor.transpose(bank[:, u, t2 * P : (t2 + 1) * P], w[:, u * P : (u + 1) * P], ident[:])
+            return bank
+
+        def words_out(bank, grx, h, on_vector):
+            dst = grx[:].bitcast(F32).rearrange("p (c u) -> p c u", u=2)[:, h * 256 : (h + 1) * 256, :]
+            src = bank[:].rearrange("p u c -> p c u")
+            if on_vector:
+                nc.vector.tensor_copy(out=dst, in_=src)
+            else:
+                nc.scalar.copy(out=dst, in_=src)
+
+        def tx(g, b):
+            s = tiles(g)
+            if b < 4:
+                bank = psum.tile([P, N], F32, name="xhb", tag="tin")
+                for t in range(GT):
+                    nc.tensor.transpose(bank[:, t * P : (t + 1) * P], s["xh"][:, t, b * P : (b + 1) * P], ident[:])
+            else:
+                bank = words_tx(x_all[:, gsl(g), :], b - 4)
+            s["tin%d" % b] = bank
+
+        def gbx(g, b, on_vector=False):
+            s = tiles(g)
+            if b == 0:
+                xnt = p2.tile([P, 4, N], BF16, name="xnt", tag="xnt")
+                grx = p2.tile([P, 4 * N], BF16, name="grx", tag="grx", align_bytes=64)
+                s["xnt"] = xnt
+                s["grx"] = grx
+            bank = s["tin%d" % b]
+            if b >= 4:
+                words_out(bank, s["grx"], b - 4, on_vector)
+            elif on_vector:
+                nc.vector.tensor_scalar(
+                    out=s["xnt"][:, b, :], in0=bank[:], scalar1=cols[:, b : b + 1], scalar2=cols[:, 4 + b : 5 + b],
+                    op0=ALU.mult, op1=ALU.add,
+                )
+            else:
+                nc.scalar.activation(
+                    out=s["xnt"][:, b, :], in_=bank[:], func=ACT.Identity,
+                    scale=cols[:, b : b + 1], bias=cols[:, 4 + b : 5 + b],
+                )
+
+        def regroup(src):
             grn = p2.tile([P, N, 4], BF16, name="grn", tag="grn", align_bytes=64)
             nc.vector.tensor_copy(
                 out=grn[:].rearrange("p (c i) j -> p c j i", i=4),
                 in_=src.rearrange("p j (c i) -> p c j i", i=4),
             )
-            nc.vector.quantize_mx(out=codes.bitcast(FP8X4), scales=plane, in_=grn[:].rearrange("p c j -> p (c j)"))
+            return grn
 
-        words_to_codes(wg_raw[:], wg_c[:], wg_p[:])
-        regroup_quant(ws_raw[:], ws_c[:], ws_p[:])
+        def quant(codes, plane, flat):
+            nc.vector.quantize_mx(out=codes.bitcast(FP8X4), scales=plane, in_=flat)
 
-        st = {}
-
-        def stage_a(g):
-            xs = x_all[:, gsl(g), :]
-            sx = small.tile([P, GT], F32, name="sx", tag="sx")
-            nm1 = small.tile([P, GT], F32, name="nm1", tag="nm1")
-            ss1 = small.tile([P, GT], F32, name="ss1", tag="ss1")
-            ve1 = small.tile([P, GT], F32, name="ve1", tag="ve1")
-            rstd1 = small.tile([P, GT], F32, name="rstd1", tag="rstd1")
-            nmr1 = small.tile([P, GT], F32, name="nmr1", tag="nmr1")
-            for t in range(GT):
-                nc.scalar.activation(out=junk[:], in_=xs[:, t, :], func=ACT.Identity, accum_out=sx[:, t : t + 1])
-            nc.gpsimd.tensor_scalar(out=nm1[:], in0=sx[:], scalar1=-1.0 / N, scalar2=0.0, op0=ALU.mult, op1=ALU.add)
-            for t in range(GT):
-                nc.scalar.activation(
-                    out=junk[:], in_=xs[:, t, :], func=ACT.Square, bias=nm1[:, t : t + 1], accum_out=ss1[:, t : t + 1]
-                )
-            nc.gpsimd.tensor_scalar(out=ve1[:], in0=ss1[:], scalar1=1.0 / N, scalar2=EPS, op0=ALU.mult, op1=ALU.add)
-            nc.gpsimd.tensor_tensor(out=rstd1[:], in0=ve1[:], in1=mhalf[:], op=ALU.pow)
-            nc.gpsimd.tensor_tensor(out=nmr1[:], in0=nm1[:], in1=rstd1[:], op=ALU.mult)
-            xh = p2.tile([P, GT, N], F32, name="xh", tag="xh")
-            for t in range(GT):
-                nc.scalar.activation(
-                    out=xh[:, t, :], in_=xs[:, t, :], func=ACT.Identity,
-                    scale=rstd1[:, t : t + 1], bias=nmr1[:, t : t + 1],
-                )
-            xnt = p2.tile([P, 4, N], BF16, name="xnt", tag="xnt")
-            for j in range(4):
-                bank = psum.tile([P, N], F32, name="xhb", tag="tin")
-                for t in range(GT):
-                    nc.tensor.transpose(bank[:, t * P : (t + 1) * P], xh[:, t, j * P : (j + 1) * P], ident[:])
-                nc.scalar.activation(
-                    out=xnt[:, j, :], in_=bank[:], func=ACT.Identity,
-                    scale=cols[:, j : j + 1], bias=cols[:, 4 + j : 5 + j],
-                )
+        def q(g):
+            s = tiles(g)
             cn = p2.tile([P, N], U32, name="cn", tag="cn", align_bytes=64)
             pn = p2.tile([P, N], U8, name="pn", tag="pn", align_bytes=64)
             cx = p2.tile([P, N], U32, name="cx", tag="cx", align_bytes=64)
             px = p2.tile([P, N], U8, name="px", tag="px", align_bytes=64)
-            words_to_codes(xs, cx[:], px[:])
-            regroup_quant(xnt[:], cn[:], pn[:])
-            st[g] = {"nm1": nm1, "cn": cn, "pn": pn, "cx": cx, "px": px}
+            grn = regroup(s["xnt"][:])
+            quant(cx[:], px[:], s["grx"][:])
+            quant(cn[:], pn[:], grn[:].rearrange("p c j -> p (c j)"))
+            s["cn"], s["pn"], s["cx"], s["px"] = cn, pn, cx, px
 
-        def stage_b1(g):
-            s = st[g]
-            xs = x_all[:, gsl(g), :]
-            gate_t = p2.tile([P, 4, N], F32, name="gate_t", tag="gate_t")
+        def mxp(g, t):
+            s = tiles(g)
+            bank = psum.tile([P, N], F32, name="preb", tag="pre")
+            nc.tensor.matmul_mx(
+                out=bank[:],
+                lhsT=s["cn"][:, t * P : (t + 1) * P].bitcast(FP8X4),
+                lhsT_scale=s["pn"][:, t * P : (t + 1) * P],
+                rhs=ws_c[:].bitcast(FP8X4),
+                rhs_scale=ws_p[:],
+                start=True,
+                stop=True,
+            )
+            s["pre%d" % t] = bank
+
+        def mxg(g, c):
+            s = tiles(g)
+            bank = psum.tile([P, N], F32, name="gtb", tag="gT")
+            nc.tensor.matmul_mx(
+                out=bank[:],
+                lhsT=wg_c[:, c * P : (c + 1) * P].bitcast(FP8X4),
+                lhsT_scale=wg_p[:, c * P : (c + 1) * P],
+                rhs=s["cx"][:].bitcast(FP8X4),
+                rhs_scale=s["px"][:],
+                start=True,
+                stop=True,
+            )
+            s["gT%d" % c] = bank
+
+        def sig(g, c):
+            s = tiles(g)
+            if c == 0:
+                gate_t = p2.tile([P, 4, N], F32, name="gate_t", tag="gate_t")
+                s["gate_t"] = gate_t
+            nc.scalar.activation(
+                out=s["gate_t"][:, c, :], in_=s["gT%d" % c][:], func=ACT.Sigmoid, bias=cols[:, 8 + c : 9 + c]
+            )
+
+        def tb(g, t):
+            s = tiles(g)
+            bank = psum.tile([P, N], F32, name="gbb", tag="gb")
             for c in range(4):
-                bank = psum.tile([P, N], F32, name="gtb", tag="gT")
-                nc.tensor.matmul_mx(
-                    out=bank[:],
-                    lhsT=wg_c[:, c * P : (c + 1) * P].bitcast(FP8X4),
-                    lhsT_scale=wg_p[:, c * P : (c + 1) * P],
-                    rhs=s["cx"][:].bitcast(FP8X4),
-                    rhs_scale=s["px"][:],
-                    start=True,
-                    stop=True,
-                )
-                nc.scalar.activation(
-                    out=gate_t[:, c, :], in_=bank[:], func=ACT.Sigmoid, bias=cols[:, 8 + c : 9 + c]
-                )
-            pot = p3.tile([P, GT, N], F32, name="pot", tag="pot")
+                nc.tensor.transpose(bank[:, c * P : (c + 1) * P], s["gate_t"][:, c, t * P : (t + 1) * P], ident[:])
+            s["gb%d" % t] = bank
+
+        def pot_op(g, t):
+            s = tiles(g)
+            if t == 0:
+                pot = p2.tile([P, GT, N], F32, name="pot", tag="pot")
+                s["pot"] = pot
+            nc.vector.scalar_tensor_tensor(
+                out=s["pot"][:, t, :], in0=prev_all[:, g * GT + t, :], scalar=DECAY, in1=s["pre%d" % t][:],
+                op0=ALU.mult, op1=ALU.add,
+            )
+
+        def pld_tail(g):
+            s = tiles(g)
+            nc.sync.dma_start(out=pot_v[:, gsl(g), :], in_=s["pot"][:])
             wk = p3.tile([P, GT, N], F32, name="wk", tag="wk")
-            for t in range(GT):
-                bank = psum.tile([P, N], F32, name="preb", tag="pre")
-                nc.tensor.matmul_mx(
-                    out=bank[:],
-                    lhsT=s["cn"][:, t * P : (t + 1) * P].bitcast(FP8X4),
-                    lhsT_scale=s["pn"][:, t * P : (t + 1) * P],
-                    rhs=ws_c[:].bitcast(FP8X4),
-                    rhs_scale=ws_p[:],
-                    start=True,
-                    stop=True,
-                )
-                nc.vector.scalar_tensor_tensor(
-                    out=pot[:, t, :], in0=prev_all[:, g * GT + t, :], scalar=DECAY, in1=bank[:],
-                    op0=ALU.mult, op1=ALU.add,
-                )
-            nc.sync.dma_start(out=pot_v[:, gsl(g), :], in_=pot[:])
-            potf = pot[:].rearrange("p t n -> p (t n)")
+            s["wk"] = wk
+            potf = s["pot"][:].rearrange("p t n -> p (t n)")
             wkf = wk[:].rearrange("p t n -> p (t n)")
             nc.vector.scalar_tensor_tensor(out=wkf, in0=potf, scalar=SLOPE, in1=potf, op0=ALU.mult, op1=ALU.max)
-            nc.vector.tensor_tensor(out=wk[:], in0=wk[:], in1=xs, op=ALU.subtract)
-            sm = small.tile([P, GT], F32, name="sm", tag="sm")
-            mu2 = small.tile([P, GT], F32, name="mu2", tag="mu2")
-            ss2 = small.tile([P, GT], F32, name="ss2", tag="ss2")
-            ve2 = small.tile([P, GT], F32, name="ve2", tag="ve2")
-            rstd2 = small.tile([P, GT], F32, name="rstd2", tag="rstd2")
+            nc.vector.tensor_tensor(out=wk[:], in0=wk[:], in1=x_all[:, gsl(g), :], op=ALU.subtract)
+
+        def m_op(g, t):
+            s = tiles(g)
+            nc.vector.tensor_tensor(out=s["wk"][:, t, :], in0=s["wk"][:, t, :], in1=s["gb%d" % t][:], op=ALU.mult)
+
+        def res(g):
+            s = tiles(g)
             for t in range(GT):
-                bank = psum.tile([P, N], F32, name="gbb", tag="gb")
+                i = g * GT + t
+                nc.vector.scalar_tensor_tensor(
+                    out=s["wk"][:, t, :], in0=s["wk"][:, t, :], scalar=1.0, in1=x_all[:, i, :],
+                    op0=ALU.mult, op1=ALU.add, accum_out=sres[:, i : i + 1],
+                )
+
+        def sq2(g):
+            s = tiles(g)
+            nc.scalar.mul(out=nmu2[:, gsl(g)], in_=sres[:, gsl(g)], mul=-1.0 / N)
+            for t in range(GT):
+                i = g * GT + t
+                nc.scalar.activation(
+                    out=junk[:], in_=s["wk"][:, t, :], func=ACT.Square, bias=nmu2[:, i : i + 1],
+                    accum_out=ss2[:, i : i + 1],
+                )
+            nc.scalar.activation(
+                out=ve2[:, gsl(g)], in_=ss2[:, gsl(g)], func=ACT.Identity, scale=1.0 / N, bias=epst[:, 0:1]
+            )
+            nc.gpsimd.tensor_tensor(out=rstd2[:, gsl(g)], in0=ve2[:, gsl(g)], in1=mhalf[:], op=ALU.pow)
+
+        def o_op(g):
+            s = tiles(g)
+            for t in range(GT):
+                i = g * GT + t
+                nc.vector.scalar_tensor_tensor(
+                    out=s["wk"][:, t, :], in0=s["wk"][:, t, :], scalar=nmu2[:, i : i + 1], in1=g_b[:],
+                    op0=ALU.add, op1=ALU.mult,
+                )
+            for t in range(GT):
+                i = g * GT + t
+                nc.vector.scalar_tensor_tensor(
+                    out=s["wk"][:, t, :], in0=s["wk"][:, t, :], scalar=rstd2[:, i : i + 1], in1=b_b[:],
+                    op0=ALU.mult, op1=ALU.add,
+                )
+            nc.sync.dma_start(out=out_v[:, gsl(g), :], in_=s["wk"][:])
+
+        st_v(0)
+        st_v(1)
+        pv = psum.tile([P, P], BF16, name="pv", tag="tin")
+        nc.tensor.transpose(pv[:], vt[:], identb[:])
+        nc.vector.tensor_copy(out=cols[:], in_=pv[:, 0:12])
+        grw = p2.tile([P, 4 * N], BF16, name="grw", tag="grx", align_bytes=64)
+        for h in range(2):
+            wb = words_tx(wg_raw[:], h)
+            words_out(wb, grw, h, False)
+        xh_v(0)
+        tx(0, 0)
+        tx(0, 1)
+        quant(wg_c[:], wg_p[:], grw[:])
+        grs = regroup(ws_raw[:])
+        for b in range(6):
+            gbx(0, b, b % 2 == 1)
+            if b + 2 < 6:
+                tx(0, b + 2)
+        quant(ws_c[:], ws_p[:], grs[:].rearrange("p c j -> p (c j)"))
+        xh_v(1)
+        tx(1, 0)
+        tx(1, 1)
+        st_sum(2)
+
+        def iteration(g):
+            if ok(g):
+                for t in range(GT):
+                    m_op(g, t)
+                    if t + 2 < GT:
+                        tb(g, t + 2)
+            if ok(g + 2) and g >= 0:
+                xh_s(g + 2)
+                tx(g + 2, 0)
+                tx(g + 2, 1)
+            if ok(g + 1):
+                q(g + 1)
+            if ok(g + 3) and g >= 0:
+                st_sum(g + 3)
+            if ok(g + 1):
+                mxp(g + 1, 0)
+                mxp(g + 1, 1)
+                mxg(g + 1, 0)
+                mxg(g + 1, 1)
                 for c in range(4):
-                    nc.tensor.transpose(bank[:, c * P : (c + 1) * P], gate_t[:, c, t * P : (t + 1) * P], ident[:])
-                nc.vector.scalar_tensor_tensor(
-                    out=wk[:, t, :], in0=wk[:, t, :], scalar=1.0, in1=bank[:],
-                    op0=ALU.mult, op1=ALU.mult, accum_out=sm[:, t : t + 1],
-                )
-            nc.vector.scalar_tensor_tensor(
-                out=mu2[:], in0=sm[:], scalar=1.0 / N, in1=s["nm1"][:], op0=ALU.mult, op1=ALU.subtract
-            )
-            for t in range(GT):
-                nc.vector.scalar_tensor_tensor(
-                    out=wk[:, t, :], in0=wk[:, t, :], scalar=mu2[:, t : t + 1], in1=xs[:, t, :],
-                    op0=ALU.subtract, op1=ALU.add,
-                )
-                nc.scalar.activation(out=junk[:], in_=wk[:, t, :], func=ACT.Square, accum_out=ss2[:, t : t + 1])
-            nc.gpsimd.tensor_scalar(out=ve2[:], in0=ss2[:], scalar1=1.0 / N, scalar2=EPS, op0=ALU.mult, op1=ALU.add)
-            nc.gpsimd.tensor_tensor(out=rstd2[:], in0=ve2[:], in1=mhalf[:], op=ALU.pow)
-            s["wk"] = wk
-            s["rstd2"] = rstd2
+                    sig(g + 1, c)
+                    if c + 2 < 4:
+                        mxg(g + 1, c + 2)
+                tb(g + 1, 0)
+                tb(g + 1, 1)
+            if ok(g):
+                res(g)
+                sq2(g)
+            if ok(g + 1):
+                for t in range(GT):
+                    pot_op(g + 1, t)
+                    if t + 2 < GT:
+                        mxp(g + 1, t + 2)
+                pld_tail(g + 1)
+            if ok(g + 3):
+                st_sq(g + 3)
+            if ok(g + 2):
+                for b in range(6):
+                    gbx(g + 2, b)
+                    if b + 2 < 6:
+                        tx(g + 2, b + 2)
+            if ok(g):
+                o_op(g)
 
-        def stage_b2(g):
-            s = st[g]
-            wk = s["wk"]
-            for t in range(GT):
-                nc.vector.scalar_tensor_tensor(
-                    out=wk[:, t, :], in0=wk[:, t, :], scalar=s["rstd2"][:, t : t + 1], in1=g_b[:],
-                    op0=ALU.mult, op1=ALU.mult,
-                )
-            nc.vector.tensor_tensor(
-                out=wk[:], in0=wk[:], in1=b_b[:].unsqueeze(1).to_broadcast([P, GT, N]), op=ALU.add
-            )
-            nc.sync.dma_start(out=out_v[:, gsl(g), :], in_=wk[:])
-
-        stage_a(0)
-        stage_a(1)
-        for g in range(NG):
-            stage_b1(g)
-            if g + 2 < NG:
-                stage_a(g + 2)
-            stage_b2(g)
+        for g in range(-1, NG):
+            iteration(g)

@@ -23,6 +23,10 @@ SLOPE = 0.01
 
 FLOPS = 2 * 2 * B * N * N
 
+D_ON_G = True
+XH_ON_G = True
+O_MODE = "xh2g"
+
 
 def tile_mnelayer_pa_t_kernel(
     tc, inputs, prev_potential, syn_weights, gate_W, gate_b, pre_gamma, pre_beta, ln_gamma, ln_beta, out_0, out_1
@@ -32,7 +36,7 @@ def tile_mnelayer_pa_t_kernel(
         ctx.enter_context(tc.manual_schedule())
         const = ctx.enter_context(tc.tile_pool(name="const", bufs=1))
         p2 = ctx.enter_context(tc.tile_pool(name="p2", bufs=2))
-        p3 = ctx.enter_context(tc.tile_pool(name="p3", bufs=3))
+        p4 = ctx.enter_context(tc.tile_pool(name="p4", bufs=4))
         psum = ctx.enter_context(tc.psum_pool(name="psum", bufs=2))
 
         x_v = inputs.rearrange("(p i) k -> p i k", i=NT)
@@ -70,6 +74,7 @@ def tile_mnelayer_pa_t_kernel(
         ss2 = const.tile([P, NT], F32, name="ss2")
         ve2 = const.tile([P, NT], F32, name="ve2")
         rstd2 = const.tile([P, NT], F32, name="rstd2")
+        nmr2 = const.tile([P, NT], F32, name="nmr2")
 
         def gsl(g):
             return slice(g * GT, (g + 1) * GT)
@@ -146,7 +151,8 @@ def tile_mnelayer_pa_t_kernel(
                 out=ve1[:, gsl(g)], in_=ss1[:, gsl(g)], func=ACT.Identity, scale=1.0 / N, bias=epst[:, 0:1]
             )
             nc.gpsimd.tensor_tensor(out=rstd1[:, gsl(g)], in0=ve1[:, gsl(g)], in1=mhalf[:], op=ALU.pow)
-            nc.gpsimd.tensor_tensor(out=nmr1[:, gsl(g)], in0=nm1[:, gsl(g)], in1=rstd1[:, gsl(g)], op=ALU.mult)
+            if not XH_ON_G:
+                nc.gpsimd.tensor_tensor(out=nmr1[:, gsl(g)], in0=nm1[:, gsl(g)], in1=rstd1[:, gsl(g)], op=ALU.mult)
 
         def xh_s(g):
             xh = p2.tile([P, GT, N], F32, name="xh", tag="xh")
@@ -156,6 +162,16 @@ def tile_mnelayer_pa_t_kernel(
                 nc.scalar.activation(
                     out=xh[:, t, :], in_=x_all[:, i, :], func=ACT.Identity,
                     scale=rstd1[:, i : i + 1], bias=nmr1[:, i : i + 1],
+                )
+
+        def xh_g(g):
+            xh = p2.tile([P, GT, N], F32, name="xh", tag="xh")
+            tiles(g)["xh"] = xh
+            for t in range(GT):
+                i = g * GT + t
+                nc.gpsimd.tensor_scalar(
+                    out=xh[:, t, :], in0=x_all[:, i, :], scalar1=nm1[:, i : i + 1], scalar2=rstd1[:, i : i + 1],
+                    op0=ALU.add, op1=ALU.mult,
                 )
 
         def words_tx(src, h):
@@ -284,12 +300,15 @@ def tile_mnelayer_pa_t_kernel(
         def pld_tail(g):
             s = tiles(g)
             nc.sync.dma_start(out=pot_v[:, gsl(g), :], in_=s["pot"][:])
-            wk = p3.tile([P, GT, N], F32, name="wk", tag="wk")
+            wk = p4.tile([P, GT, N], F32, name="wk", tag="wk")
             s["wk"] = wk
             potf = s["pot"][:].rearrange("p t n -> p (t n)")
             wkf = wk[:].rearrange("p t n -> p (t n)")
             nc.vector.scalar_tensor_tensor(out=wkf, in0=potf, scalar=SLOPE, in1=potf, op0=ALU.mult, op1=ALU.max)
-            nc.vector.tensor_tensor(out=wk[:], in0=wk[:], in1=x_all[:, gsl(g), :], op=ALU.subtract)
+            if D_ON_G:
+                nc.gpsimd.tensor_tensor(out=wk[:], in0=wk[:], in1=x_all[:, gsl(g), :], op=ALU.subtract)
+            else:
+                nc.vector.tensor_tensor(out=wk[:], in0=wk[:], in1=x_all[:, gsl(g), :], op=ALU.subtract)
 
         def m_op(g, t):
             s = tiles(g)
@@ -317,6 +336,33 @@ def tile_mnelayer_pa_t_kernel(
                 out=ve2[:, gsl(g)], in_=ss2[:, gsl(g)], func=ACT.Identity, scale=1.0 / N, bias=epst[:, 0:1]
             )
             nc.gpsimd.tensor_tensor(out=rstd2[:, gsl(g)], in0=ve2[:, gsl(g)], in1=mhalf[:], op=ALU.pow)
+            if O_MODE != "stt":
+                nc.gpsimd.tensor_tensor(out=nmr2[:, gsl(g)], in0=nmu2[:, gsl(g)], in1=rstd2[:, gsl(g)], op=ALU.mult)
+
+        def xh2(g):
+            s = tiles(g)
+            for t in range(GT):
+                i = g * GT + t
+                nc.scalar.activation(
+                    out=s["wk"][:, t, :], in_=s["wk"][:, t, :], func=ACT.Identity,
+                    scale=rstd2[:, i : i + 1], bias=nmr2[:, i : i + 1],
+                )
+
+        def o_wide(g):
+            s = tiles(g)
+            wk = s["wk"]
+            nc.vector.tensor_tensor(
+                out=wk[:], in0=wk[:], in1=g_b[:].unsqueeze(1).to_broadcast([P, GT, N]), op=ALU.mult
+            )
+            if O_MODE == "xh2g":
+                nc.gpsimd.tensor_tensor(
+                    out=wk[:], in0=wk[:], in1=b_b[:].unsqueeze(1).to_broadcast([P, GT, N]), op=ALU.add
+                )
+            else:
+                nc.vector.tensor_tensor(
+                    out=wk[:], in0=wk[:], in1=b_b[:].unsqueeze(1).to_broadcast([P, GT, N]), op=ALU.add
+                )
+            nc.sync.dma_start(out=out_v[:, gsl(g), :], in_=wk[:])
 
         def o_op(g):
             s = tiles(g)
@@ -343,6 +389,7 @@ def tile_mnelayer_pa_t_kernel(
         for h in range(2):
             wb = words_tx(wg_raw[:], h)
             words_out(wb, grw, h, False)
+        st_sum(2)
         xh_v(0)
         tx(0, 0)
         tx(0, 1)
@@ -352,11 +399,16 @@ def tile_mnelayer_pa_t_kernel(
             gbx(0, b, b % 2 == 1)
             if b + 2 < 6:
                 tx(0, b + 2)
+        st_sq(2)
         quant(ws_c[:], ws_p[:], grs[:].rearrange("p c j -> p (c j)"))
         xh_v(1)
         tx(1, 0)
         tx(1, 1)
-        st_sum(2)
+        q(0)
+        mxp(0, 0)
+        mxp(0, 1)
+        mxg(0, 0)
+        mxg(0, 1)
 
         def iteration(g):
             if ok(g):
@@ -364,19 +416,28 @@ def tile_mnelayer_pa_t_kernel(
                     m_op(g, t)
                     if t + 2 < GT:
                         tb(g, t + 2)
-            if ok(g + 2) and g >= 0:
-                xh_s(g + 2)
-                tx(g + 2, 0)
-                tx(g + 2, 1)
+            if ok(g - 1) and O_MODE != "stt":
+                xh2(g - 1)
+            if ok(g + 3):
+                if XH_ON_G:
+                    xh_g(g + 3)
+                else:
+                    xh_s(g + 3)
+            for b in range(6):
+                if ok(g + 2):
+                    gbx(g + 2, b)
+                    if b + 2 < 6:
+                        tx(g + 2, b + 2)
+                if ok(g + 1) and b < GT:
+                    pot_op(g + 1, b)
+                    if b + 2 < GT:
+                        mxp(g + 1, b + 2)
             if ok(g + 1):
-                q(g + 1)
-            if ok(g + 3) and g >= 0:
-                st_sum(g + 3)
+                pld_tail(g + 1)
+            if ok(g + 3):
+                tx(g + 3, 0)
+                tx(g + 3, 1)
             if ok(g + 1):
-                mxp(g + 1, 0)
-                mxp(g + 1, 1)
-                mxg(g + 1, 0)
-                mxg(g + 1, 1)
                 for c in range(4):
                     sig(g + 1, c)
                     if c + 2 < 4:
@@ -385,22 +446,23 @@ def tile_mnelayer_pa_t_kernel(
                 tb(g + 1, 1)
             if ok(g):
                 res(g)
-                sq2(g)
-            if ok(g + 1):
-                for t in range(GT):
-                    pot_op(g + 1, t)
-                    if t + 2 < GT:
-                        mxp(g + 1, t + 2)
-                pld_tail(g + 1)
-            if ok(g + 3):
-                st_sq(g + 3)
-            if ok(g + 2):
-                for b in range(6):
-                    gbx(g + 2, b)
-                    if b + 2 < 6:
-                        tx(g + 2, b + 2)
+            if ok(g + 4):
+                st_sum(g + 4)
             if ok(g):
-                o_op(g)
+                sq2(g)
+            if ok(g - 1):
+                if O_MODE == "stt":
+                    o_op(g - 1)
+                else:
+                    o_wide(g - 1)
+            if ok(g + 4):
+                st_sq(g + 4)
+            if ok(g + 2):
+                q(g + 2)
+                mxp(g + 2, 0)
+                mxp(g + 2, 1)
+                mxg(g + 2, 0)
+                mxg(g + 2, 1)
 
-        for g in range(-1, NG):
+        for g in range(-1, NG + 1):
             iteration(g)

@@ -23,10 +23,6 @@ SLOPE = 0.01
 
 FLOPS = 2 * 2 * B * N * N
 
-D_ON_G = True
-XH_ON_G = True
-O_MODE = "xh2g"
-
 
 def tile_mnelayer_pa_t_kernel(
     tc, inputs, prev_potential, syn_weights, gate_W, gate_b, pre_gamma, pre_beta, ln_gamma, ln_beta, out_0, out_1
@@ -36,8 +32,9 @@ def tile_mnelayer_pa_t_kernel(
         ctx.enter_context(tc.manual_schedule())
         const = ctx.enter_context(tc.tile_pool(name="const", bufs=1))
         p2 = ctx.enter_context(tc.tile_pool(name="p2", bufs=2))
-        p4 = ctx.enter_context(tc.tile_pool(name="p4", bufs=4))
-        psum = ctx.enter_context(tc.psum_pool(name="psum", bufs=2))
+        p3 = ctx.enter_context(tc.tile_pool(name="p3", bufs=3))
+        ps_s = ctx.enter_context(tc.psum_pool(name="ps_s", bufs=3))
+        ps_v = ctx.enter_context(tc.psum_pool(name="ps_v", bufs=5))
 
         x_v = inputs.rearrange("(p i) k -> p i k", i=NT)
         prev_v = prev_potential.rearrange("(p i) k -> p i k", i=NT)
@@ -56,7 +53,8 @@ def tile_mnelayer_pa_t_kernel(
         epst = const.tile([P, 1], F32, name="epst")
         ident = const.tile([P, P], F32, name="ident")
         identb = const.tile([P, P], BF16, name="identb")
-        junk = const.tile([P, N], BF16, name="junk")
+        junk = const.tile([P, 8, N], BF16, name="junk")
+        jn = [0]
         ws_c = const.tile([P, N], U32, name="ws_c", align_bytes=64)
         ws_p = const.tile([P, N], U8, name="ws_p", align_bytes=64)
         wg_c = const.tile([P, N], U32, name="wg_c", align_bytes=64)
@@ -74,7 +72,6 @@ def tile_mnelayer_pa_t_kernel(
         ss2 = const.tile([P, NT], F32, name="ss2")
         ve2 = const.tile([P, NT], F32, name="ve2")
         rstd2 = const.tile([P, NT], F32, name="rstd2")
-        nmr2 = const.tile([P, NT], F32, name="nmr2")
 
         def gsl(g):
             return slice(g * GT, (g + 1) * GT)
@@ -88,24 +85,30 @@ def tile_mnelayer_pa_t_kernel(
         make_identity(nc, ident[:])
         make_identity(nc, identb[:])
 
-        nc.sync.dma_start(out=x_all[:, gsl(0), :], in_=x_v[:, gsl(0), :])
+        def load_x(g):
+            nc.sync.dma_start(out=x_all[:, gsl(g), :], in_=x_v[:, gsl(g), :])
+
+        def load_prev(g):
+            nc.sync.dma_start(out=prev_all[:, gsl(g), :], in_=prev_v[:, gsl(g), :])
+
+        load_x(0)
         nc.sync.dma_start(out=vt[0:4, :], in_=pre_gamma.rearrange("(j p) -> j p", p=P))
         nc.sync.dma_start(out=vt[4:8, :], in_=pre_beta.rearrange("(j p) -> j p", p=P))
         nc.sync.dma_start(out=vt[8:12, :], in_=gate_b.rearrange("(j p) -> j p", p=P))
-        nc.sync.dma_start(out=x_all[:, gsl(1), :], in_=x_v[:, gsl(1), :])
-        nc.sync.dma_start(out=wg_raw[:], in_=gate_W.rearrange("(c m) k -> m c k", m=P))
         nc.sync.dma_start(out=ws_raw[:], in_=syn_weights.rearrange("(j p) n -> p j n", p=P))
-        nc.sync.dma_start(out=x_all[:, gsl(2), :], in_=x_v[:, gsl(2), :])
-        nc.sync.dma_start(out=prev_all[:, gsl(0), :], in_=prev_v[:, gsl(0), :])
+        load_x(1)
+        load_x(2)
+        nc.sync.dma_start(out=wg_raw[:], in_=gate_W.rearrange("(c m) k -> m c k", m=P))
+        load_prev(0)
+        load_x(3)
         nc.sync.dma_start(out=g_b[:], in_=ln_gamma.partition_broadcast(P))
         nc.sync.dma_start(out=b_b[:], in_=ln_beta.partition_broadcast(P))
-        nc.sync.dma_start(out=x_all[:, gsl(3), :], in_=x_v[:, gsl(3), :])
-        nc.sync.dma_start(out=prev_all[:, gsl(1), :], in_=prev_v[:, gsl(1), :])
+        load_prev(1)
         for g in range(4, NG):
-            nc.sync.dma_start(out=x_all[:, gsl(g), :], in_=x_v[:, gsl(g), :])
-            nc.sync.dma_start(out=prev_all[:, gsl(g - 2), :], in_=prev_v[:, gsl(g - 2), :])
-        for g in range(NG - 2, NG):
-            nc.sync.dma_start(out=prev_all[:, gsl(g), :], in_=prev_v[:, gsl(g), :])
+            load_x(g)
+            load_prev(g - 2)
+        load_prev(NG - 2)
+        load_prev(NG - 1)
 
         st = {}
 
@@ -113,6 +116,10 @@ def tile_mnelayer_pa_t_kernel(
             if g not in st:
                 st[g] = {}
             return st[g]
+
+        def junk_ap():
+            jn[0] = (jn[0] + 1) % 8
+            return junk[:, jn[0], :]
 
         def st_v(g):
             for t in range(GT):
@@ -137,22 +144,25 @@ def tile_mnelayer_pa_t_kernel(
         def st_sum(g):
             for t in range(GT):
                 i = g * GT + t
-                nc.scalar.activation(out=junk[:], in_=x_all[:, i, :], func=ACT.Identity, accum_out=sx[:, i : i + 1])
+                nc.scalar.activation(out=junk_ap(), in_=x_all[:, i, :], func=ACT.Identity, accum_out=sx[:, i : i + 1])
+
+        def nm1_op(g):
             nc.scalar.mul(out=nm1[:, gsl(g)], in_=sx[:, gsl(g)], mul=-1.0 / N)
 
         def st_sq(g):
             for t in range(GT):
                 i = g * GT + t
                 nc.scalar.activation(
-                    out=junk[:], in_=x_all[:, i, :], func=ACT.Square, bias=nm1[:, i : i + 1],
+                    out=junk_ap(), in_=x_all[:, i, :], func=ACT.Square, bias=nm1[:, i : i + 1],
                     accum_out=ss1[:, i : i + 1],
                 )
+
+        def ve1_op(g):
             nc.scalar.activation(
                 out=ve1[:, gsl(g)], in_=ss1[:, gsl(g)], func=ACT.Identity, scale=1.0 / N, bias=epst[:, 0:1]
             )
             nc.gpsimd.tensor_tensor(out=rstd1[:, gsl(g)], in0=ve1[:, gsl(g)], in1=mhalf[:], op=ALU.pow)
-            if not XH_ON_G:
-                nc.gpsimd.tensor_tensor(out=nmr1[:, gsl(g)], in0=nm1[:, gsl(g)], in1=rstd1[:, gsl(g)], op=ALU.mult)
+            nc.gpsimd.tensor_tensor(out=nmr1[:, gsl(g)], in0=nm1[:, gsl(g)], in1=rstd1[:, gsl(g)], op=ALU.mult)
 
         def xh_s(g):
             xh = p2.tile([P, GT, N], F32, name="xh", tag="xh")
@@ -164,18 +174,8 @@ def tile_mnelayer_pa_t_kernel(
                     scale=rstd1[:, i : i + 1], bias=nmr1[:, i : i + 1],
                 )
 
-        def xh_g(g):
-            xh = p2.tile([P, GT, N], F32, name="xh", tag="xh")
-            tiles(g)["xh"] = xh
-            for t in range(GT):
-                i = g * GT + t
-                nc.gpsimd.tensor_scalar(
-                    out=xh[:, t, :], in0=x_all[:, i, :], scalar1=nm1[:, i : i + 1], scalar2=rstd1[:, i : i + 1],
-                    op0=ALU.add, op1=ALU.mult,
-                )
-
         def words_tx(src, h):
-            bank = psum.tile([P, 2, 256], F32, name="xwb", tag="tin")
+            bank = ps_s.tile([P, 2, 256], F32, name="xwb", tag="sps")
             for t2 in range(2):
                 w = src[:, 2 * h + t2, :].bitcast(F32)
                 for u in range(2):
@@ -193,7 +193,7 @@ def tile_mnelayer_pa_t_kernel(
         def tx(g, b):
             s = tiles(g)
             if b < 4:
-                bank = psum.tile([P, N], F32, name="xhb", tag="tin")
+                bank = ps_s.tile([P, N], F32, name="xhb", tag="sps")
                 for t in range(GT):
                     nc.tensor.transpose(bank[:, t * P : (t + 1) * P], s["xh"][:, t, b * P : (b + 1) * P], ident[:])
             else:
@@ -245,7 +245,7 @@ def tile_mnelayer_pa_t_kernel(
 
         def mxp(g, t):
             s = tiles(g)
-            bank = psum.tile([P, N], F32, name="preb", tag="pre")
+            bank = ps_v.tile([P, N], F32, name="preb", tag="vps")
             nc.tensor.matmul_mx(
                 out=bank[:],
                 lhsT=s["cn"][:, t * P : (t + 1) * P].bitcast(FP8X4),
@@ -259,7 +259,7 @@ def tile_mnelayer_pa_t_kernel(
 
         def mxg(g, c):
             s = tiles(g)
-            bank = psum.tile([P, N], F32, name="gtb", tag="gT")
+            bank = ps_s.tile([P, N], F32, name="gtb", tag="sps")
             nc.tensor.matmul_mx(
                 out=bank[:],
                 lhsT=wg_c[:, c * P : (c + 1) * P].bitcast(FP8X4),
@@ -282,7 +282,7 @@ def tile_mnelayer_pa_t_kernel(
 
         def tb(g, t):
             s = tiles(g)
-            bank = psum.tile([P, N], F32, name="gbb", tag="gb")
+            bank = ps_v.tile([P, N], F32, name="gbb", tag="vps")
             for c in range(4):
                 nc.tensor.transpose(bank[:, c * P : (c + 1) * P], s["gate_t"][:, c, t * P : (t + 1) * P], ident[:])
             s["gb%d" % t] = bank
@@ -300,15 +300,18 @@ def tile_mnelayer_pa_t_kernel(
         def pld_tail(g):
             s = tiles(g)
             nc.sync.dma_start(out=pot_v[:, gsl(g), :], in_=s["pot"][:])
-            wk = p4.tile([P, GT, N], F32, name="wk", tag="wk")
+            wk = p3.tile([P, GT, N], F32, name="wk", tag="wk")
             s["wk"] = wk
-            potf = s["pot"][:].rearrange("p t n -> p (t n)")
-            wkf = wk[:].rearrange("p t n -> p (t n)")
-            nc.vector.scalar_tensor_tensor(out=wkf, in0=potf, scalar=SLOPE, in1=potf, op0=ALU.mult, op1=ALU.max)
-            if D_ON_G:
-                nc.gpsimd.tensor_tensor(out=wk[:], in0=wk[:], in1=x_all[:, gsl(g), :], op=ALU.subtract)
-            else:
-                nc.vector.tensor_tensor(out=wk[:], in0=wk[:], in1=x_all[:, gsl(g), :], op=ALU.subtract)
+            for h in range(2):
+                ph = s["pot"][:, 2 * h : 2 * h + 2, :].rearrange("p t n -> p (t n)")
+                wh = wk[:, 2 * h : 2 * h + 2, :].rearrange("p t n -> p (t n)")
+                nc.vector.scalar_tensor_tensor(out=wh, in0=ph, scalar=SLOPE, in1=ph, op0=ALU.mult, op1=ALU.max)
+            for h in range(2):
+                i0 = g * GT + 2 * h
+                nc.vector.tensor_tensor(
+                    out=wk[:, 2 * h : 2 * h + 2, :], in0=wk[:, 2 * h : 2 * h + 2, :], in1=x_all[:, i0 : i0 + 2, :],
+                    op=ALU.subtract,
+                )
 
         def m_op(g, t):
             s = tiles(g)
@@ -323,46 +326,21 @@ def tile_mnelayer_pa_t_kernel(
                     op0=ALU.mult, op1=ALU.add, accum_out=sres[:, i : i + 1],
                 )
 
-        def sq2(g):
-            s = tiles(g)
+        def nmu2_op(g):
             nc.scalar.mul(out=nmu2[:, gsl(g)], in_=sres[:, gsl(g)], mul=-1.0 / N)
-            for t in range(GT):
-                i = g * GT + t
-                nc.scalar.activation(
-                    out=junk[:], in_=s["wk"][:, t, :], func=ACT.Square, bias=nmu2[:, i : i + 1],
-                    accum_out=ss2[:, i : i + 1],
-                )
+
+        def square2(g, t):
+            i = g * GT + t
             nc.scalar.activation(
-                out=ve2[:, gsl(g)], in_=ss2[:, gsl(g)], func=ACT.Identity, scale=1.0 / N, bias=epst[:, 0:1]
+                out=junk_ap(), in_=tiles(g)["wk"][:, t, :], func=ACT.Square, bias=nmu2[:, i : i + 1],
+                accum_out=ss2[:, i : i + 1],
             )
-            nc.gpsimd.tensor_tensor(out=rstd2[:, gsl(g)], in0=ve2[:, gsl(g)], in1=mhalf[:], op=ALU.pow)
-            if O_MODE != "stt":
-                nc.gpsimd.tensor_tensor(out=nmr2[:, gsl(g)], in0=nmu2[:, gsl(g)], in1=rstd2[:, gsl(g)], op=ALU.mult)
 
-        def xh2(g):
-            s = tiles(g)
-            for t in range(GT):
-                i = g * GT + t
-                nc.scalar.activation(
-                    out=s["wk"][:, t, :], in_=s["wk"][:, t, :], func=ACT.Identity,
-                    scale=rstd2[:, i : i + 1], bias=nmr2[:, i : i + 1],
-                )
-
-        def o_wide(g):
-            s = tiles(g)
-            wk = s["wk"]
-            nc.vector.tensor_tensor(
-                out=wk[:], in0=wk[:], in1=g_b[:].unsqueeze(1).to_broadcast([P, GT, N]), op=ALU.mult
+        def ve2_op(lo, hi):
+            nc.scalar.activation(
+                out=ve2[:, lo:hi], in_=ss2[:, lo:hi], func=ACT.Identity, scale=1.0 / N, bias=epst[:, 0:1]
             )
-            if O_MODE == "xh2g":
-                nc.gpsimd.tensor_tensor(
-                    out=wk[:], in0=wk[:], in1=b_b[:].unsqueeze(1).to_broadcast([P, GT, N]), op=ALU.add
-                )
-            else:
-                nc.vector.tensor_tensor(
-                    out=wk[:], in0=wk[:], in1=b_b[:].unsqueeze(1).to_broadcast([P, GT, N]), op=ALU.add
-                )
-            nc.sync.dma_start(out=out_v[:, gsl(g), :], in_=wk[:])
+            nc.gpsimd.tensor_tensor(out=rstd2[:, lo:hi], in0=ve2[:, lo:hi], in1=mhalf[:, 0 : hi - lo], op=ALU.pow)
 
         def o_op(g):
             s = tiles(g)
@@ -378,91 +356,94 @@ def tile_mnelayer_pa_t_kernel(
                     out=s["wk"][:, t, :], in0=s["wk"][:, t, :], scalar=rstd2[:, i : i + 1], in1=b_b[:],
                     op0=ALU.mult, op1=ALU.add,
                 )
-            nc.sync.dma_start(out=out_v[:, gsl(g), :], in_=s["wk"][:])
+                if g == NG - 1:
+                    nc.sync.dma_start(out=out_v[:, i, :], in_=s["wk"][:, t, :])
+            if g < NG - 1:
+                nc.sync.dma_start(out=out_v[:, gsl(g), :], in_=s["wk"][:])
+
+        VG = (0, 1)
 
         st_v(0)
-        st_v(1)
-        pv = psum.tile([P, P], BF16, name="pv", tag="tin")
+        pv = ps_s.tile([P, P], BF16, name="pv", tag="sps")
         nc.tensor.transpose(pv[:], vt[:], identb[:])
         nc.vector.tensor_copy(out=cols[:], in_=pv[:, 0:12])
-        grw = p2.tile([P, 4 * N], BF16, name="grw", tag="grx", align_bytes=64)
-        for h in range(2):
-            wb = words_tx(wg_raw[:], h)
-            words_out(wb, grw, h, False)
-        st_sum(2)
-        xh_v(0)
-        tx(0, 0)
-        tx(0, 1)
-        quant(wg_c[:], wg_p[:], grw[:])
         grs = regroup(ws_raw[:])
-        for b in range(6):
-            gbx(0, b, b % 2 == 1)
-            if b + 2 < 6:
-                tx(0, b + 2)
-        st_sq(2)
         quant(ws_c[:], ws_p[:], grs[:].rearrange("p c j -> p (c j)"))
-        xh_v(1)
-        tx(1, 0)
-        tx(1, 1)
-        q(0)
-        mxp(0, 0)
-        mxp(0, 1)
-        mxg(0, 0)
-        mxg(0, 1)
+        xh_v(0)
+        for b in range(3):
+            tx(0, b)
+        st_sum(2)
+        st_v(1)
+        grw = p2.tile([P, 4 * N], BF16, name="grw", tag="grx", align_bytes=64)
+        wbs = []
+        for b in range(6):
+            gbx(0, b)
+            if b + 3 < 6:
+                tx(0, b + 3)
+            elif b < 5:
+                wbs.append(words_tx(wg_raw[:], b - 3))
+        for h in range(2):
+            words_out(wbs[h], grw, h, False)
 
         def iteration(g):
             if ok(g):
                 for t in range(GT):
                     m_op(g, t)
-                    if t + 2 < GT:
-                        tb(g, t + 2)
-            if ok(g - 1) and O_MODE != "stt":
-                xh2(g - 1)
-            if ok(g + 3):
-                if XH_ON_G:
-                    xh_g(g + 3)
-                else:
-                    xh_s(g + 3)
-            for b in range(6):
+            if g >= 0:
+                if ok(g + 3):
+                    st_sum(g + 3)
                 if ok(g + 2):
-                    gbx(g + 2, b)
-                    if b + 2 < 6:
-                        tx(g + 2, b + 2)
-                if ok(g + 1) and b < GT:
-                    pot_op(g + 1, b)
-                    if b + 2 < GT:
-                        mxp(g + 1, b + 2)
+                    xh_s(g + 2)
             if ok(g + 1):
-                pld_tail(g + 1)
-            if ok(g + 3):
-                tx(g + 3, 0)
-                tx(g + 3, 1)
+                q(g + 1)
+            if g == -1:
+                quant(wg_c[:], wg_p[:], grw[:])
+                xh_v(1)
             if ok(g + 1):
-                for c in range(4):
+                for c in range(3):
+                    mxg(g + 1, c)
+                for t in range(GT):
+                    mxp(g + 1, t)
+            for c in range(4):
+                if ok(g + 1):
                     sig(g + 1, c)
-                    if c + 2 < 4:
-                        mxg(g + 1, c + 2)
+                    if c == 0:
+                        mxg(g + 1, 3)
+                if ok(g + 2) and c > 0:
+                    tx(g + 2, c - 1)
+            if ok(g + 1):
                 tb(g + 1, 0)
-                tb(g + 1, 1)
             if ok(g):
                 res(g)
-            if ok(g + 4):
-                st_sum(g + 4)
+            if ok(g + 3):
+                nm1_op(g + 3)
             if ok(g):
-                sq2(g)
-            if ok(g - 1):
-                if O_MODE == "stt":
-                    o_op(g - 1)
-                else:
-                    o_wide(g - 1)
-            if ok(g + 4):
-                st_sq(g + 4)
+                nmu2_op(g)
+                for t in range(GT):
+                    square2(g, t)
+                    if g == NG - 1 and t == 1:
+                        ve2_op(g * GT, g * GT + 2)
+                if g == NG - 1:
+                    ve2_op(g * GT + 2, g * GT + 4)
+            if ok(g + 1):
+                for t in range(GT):
+                    pot_op(g + 1, t)
+                    if t + 1 < GT:
+                        tb(g + 1, t + 1)
+                pld_tail(g + 1)
+            if ok(g + 3):
+                st_sq(g + 3)
+            if ok(g) and g < NG - 1:
+                ve2_op(g * GT, g * GT + GT)
+            if ok(g + 3):
+                ve1_op(g + 3)
             if ok(g + 2):
-                q(g + 2)
-                mxp(g + 2, 0)
-                mxp(g + 2, 1)
-                mxg(g + 2, 0)
-                mxg(g + 2, 1)
+                for b in range(6):
+                    gbx(g + 2, b)
+                    if b + 3 < 6:
+                        tx(g + 2, b + 3)
+            if ok(g):
+                o_op(g)
 
-        for g in range(-1, NG + 1):
+        for g in range(-1, NG):
             iteration(g)

@@ -32,7 +32,7 @@ def tile_mnelayer_pa_t_kernel(
         ctx.enter_context(tc.manual_schedule())
         const = ctx.enter_context(tc.tile_pool(name="const", bufs=1))
         p2 = ctx.enter_context(tc.tile_pool(name="p2", bufs=2))
-        p3 = ctx.enter_context(tc.tile_pool(name="p3", bufs=3))
+        p4 = ctx.enter_context(tc.tile_pool(name="p4", bufs=4))
         ps_s = ctx.enter_context(tc.psum_pool(name="ps_s", bufs=3))
         ps_v = ctx.enter_context(tc.psum_pool(name="ps_v", bufs=5))
 
@@ -300,7 +300,7 @@ def tile_mnelayer_pa_t_kernel(
         def pld_tail(g):
             s = tiles(g)
             nc.sync.dma_start(out=pot_v[:, gsl(g), :], in_=s["pot"][:])
-            wk = p3.tile([P, GT, N], F32, name="wk", tag="wk")
+            wk = p4.tile([P, GT, N], F32, name="wk", tag="wk")
             s["wk"] = wk
             for h in range(2):
                 ph = s["pot"][:, 2 * h : 2 * h + 2, :].rearrange("p t n -> p (t n)")
@@ -361,8 +361,6 @@ def tile_mnelayer_pa_t_kernel(
             if g < NG - 1:
                 nc.sync.dma_start(out=out_v[:, gsl(g), :], in_=s["wk"][:])
 
-        VG = (0, 1)
-
         st_v(0)
         pv = ps_s.tile([P, P], BF16, name="pv", tag="sps")
         nc.tensor.transpose(pv[:], vt[:], identb[:])
@@ -384,16 +382,19 @@ def tile_mnelayer_pa_t_kernel(
                 wbs.append(words_tx(wg_raw[:], b - 3))
         for h in range(2):
             words_out(wbs[h], grw, h, False)
+        nm1_op(2)
+        st_sq(2)
 
         def iteration(g):
             if ok(g):
                 for t in range(GT):
                     m_op(g, t)
-            if g >= 0:
-                if ok(g + 3):
-                    st_sum(g + 3)
-                if ok(g + 2):
-                    xh_s(g + 2)
+            if ok(g + 2) and g >= 0:
+                xh_s(g + 2)
+            if ok(g + 3):
+                ve1_op(g + 3)
+            if ok(g + 4):
+                st_sum(g + 4)
             if ok(g + 1):
                 q(g + 1)
             if g == -1:
@@ -415,9 +416,6 @@ def tile_mnelayer_pa_t_kernel(
                 tb(g + 1, 0)
             if ok(g):
                 res(g)
-            if ok(g + 3):
-                nm1_op(g + 3)
-            if ok(g):
                 nmu2_op(g)
                 for t in range(GT):
                     square2(g, t)
@@ -431,19 +429,18 @@ def tile_mnelayer_pa_t_kernel(
                     if t + 1 < GT:
                         tb(g + 1, t + 1)
                 pld_tail(g + 1)
-            if ok(g + 3):
-                st_sq(g + 3)
-            if ok(g) and g < NG - 1:
-                ve2_op(g * GT, g * GT + GT)
-            if ok(g + 3):
-                ve1_op(g + 3)
-            if ok(g + 2):
-                for b in range(6):
+            for b in range(6):
+                if ok(g + 2):
                     gbx(g + 2, b)
                     if b + 3 < 6:
                         tx(g + 2, b + 3)
-            if ok(g):
-                o_op(g)
+                if b == 1 and ok(g) and g < NG - 1:
+                    ve2_op(g * GT, g * GT + GT)
+            if ok(g + 4):
+                nm1_op(g + 4)
+                st_sq(g + 4)
+            if ok(g - 1):
+                o_op(g - 1)
 
-        for g in range(-1, NG):
+        for g in range(-1, NG + 1):
             iteration(g)

@@ -33,6 +33,7 @@ def tile_mnelayer_pa_t_kernel(
         const = ctx.enter_context(tc.tile_pool(name="const", bufs=1))
         p2 = ctx.enter_context(tc.tile_pool(name="p2", bufs=2))
         p4 = ctx.enter_context(tc.tile_pool(name="p4", bufs=4))
+        p5 = ctx.enter_context(tc.tile_pool(name="p5", bufs=5))
         ps_s = ctx.enter_context(tc.psum_pool(name="ps_s", bufs=3))
         ps_v = ctx.enter_context(tc.psum_pool(name="ps_v", bufs=5))
 
@@ -51,6 +52,7 @@ def tile_mnelayer_pa_t_kernel(
         cols = const.tile([P, 12], F32, name="cols")
         mhalf = const.tile([P, GT], F32, name="mhalf")
         epst = const.tile([P, 1], F32, name="epst")
+        ones = const.tile([P, 32], BF16, name="ones")
         ident = const.tile([P, P], F32, name="ident")
         identb = const.tile([P, P], BF16, name="identb")
         junk = const.tile([P, 8, N], BF16, name="junk")
@@ -82,6 +84,7 @@ def tile_mnelayer_pa_t_kernel(
         nc.vector.memset(vt[:], 0.0)
         nc.vector.memset(mhalf[:], -0.5)
         nc.vector.memset(epst[:], EPS)
+        nc.vector.memset(ones[:], 1.0)
         make_identity(nc, ident[:])
         make_identity(nc, identb[:])
 
@@ -190,36 +193,62 @@ def tile_mnelayer_pa_t_kernel(
             else:
                 nc.scalar.copy(out=dst, in_=src)
 
+        def wtx(g, h):
+            tiles(g)["xwb%d" % h] = words_tx(x_all[:, gsl(g), :], h)
+
+        def xw_out(g, h):
+            s = tiles(g)
+            if h == 0:
+                grx = p4.tile([P, 4 * N], BF16, name="grx", tag="grx", align_bytes=64)
+                s["grx"] = grx
+            words_out(s["xwb%d" % h], s["grx"], h, False)
+
+        def qx(g):
+            s = tiles(g)
+            cx = p5.tile([P, N], U32, name="cx", tag="cx", align_bytes=64)
+            px = p5.tile([P, N], U8, name="px", tag="px", align_bytes=64)
+            quant(cx[:], px[:], s["grx"][:])
+            s["cx"], s["px"] = cx, px
+
+        def sumx(g):
+            s = tiles(g)
+            sb = ps_s.tile([P, GT, 32], F32, name="sb", tag="sps")
+            gr3 = s["grx"][:].rearrange("p (c t) -> p c t", t=4)
+            for t in range(GT):
+                for k in range(4):
+                    nc.tensor.matmul(
+                        out=sb[:, t, :], lhsT=gr3[:, t * P : (t + 1) * P, k], rhs=ones[:], start=(k == 0), stop=(k == 3)
+                    )
+            s["sb"] = sb
+
+        def nm1_pe(g):
+            nc.scalar.mul(out=nm1[:, gsl(g)], in_=tiles(g)["sb"][:, :, 0], mul=-1.0 / N)
+
         def tx(g, b):
             s = tiles(g)
-            if b < 4:
-                bank = ps_s.tile([P, N], F32, name="xhb", tag="sps")
-                for t in range(GT):
-                    nc.tensor.transpose(bank[:, t * P : (t + 1) * P], s["xh"][:, t, b * P : (b + 1) * P], ident[:])
-            else:
-                bank = words_tx(x_all[:, gsl(g), :], b - 4)
+            bank = ps_s.tile([P, N], F32, name="xhb", tag="sps")
+            for t in range(GT):
+                nc.tensor.transpose(bank[:, t * P : (t + 1) * P], s["xh"][:, t, b * P : (b + 1) * P], ident[:])
             s["tin%d" % b] = bank
 
-        def gbx(g, b, on_vector=False):
+        def gbn(g, b):
             s = tiles(g)
             if b == 0:
                 xnt = p2.tile([P, 4, N], BF16, name="xnt", tag="xnt")
-                grx = p2.tile([P, 4 * N], BF16, name="grx", tag="grx", align_bytes=64)
                 s["xnt"] = xnt
-                s["grx"] = grx
-            bank = s["tin%d" % b]
-            if b >= 4:
-                words_out(bank, s["grx"], b - 4, on_vector)
-            elif on_vector:
-                nc.vector.tensor_scalar(
-                    out=s["xnt"][:, b, :], in0=bank[:], scalar1=cols[:, b : b + 1], scalar2=cols[:, 4 + b : 5 + b],
-                    op0=ALU.mult, op1=ALU.add,
-                )
-            else:
-                nc.scalar.activation(
-                    out=s["xnt"][:, b, :], in_=bank[:], func=ACT.Identity,
-                    scale=cols[:, b : b + 1], bias=cols[:, 4 + b : 5 + b],
-                )
+            nc.scalar.activation(
+                out=s["xnt"][:, b, :], in_=s["tin%d" % b][:], func=ACT.Identity,
+                scale=cols[:, b : b + 1], bias=cols[:, 4 + b : 5 + b],
+            )
+
+        def regroup_s(g):
+            s = tiles(g)
+            grn = p2.tile([P, N, 4], BF16, name="grn", tag="grn", align_bytes=64)
+            nc.scalar.copy(
+                out=grn[:].rearrange("p (c i) j -> p c j i", i=4),
+                in_=s["xnt"][:].rearrange("p j (c i) -> p c j i", i=4),
+            )
+            s["grn"] = grn
 
         def regroup(src):
             grn = p2.tile([P, N, 4], BF16, name="grn", tag="grn", align_bytes=64)
@@ -232,16 +261,14 @@ def tile_mnelayer_pa_t_kernel(
         def quant(codes, plane, flat):
             nc.vector.quantize_mx(out=codes.bitcast(FP8X4), scales=plane, in_=flat)
 
-        def q(g):
+        def qn(g):
             s = tiles(g)
+            if g in RG_V:
+                s["grn"] = regroup(s["xnt"][:])
             cn = p2.tile([P, N], U32, name="cn", tag="cn", align_bytes=64)
             pn = p2.tile([P, N], U8, name="pn", tag="pn", align_bytes=64)
-            cx = p2.tile([P, N], U32, name="cx", tag="cx", align_bytes=64)
-            px = p2.tile([P, N], U8, name="px", tag="px", align_bytes=64)
-            grn = regroup(s["xnt"][:])
-            quant(cx[:], px[:], s["grx"][:])
-            quant(cn[:], pn[:], grn[:].rearrange("p c j -> p (c j)"))
-            s["cn"], s["pn"], s["cx"], s["px"] = cn, pn, cx, px
+            quant(cn[:], pn[:], s["grn"][:].rearrange("p c j -> p (c j)"))
+            s["cn"], s["pn"] = cn, pn
 
         def mxp(g, t):
             s = tiles(g)
@@ -361,10 +388,16 @@ def tile_mnelayer_pa_t_kernel(
             if g < NG - 1:
                 nc.sync.dma_start(out=out_v[:, gsl(g), :], in_=s["wk"][:])
 
+        RG_V = (0, 1)
+
         st_v(0)
         pv = ps_s.tile([P, P], BF16, name="pv", tag="sps")
         nc.tensor.transpose(pv[:], vt[:], identb[:])
         nc.vector.tensor_copy(out=cols[:], in_=pv[:, 0:12])
+        wtx(0, 0)
+        wtx(0, 1)
+        xw_out(0, 0)
+        xw_out(0, 1)
         grs = regroup(ws_raw[:])
         quant(ws_c[:], ws_p[:], grs[:].rearrange("p c j -> p (c j)"))
         xh_v(0)
@@ -372,16 +405,33 @@ def tile_mnelayer_pa_t_kernel(
             tx(0, b)
         st_sum(2)
         st_v(1)
-        grw = p2.tile([P, 4 * N], BF16, name="grw", tag="grx", align_bytes=64)
+        qx(0)
+        grw = p4.tile([P, 4 * N], BF16, name="grw", tag="grx", align_bytes=64)
         wbs = []
-        for b in range(6):
-            gbx(0, b)
-            if b + 3 < 6:
-                tx(0, b + 3)
-            elif b < 5:
-                wbs.append(words_tx(wg_raw[:], b - 3))
-        for h in range(2):
-            words_out(wbs[h], grw, h, False)
+        for b in range(4):
+            gbn(0, b)
+            if b == 0:
+                tx(0, 3)
+            elif b < 3:
+                wbs.append(words_tx(wg_raw[:], b - 1))
+            else:
+                wtx(1, 0)
+        qn(0)
+        for t in range(GT):
+            mxp(0, t)
+        words_out(wbs[0], grw, 0, False)
+        wtx(1, 1)
+        words_out(wbs[1], grw, 1, False)
+        wtx(2, 0)
+        quant(wg_c[:], wg_p[:], grw[:])
+        xw_out(1, 0)
+        wtx(2, 1)
+        xw_out(1, 1)
+        wtx(3, 0)
+        xw_out(2, 0)
+        wtx(3, 1)
+        xw_out(2, 1)
+        mxg(0, 0)
         nm1_op(2)
         st_sq(2)
 
@@ -389,27 +439,26 @@ def tile_mnelayer_pa_t_kernel(
             if ok(g):
                 for t in range(GT):
                     m_op(g, t)
+            if ok(g + 1) and g >= 0:
+                qn(g + 1)
+                for t in range(GT):
+                    mxp(g + 1, t)
             if ok(g + 2) and g >= 0:
                 xh_s(g + 2)
             if ok(g + 3):
                 ve1_op(g + 3)
-            if ok(g + 4):
-                st_sum(g + 4)
-            if ok(g + 1):
-                q(g + 1)
-            if g == -1:
-                quant(wg_c[:], wg_p[:], grw[:])
-                xh_v(1)
-            if ok(g + 1):
-                for c in range(3):
-                    mxg(g + 1, c)
-                for t in range(GT):
-                    mxp(g + 1, t)
+            for h in range(2):
+                if ok(g + 4):
+                    xw_out(g + 4, h)
+                if ok(g + 1):
+                    mxg(g + 1, h + 1)
             for c in range(4):
                 if ok(g + 1):
                     sig(g + 1, c)
                     if c == 0:
                         mxg(g + 1, 3)
+                if g == -1 and c == 0:
+                    xh_v(1)
                 if ok(g + 2) and c > 0:
                     tx(g + 2, c - 1)
             if ok(g + 1):
@@ -429,15 +478,30 @@ def tile_mnelayer_pa_t_kernel(
                     if t + 1 < GT:
                         tb(g + 1, t + 1)
                 pld_tail(g + 1)
-            for b in range(6):
-                if ok(g + 2):
-                    gbx(g + 2, b)
-                    if b + 3 < 6:
-                        tx(g + 2, b + 3)
-                if b == 1 and ok(g) and g < NG - 1:
-                    ve2_op(g * GT, g * GT + GT)
+            if g == -1:
+                qx(1)
+                qx(2)
             if ok(g + 4):
-                nm1_op(g + 4)
+                qx(g + 4)
+            for b in range(4):
+                if ok(g + 2):
+                    gbn(g + 2, b)
+                if b == 0 and ok(g + 2):
+                    tx(g + 2, 3)
+                if b == 1:
+                    if ok(g + 4):
+                        sumx(g + 4)
+                    if ok(g) and g < NG - 1:
+                        ve2_op(g * GT, g * GT + GT)
+                if b >= 2 and ok(g + 5):
+                    wtx(g + 5, b - 2)
+            if ok(g + 2) and g + 2 not in RG_V:
+                regroup_s(g + 2)
+            if ok(g + 4):
+                nm1_pe(g + 4)
+            if ok(g + 2):
+                mxg(g + 2, 0)
+            if ok(g + 4):
                 st_sq(g + 4)
             if ok(g - 1):
                 o_op(g - 1)

@@ -74,6 +74,10 @@ def tile_mnelayer_pa_t_kernel(
         ss2 = const.tile([P, NT], F32, name="ss2")
         ve2 = const.tile([P, NT], F32, name="ve2")
         rstd2 = const.tile([P, NT], F32, name="rstd2")
+        sd1 = const.tile([P, 2 * GT], F32, name="sd1")
+        sd2 = const.tile([P, GT], F32, name="sd2")
+        rstd2b = const.tile([P, GT], F32, name="rstd2b")
+        dummy = const.tile([P, 2], F32, name="dummy")
 
         def gsl(g):
             return slice(g * GT, (g + 1) * GT)
@@ -85,6 +89,7 @@ def tile_mnelayer_pa_t_kernel(
         nc.vector.memset(mhalf[:], -0.5)
         nc.vector.memset(epst[:], EPS)
         nc.vector.memset(ones[:], 1.0)
+        nc.scalar.activation(out=dummy[:, 0:1], in_=epst[:, 0:1], func=ACT.Sqrt)
         make_identity(nc, ident[:])
         make_identity(nc, identb[:])
 
@@ -94,7 +99,8 @@ def tile_mnelayer_pa_t_kernel(
         def load_prev(g):
             nc.sync.dma_start(out=prev_all[:, gsl(g), :], in_=prev_v[:, gsl(g), :])
 
-        load_x(0)
+        nc.sync.dma_start(out=x_all[:, 0:2, :], in_=x_v[:, 0:2, :])
+        nc.sync.dma_start(out=x_all[:, 2:4, :], in_=x_v[:, 2:4, :])
         nc.sync.dma_start(out=vt[0:4, :], in_=pre_gamma.rearrange("(j p) -> j p", p=P))
         nc.sync.dma_start(out=vt[4:8, :], in_=pre_beta.rearrange("(j p) -> j p", p=P))
         nc.sync.dma_start(out=vt[8:12, :], in_=gate_b.rearrange("(j p) -> j p", p=P))
@@ -104,14 +110,17 @@ def tile_mnelayer_pa_t_kernel(
         nc.sync.dma_start(out=wg_raw[:], in_=gate_W.rearrange("(c m) k -> m c k", m=P))
         load_prev(0)
         load_x(3)
+        load_x(4)
+        load_prev(1)
+        load_x(5)
         nc.sync.dma_start(out=g_b[:], in_=ln_gamma.partition_broadcast(P))
         nc.sync.dma_start(out=b_b[:], in_=ln_beta.partition_broadcast(P))
-        load_prev(1)
+        load_prev(2)
+        load_x(6)
+        load_prev(3)
+        load_x(7)
         for g in range(4, NG):
-            load_x(g)
-            load_prev(g - 2)
-        load_prev(NG - 2)
-        load_prev(NG - 1)
+            load_prev(g)
 
         st = {}
 
@@ -129,12 +138,12 @@ def tile_mnelayer_pa_t_kernel(
                 i = g * GT + t
                 nc.vector.bn_stats(out=bst[:, i, :], in_=x_all[:, i, :])
                 nc.vector.bn_aggr(out=mv[:, i, :], in_=bst[:, i, :])
-            nc.gpsimd.tensor_scalar(
-                out=ve1[:, gsl(g)], in0=mv[:, gsl(g), 1], scalar1=EPS, scalar2=1.0, op0=ALU.add, op1=ALU.mult
-            )
-            nc.gpsimd.tensor_tensor(out=rstd1[:, gsl(g)], in0=ve1[:, gsl(g)], in1=mhalf[:], op=ALU.pow)
+
+        def sqrt1(g):
+            nc.scalar.activation(out=sd1[:, gsl(g)], in_=mv[:, gsl(g), 1], func=ACT.Sqrt, bias=epst[:, 0:1])
 
         def xh_v(g):
+            nc.vector.reciprocal(out=rstd1[:, gsl(g)], in_=sd1[:, gsl(g)])
             xh = p2.tile([P, GT, N], F32, name="xh", tag="xh")
             tiles(g)["xh"] = xh
             for t in range(GT):
@@ -165,7 +174,9 @@ def tile_mnelayer_pa_t_kernel(
                 out=ve1[:, gsl(g)], in_=ss1[:, gsl(g)], func=ACT.Identity, scale=1.0 / N, bias=epst[:, 0:1]
             )
             nc.gpsimd.tensor_tensor(out=rstd1[:, gsl(g)], in0=ve1[:, gsl(g)], in1=mhalf[:], op=ALU.pow)
-            nc.gpsimd.tensor_tensor(out=nmr1[:, gsl(g)], in0=nm1[:, gsl(g)], in1=rstd1[:, gsl(g)], op=ALU.mult)
+
+        def nmr1_v(g):
+            nc.vector.tensor_tensor(out=nmr1[:, gsl(g)], in0=nm1[:, gsl(g)], in1=rstd1[:, gsl(g)], op=ALU.mult)
 
         def xh_s(g):
             xh = p2.tile([P, GT, N], F32, name="xh", tag="xh")
@@ -369,6 +380,12 @@ def tile_mnelayer_pa_t_kernel(
             )
             nc.gpsimd.tensor_tensor(out=rstd2[:, lo:hi], in0=ve2[:, lo:hi], in1=mhalf[:, 0 : hi - lo], op=ALU.pow)
 
+        def sqrt2_last(lo, hi):
+            base = (NG - 1) * GT
+            nc.scalar.activation(
+                out=sd2[:, lo:hi], in_=ss2[:, base + lo : base + hi], func=ACT.Sqrt, scale=1.0 / N, bias=epst[:, 0:1]
+            )
+
         def o_op(g):
             s = tiles(g)
             for t in range(GT):
@@ -377,10 +394,13 @@ def tile_mnelayer_pa_t_kernel(
                     out=s["wk"][:, t, :], in0=s["wk"][:, t, :], scalar=nmu2[:, i : i + 1], in1=g_b[:],
                     op0=ALU.add, op1=ALU.mult,
                 )
+            if g == NG - 1:
+                nc.vector.reciprocal(out=rstd2b[:], in_=sd2[:])
             for t in range(GT):
                 i = g * GT + t
                 nc.vector.scalar_tensor_tensor(
-                    out=s["wk"][:, t, :], in0=s["wk"][:, t, :], scalar=rstd2[:, i : i + 1], in1=b_b[:],
+                    out=s["wk"][:, t, :], in0=s["wk"][:, t, :],
+                    scalar=(rstd2b[:, t : t + 1] if g == NG - 1 else rstd2[:, i : i + 1]), in1=b_b[:],
                     op0=ALU.mult, op1=ALU.add,
                 )
                 if g == NG - 1:
@@ -398,6 +418,7 @@ def tile_mnelayer_pa_t_kernel(
         wtx(0, 1)
         xw_out(0, 0)
         xw_out(0, 1)
+        sqrt1(0)
         grs = regroup(ws_raw[:])
         quant(ws_c[:], ws_p[:], grs[:].rearrange("p c j -> p (c j)"))
         xh_v(0)
@@ -416,6 +437,7 @@ def tile_mnelayer_pa_t_kernel(
                 wbs.append(words_tx(wg_raw[:], b - 1))
             else:
                 wtx(1, 0)
+        sqrt1(1)
         qn(0)
         for t in range(GT):
             mxp(0, t)
@@ -463,21 +485,23 @@ def tile_mnelayer_pa_t_kernel(
                     tx(g + 2, c - 1)
             if ok(g + 1):
                 tb(g + 1, 0)
+            if g + 1 == NG - 1:
+                nc.scalar.activation(out=dummy[:, 1:2], in_=epst[:, 0:1], func=ACT.Sqrt)
             if ok(g):
                 res(g)
                 nmu2_op(g)
                 for t in range(GT):
                     square2(g, t)
-                    if g == NG - 1 and t == 1:
-                        ve2_op(g * GT, g * GT + 2)
                 if g == NG - 1:
-                    ve2_op(g * GT + 2, g * GT + 4)
+                    sqrt2_last(0, GT)
             if ok(g + 1):
                 for t in range(GT):
                     pot_op(g + 1, t)
                     if t + 1 < GT:
                         tb(g + 1, t + 1)
                 pld_tail(g + 1)
+            if ok(g + 3):
+                nmr1_v(g + 3)
             if g == -1:
                 qx(1)
                 qx(2)

@@ -12,16 +12,25 @@ ALU = mybir.AluOpType
 ACT = mybir.ActivationFunctionType
 
 P = 128
-B = 4096
-N = 512
-NT = B // P
+ROWS = 4096
+D = 512
+TILES = ROWS // P
 GT = 4
-NG = NT // GT
+GROUPS = TILES // GT
+LAST = GROUPS - 1
+CHUNKS = D // P
+PACK = 4
 EPS = 1e-5
 DECAY = 0.9
 SLOPE = 0.01
+SUM_COLS = 32
+JUNK_BUFS = 8
+SCALAR_BANKS = 3
+VECTOR_BANKS = 5
+ON_VECTOR = (0, 1)
+SUMS_ON_SCALAR = 2
 
-FLOPS = 2 * 2 * B * N * N
+FLOPS = 2 * 2 * ROWS * D * D
 
 
 def tile_mnelayer_pa_t_kernel(
@@ -31,504 +40,511 @@ def tile_mnelayer_pa_t_kernel(
     with ExitStack() as ctx:
         ctx.enter_context(tc.manual_schedule())
         const = ctx.enter_context(tc.tile_pool(name="const", bufs=1))
-        p2 = ctx.enter_context(tc.tile_pool(name="p2", bufs=2))
-        p4 = ctx.enter_context(tc.tile_pool(name="p4", bufs=4))
-        p5 = ctx.enter_context(tc.tile_pool(name="p5", bufs=5))
-        ps_s = ctx.enter_context(tc.psum_pool(name="ps_s", bufs=3))
-        ps_v = ctx.enter_context(tc.psum_pool(name="ps_v", bufs=5))
+        two = ctx.enter_context(tc.tile_pool(name="two", bufs=2))
+        four = ctx.enter_context(tc.tile_pool(name="four", bufs=4))
+        five = ctx.enter_context(tc.tile_pool(name="five", bufs=5))
+        for_scalar = ctx.enter_context(tc.psum_pool(name="for_scalar", bufs=SCALAR_BANKS))
+        for_vector = ctx.enter_context(tc.psum_pool(name="for_vector", bufs=VECTOR_BANKS))
 
-        x_v = inputs.rearrange("(p i) k -> p i k", i=NT)
-        prev_v = prev_potential.rearrange("(p i) k -> p i k", i=NT)
-        out_v = out_0.rearrange("(p i) k -> p i k", i=NT)
-        pot_v = out_1.rearrange("(p i) k -> p i k", i=NT)
+        x_dram = inputs.rearrange("(p i) k -> p i k", i=TILES)
+        prev_dram = prev_potential.rearrange("(p i) k -> p i k", i=TILES)
+        out_dram = out_0.rearrange("(p i) k -> p i k", i=TILES)
+        pot_dram = out_1.rearrange("(p i) k -> p i k", i=TILES)
 
-        x_all = const.tile([P, NT, N], BF16, name="x_all")
-        prev_all = const.tile([P, NT, N], BF16, name="prev_all")
-        wg_raw = const.tile([P, GT, N], BF16, name="wg_raw")
-        ws_raw = const.tile([P, GT, N], BF16, name="ws_raw")
-        vt = const.tile([P, P], BF16, name="vt")
-        g_b = const.tile([P, N], BF16, name="g_b")
-        b_b = const.tile([P, N], BF16, name="b_b")
-        cols = const.tile([P, 12], F32, name="cols")
-        mhalf = const.tile([P, GT], F32, name="mhalf")
-        epst = const.tile([P, 1], F32, name="epst")
-        ones = const.tile([P, 32], BF16, name="ones")
+        x_all = const.tile([P, TILES, D], BF16, name="x_all")
+        prev_all = const.tile([P, TILES, D], BF16, name="prev_all")
+        gate_w_rows = const.tile([P, CHUNKS, D], BF16, name="gate_w_rows")
+        syn_rows = const.tile([P, PACK, D], BF16, name="syn_rows")
+        vec_rows = const.tile([P, P], BF16, name="vec_rows")
+        gamma2 = const.tile([P, D], BF16, name="gamma2")
+        beta2 = const.tile([P, D], BF16, name="beta2")
+        vec_cols = const.tile([P, 3 * CHUNKS], F32, name="vec_cols")
+        minus_half = const.tile([P, GT], F32, name="minus_half")
+        eps_col = const.tile([P, 1], F32, name="eps_col")
+        ones = const.tile([P, SUM_COLS], BF16, name="ones")
         ident = const.tile([P, P], F32, name="ident")
-        identb = const.tile([P, P], BF16, name="identb")
-        junk = const.tile([P, 8, N], BF16, name="junk")
-        jn = [0]
-        ws_c = const.tile([P, N], U32, name="ws_c", align_bytes=64)
-        ws_p = const.tile([P, N], U8, name="ws_p", align_bytes=64)
-        wg_c = const.tile([P, N], U32, name="wg_c", align_bytes=64)
-        wg_p = const.tile([P, N], U8, name="wg_p", align_bytes=64)
-        bst = const.tile([P, NT, 6], F32, name="bst")
-        mv = const.tile([P, NT, 2], F32, name="mv")
-        sx = const.tile([P, NT], F32, name="sx")
-        nm1 = const.tile([P, NT], F32, name="nm1")
-        ss1 = const.tile([P, NT], F32, name="ss1")
-        ve1 = const.tile([P, NT], F32, name="ve1")
-        rstd1 = const.tile([P, NT], F32, name="rstd1")
-        nmr1 = const.tile([P, NT], F32, name="nmr1")
-        sres = const.tile([P, NT], F32, name="sres")
-        nmu2 = const.tile([P, NT], F32, name="nmu2")
-        ss2 = const.tile([P, NT], F32, name="ss2")
-        ve2 = const.tile([P, NT], F32, name="ve2")
-        rstd2 = const.tile([P, NT], F32, name="rstd2")
-        sd1 = const.tile([P, 2 * GT], F32, name="sd1")
-        sd2 = const.tile([P, GT], F32, name="sd2")
-        rstd2b = const.tile([P, GT], F32, name="rstd2b")
-        dummy = const.tile([P, 2], F32, name="dummy")
+        ident_bf = const.tile([P, P], BF16, name="ident_bf")
+        junk = const.tile([P, JUNK_BUFS, D], BF16, name="junk")
+        junk_turn = [0]
+        syn_codes = const.tile([P, D], U32, name="syn_codes", align_bytes=64)
+        syn_scales = const.tile([P, D], U8, name="syn_scales", align_bytes=64)
+        gate_codes = const.tile([P, D], U32, name="gate_codes", align_bytes=64)
+        gate_scales = const.tile([P, D], U8, name="gate_scales", align_bytes=64)
+        bn6 = const.tile([P, len(ON_VECTOR) * GT, 6], F32, name="bn6")
+        mean_var1 = const.tile([P, len(ON_VECTOR) * GT, 2], F32, name="mean_var1")
+        sum1 = const.tile([P, GT], F32, name="sum1")
+        neg_mean1 = const.tile([P, TILES], F32, name="neg_mean1")
+        sq_dev1 = const.tile([P, TILES], F32, name="sq_dev1")
+        var_eps1 = const.tile([P, TILES], F32, name="var_eps1")
+        rstd1 = const.tile([P, TILES], F32, name="rstd1")
+        neg_mean_rstd1 = const.tile([P, TILES], F32, name="neg_mean_rstd1")
+        sum2 = const.tile([P, TILES], F32, name="sum2")
+        neg_mean2 = const.tile([P, TILES], F32, name="neg_mean2")
+        sq_dev2 = const.tile([P, TILES], F32, name="sq_dev2")
+        var_eps2 = const.tile([P, TILES], F32, name="var_eps2")
+        rstd2 = const.tile([P, TILES], F32, name="rstd2")
+        std1 = const.tile([P, len(ON_VECTOR) * GT], F32, name="std1")
+        std2_last = const.tile([P, GT], F32, name="std2_last")
+        rstd2_last = const.tile([P, GT], F32, name="rstd2_last")
+        table_warmer = const.tile([P, 2], F32, name="table_warmer")
 
-        def gsl(g):
+        def tiles_of(g):
             return slice(g * GT, (g + 1) * GT)
 
-        def ok(g):
-            return 0 <= g < NG
+        def exists(g):
+            return 0 <= g < GROUPS
 
-        nc.vector.memset(vt[:], 0.0)
-        nc.vector.memset(mhalf[:], -0.5)
-        nc.vector.memset(epst[:], EPS)
+        nc.vector.memset(vec_rows[:], 0.0)
+        nc.vector.memset(minus_half[:], -0.5)
+        nc.vector.memset(eps_col[:], EPS)
         nc.vector.memset(ones[:], 1.0)
-        nc.scalar.activation(out=dummy[:, 0:1], in_=epst[:, 0:1], func=ACT.Sqrt)
+        nc.scalar.activation(out=table_warmer[:, 0:1], in_=eps_col[:, 0:1], func=ACT.Sqrt)
         make_identity(nc, ident[:])
-        make_identity(nc, identb[:])
+        make_identity(nc, ident_bf[:])
 
         def load_x(g):
-            nc.sync.dma_start(out=x_all[:, gsl(g), :], in_=x_v[:, gsl(g), :])
+            nc.sync.dma_start(out=x_all[:, tiles_of(g), :], in_=x_dram[:, tiles_of(g), :])
 
         def load_prev(g):
-            nc.sync.dma_start(out=prev_all[:, gsl(g), :], in_=prev_v[:, gsl(g), :])
+            nc.sync.dma_start(out=prev_all[:, tiles_of(g), :], in_=prev_dram[:, tiles_of(g), :])
 
-        nc.sync.dma_start(out=x_all[:, 0:2, :], in_=x_v[:, 0:2, :])
-        nc.sync.dma_start(out=x_all[:, 2:4, :], in_=x_v[:, 2:4, :])
-        nc.sync.dma_start(out=vt[0:4, :], in_=pre_gamma.rearrange("(j p) -> j p", p=P))
-        nc.sync.dma_start(out=vt[4:8, :], in_=pre_beta.rearrange("(j p) -> j p", p=P))
-        nc.sync.dma_start(out=vt[8:12, :], in_=gate_b.rearrange("(j p) -> j p", p=P))
-        nc.sync.dma_start(out=ws_raw[:], in_=syn_weights.rearrange("(j p) n -> p j n", p=P))
+        nc.sync.dma_start(out=x_all[:, 0:2, :], in_=x_dram[:, 0:2, :])
+        nc.sync.dma_start(out=x_all[:, 2:4, :], in_=x_dram[:, 2:4, :])
+        for a, vec in enumerate((pre_gamma, pre_beta, gate_b)):
+            nc.sync.dma_start(out=vec_rows[a * CHUNKS : (a + 1) * CHUNKS, :], in_=vec.rearrange("(j p) -> j p", p=P))
+        nc.sync.dma_start(out=syn_rows[:], in_=syn_weights.rearrange("(j p) n -> p j n", p=P))
         load_x(1)
         load_x(2)
-        nc.sync.dma_start(out=wg_raw[:], in_=gate_W.rearrange("(c m) k -> m c k", m=P))
+        nc.sync.dma_start(out=gate_w_rows[:], in_=gate_W.rearrange("(c m) k -> m c k", m=P))
         load_prev(0)
         load_x(3)
         load_x(4)
         load_prev(1)
         load_x(5)
-        nc.sync.dma_start(out=g_b[:], in_=ln_gamma.partition_broadcast(P))
-        nc.sync.dma_start(out=b_b[:], in_=ln_beta.partition_broadcast(P))
+        nc.sync.dma_start(out=gamma2[:], in_=ln_gamma.partition_broadcast(P))
+        nc.sync.dma_start(out=beta2[:], in_=ln_beta.partition_broadcast(P))
         load_prev(2)
         load_x(6)
         load_prev(3)
         load_x(7)
-        for g in range(4, NG):
+        for g in range(4, GROUPS):
             load_prev(g)
 
-        st = {}
+        held = {}
 
-        def tiles(g):
-            if g not in st:
-                st[g] = {}
-            return st[g]
+        def of(g):
+            if g not in held:
+                held[g] = {}
+            return held[g]
 
-        def junk_ap():
-            jn[0] = (jn[0] + 1) % 8
-            return junk[:, jn[0], :]
+        def junk_out():
+            junk_turn[0] = (junk_turn[0] + 1) % JUNK_BUFS
+            return junk[:, junk_turn[0], :]
 
-        def st_v(g):
-            for t in range(GT):
-                i = g * GT + t
-                nc.vector.bn_stats(out=bst[:, i, :], in_=x_all[:, i, :])
-                nc.vector.bn_aggr(out=mv[:, i, :], in_=bst[:, i, :])
+        def stats1_on_vector(g):
+            for i in range(g * GT, (g + 1) * GT):
+                nc.vector.bn_stats(out=bn6[:, i, :], in_=x_all[:, i, :])
+                nc.vector.bn_aggr(out=mean_var1[:, i, :], in_=bn6[:, i, :])
 
-        def sqrt1(g):
-            nc.scalar.activation(out=sd1[:, gsl(g)], in_=mv[:, gsl(g), 1], func=ACT.Sqrt, bias=epst[:, 0:1])
+        def std1_on_scalar(g):
+            nc.scalar.activation(
+                out=std1[:, tiles_of(g)], in_=mean_var1[:, tiles_of(g), 1], func=ACT.Sqrt, bias=eps_col[:, 0:1]
+            )
 
-        def xh_v(g):
-            nc.vector.reciprocal(out=rstd1[:, gsl(g)], in_=sd1[:, gsl(g)])
-            xh = p2.tile([P, GT, N], F32, name="xh", tag="xh")
-            tiles(g)["xh"] = xh
+        def xhat_on_vector(g):
+            nc.vector.reciprocal(out=rstd1[:, tiles_of(g)], in_=std1[:, tiles_of(g)])
+            xhat = two.tile([P, GT, D], F32, name="xhat", tag="xhat")
+            of(g)["xhat"] = xhat
             for t in range(GT):
                 i = g * GT + t
                 nc.vector.tensor_scalar(
-                    out=xh[:, t, :], in0=x_all[:, i, :], scalar1=mv[:, i, 0:1], scalar2=rstd1[:, i : i + 1],
+                    out=xhat[:, t, :], in0=x_all[:, i, :], scalar1=mean_var1[:, i, 0:1], scalar2=rstd1[:, i : i + 1],
                     op0=ALU.subtract, op1=ALU.mult,
                 )
 
-        def st_sum(g):
+        def row_sums_on_scalar(g):
             for t in range(GT):
-                i = g * GT + t
-                nc.scalar.activation(out=junk_ap(), in_=x_all[:, i, :], func=ACT.Identity, accum_out=sx[:, i : i + 1])
-
-        def nm1_op(g):
-            nc.scalar.mul(out=nm1[:, gsl(g)], in_=sx[:, gsl(g)], mul=-1.0 / N)
-
-        def st_sq(g):
-            for t in range(GT):
-                i = g * GT + t
                 nc.scalar.activation(
-                    out=junk_ap(), in_=x_all[:, i, :], func=ACT.Square, bias=nm1[:, i : i + 1],
-                    accum_out=ss1[:, i : i + 1],
+                    out=junk_out(), in_=x_all[:, g * GT + t, :], func=ACT.Identity, accum_out=sum1[:, t : t + 1]
                 )
 
-        def ve1_op(g):
+        def neg_mean1_from_scalar_sums(g):
+            nc.scalar.mul(out=neg_mean1[:, tiles_of(g)], in_=sum1[:], mul=-1.0 / D)
+
+        def row_sums_on_tensor(g):
+            sums = for_scalar.tile([P, GT, SUM_COLS], F32, name="sums", tag="bank")
+            x_t = of(g)["x_t"][:].rearrange("p (n v) -> p n v", v=PACK)
+            for t in range(GT):
+                for v in range(PACK):
+                    nc.tensor.matmul(
+                        out=sums[:, t, :], lhsT=x_t[:, t * P : (t + 1) * P, v], rhs=ones[:],
+                        start=(v == 0), stop=(v == PACK - 1),
+                    )
+            of(g)["sums"] = sums
+
+        def neg_mean1_from_tensor_sums(g):
+            nc.scalar.mul(out=neg_mean1[:, tiles_of(g)], in_=of(g)["sums"][:, :, 0], mul=-1.0 / D)
+
+        def squared_deviations1(g):
+            for i in range(g * GT, (g + 1) * GT):
+                nc.scalar.activation(
+                    out=junk_out(), in_=x_all[:, i, :], func=ACT.Square, bias=neg_mean1[:, i : i + 1],
+                    accum_out=sq_dev1[:, i : i + 1],
+                )
+
+        def rstd1_by_pow(g):
             nc.scalar.activation(
-                out=ve1[:, gsl(g)], in_=ss1[:, gsl(g)], func=ACT.Identity, scale=1.0 / N, bias=epst[:, 0:1]
+                out=var_eps1[:, tiles_of(g)], in_=sq_dev1[:, tiles_of(g)], func=ACT.Identity, scale=1.0 / D,
+                bias=eps_col[:, 0:1],
             )
-            nc.gpsimd.tensor_tensor(out=rstd1[:, gsl(g)], in0=ve1[:, gsl(g)], in1=mhalf[:], op=ALU.pow)
+            nc.gpsimd.tensor_tensor(
+                out=rstd1[:, tiles_of(g)], in0=var_eps1[:, tiles_of(g)], in1=minus_half[:], op=ALU.pow
+            )
 
-        def nmr1_v(g):
-            nc.vector.tensor_tensor(out=nmr1[:, gsl(g)], in0=nm1[:, gsl(g)], in1=rstd1[:, gsl(g)], op=ALU.mult)
+        def neg_mean_times_rstd1(g):
+            nc.vector.tensor_tensor(
+                out=neg_mean_rstd1[:, tiles_of(g)], in0=neg_mean1[:, tiles_of(g)], in1=rstd1[:, tiles_of(g)],
+                op=ALU.mult,
+            )
 
-        def xh_s(g):
-            xh = p2.tile([P, GT, N], F32, name="xh", tag="xh")
-            tiles(g)["xh"] = xh
+        def xhat_on_scalar(g):
+            xhat = two.tile([P, GT, D], F32, name="xhat", tag="xhat")
+            of(g)["xhat"] = xhat
             for t in range(GT):
                 i = g * GT + t
                 nc.scalar.activation(
-                    out=xh[:, t, :], in_=x_all[:, i, :], func=ACT.Identity,
-                    scale=rstd1[:, i : i + 1], bias=nmr1[:, i : i + 1],
+                    out=xhat[:, t, :], in_=x_all[:, i, :], func=ACT.Identity,
+                    scale=rstd1[:, i : i + 1], bias=neg_mean_rstd1[:, i : i + 1],
                 )
 
-        def words_tx(src, h):
-            bank = ps_s.tile([P, 2, 256], F32, name="xwb", tag="sps")
-            for t2 in range(2):
-                w = src[:, 2 * h + t2, :].bitcast(F32)
+        def transpose_words(rows, h):
+            bank = for_scalar.tile([P, 2, 2 * P], F32, name="word_bank", tag="bank")
+            for t in range(2):
+                words = rows[:, 2 * h + t, :].bitcast(F32)
                 for u in range(2):
-                    nc.tensor.transpose(bank[:, u, t2 * P : (t2 + 1) * P], w[:, u * P : (u + 1) * P], ident[:])
+                    nc.tensor.transpose(bank[:, u, t * P : (t + 1) * P], words[:, u * P : (u + 1) * P], ident[:])
             return bank
 
-        def words_out(bank, grx, h, on_vector):
-            dst = grx[:].bitcast(F32).rearrange("p (c u) -> p c u", u=2)[:, h * 256 : (h + 1) * 256, :]
-            src = bank[:].rearrange("p u c -> p c u")
-            if on_vector:
-                nc.vector.tensor_copy(out=dst, in_=src)
-            else:
-                nc.scalar.copy(out=dst, in_=src)
-
-        def wtx(g, h):
-            tiles(g)["xwb%d" % h] = words_tx(x_all[:, gsl(g), :], h)
-
-        def xw_out(g, h):
-            s = tiles(g)
-            if h == 0:
-                grx = p4.tile([P, 4 * N], BF16, name="grx", tag="grx", align_bytes=64)
-                s["grx"] = grx
-            words_out(s["xwb%d" % h], s["grx"], h, False)
-
-        def qx(g):
-            s = tiles(g)
-            cx = p5.tile([P, N], U32, name="cx", tag="cx", align_bytes=64)
-            px = p5.tile([P, N], U8, name="px", tag="px", align_bytes=64)
-            quant(cx[:], px[:], s["grx"][:])
-            s["cx"], s["px"] = cx, px
-
-        def sumx(g):
-            s = tiles(g)
-            sb = ps_s.tile([P, GT, 32], F32, name="sb", tag="sps")
-            gr3 = s["grx"][:].rearrange("p (c t) -> p c t", t=4)
-            for t in range(GT):
-                for k in range(4):
-                    nc.tensor.matmul(
-                        out=sb[:, t, :], lhsT=gr3[:, t * P : (t + 1) * P, k], rhs=ones[:], start=(k == 0), stop=(k == 3)
-                    )
-            s["sb"] = sb
-
-        def nm1_pe(g):
-            nc.scalar.mul(out=nm1[:, gsl(g)], in_=tiles(g)["sb"][:, :, 0], mul=-1.0 / N)
-
-        def tx(g, b):
-            s = tiles(g)
-            bank = ps_s.tile([P, N], F32, name="xhb", tag="sps")
-            for t in range(GT):
-                nc.tensor.transpose(bank[:, t * P : (t + 1) * P], s["xh"][:, t, b * P : (b + 1) * P], ident[:])
-            s["tin%d" % b] = bank
-
-        def gbn(g, b):
-            s = tiles(g)
-            if b == 0:
-                xnt = p2.tile([P, 4, N], BF16, name="xnt", tag="xnt")
-                s["xnt"] = xnt
-            nc.scalar.activation(
-                out=s["xnt"][:, b, :], in_=s["tin%d" % b][:], func=ACT.Identity,
-                scale=cols[:, b : b + 1], bias=cols[:, 4 + b : 5 + b],
-            )
-
-        def regroup_s(g):
-            s = tiles(g)
-            grn = p2.tile([P, N, 4], BF16, name="grn", tag="grn", align_bytes=64)
+        def copy_words(bank, dst, h):
             nc.scalar.copy(
-                out=grn[:].rearrange("p (c i) j -> p c j i", i=4),
-                in_=s["xnt"][:].rearrange("p j (c i) -> p c j i", i=4),
+                out=dst[:].bitcast(F32).rearrange("p (n u) -> p n u", u=2)[:, h * 2 * P : (h + 1) * 2 * P, :],
+                in_=bank[:].rearrange("p u n -> p n u"),
             )
-            s["grn"] = grn
 
-        def regroup(src):
-            grn = p2.tile([P, N, 4], BF16, name="grn", tag="grn", align_bytes=64)
-            nc.vector.tensor_copy(
-                out=grn[:].rearrange("p (c i) j -> p c j i", i=4),
-                in_=src.rearrange("p j (c i) -> p c j i", i=4),
+        def transpose_x(g, h):
+            of(g)["word_bank%d" % h] = transpose_words(x_all[:, tiles_of(g), :], h)
+
+        def copy_x(g, h):
+            s = of(g)
+            if h == 0:
+                x_t = four.tile([P, PACK * D], BF16, name="x_t", tag="x_t", align_bytes=64)
+                s["x_t"] = x_t
+            copy_words(s["word_bank%d" % h], s["x_t"], h)
+
+        def quantise(codes, scales, values):
+            nc.vector.quantize_mx(out=codes.bitcast(FP8X4), scales=scales, in_=values)
+
+        def quantise_x(g):
+            s = of(g)
+            x_codes = five.tile([P, D], U32, name="x_codes", tag="x_codes", align_bytes=64)
+            x_scales = five.tile([P, D], U8, name="x_scales", tag="x_scales", align_bytes=64)
+            quantise(x_codes[:], x_scales[:], s["x_t"][:])
+            s["x_codes"], s["x_scales"] = x_codes, x_scales
+
+        def transpose_xhat(g, j):
+            s = of(g)
+            bank = for_scalar.tile([P, D], F32, name="xhat_bank", tag="bank")
+            for t in range(GT):
+                nc.tensor.transpose(bank[:, t * P : (t + 1) * P], s["xhat"][:, t, j * P : (j + 1) * P], ident[:])
+            s["xhat_bank%d" % j] = bank
+
+        def gain_and_shift1(g, j):
+            s = of(g)
+            if j == 0:
+                xn_planes = two.tile([P, PACK, D], BF16, name="xn_planes", tag="xn_planes")
+                s["xn_planes"] = xn_planes
+            nc.scalar.activation(
+                out=s["xn_planes"][:, j, :], in_=s["xhat_bank%d" % j][:], func=ACT.Identity,
+                scale=vec_cols[:, j : j + 1], bias=vec_cols[:, CHUNKS + j : CHUNKS + j + 1],
             )
-            return grn
 
-        def quant(codes, plane, flat):
-            nc.vector.quantize_mx(out=codes.bitcast(FP8X4), scales=plane, in_=flat)
+        def regrouped_views(planes):
+            grouped = two.tile([P, D, PACK], BF16, name="grouped", tag="grouped", align_bytes=64)
+            return (
+                grouped,
+                grouped[:].rearrange("p (n i) j -> p n j i", i=4),
+                planes.rearrange("p j (n i) -> p n j i", i=4),
+            )
 
-        def qn(g):
-            s = tiles(g)
-            if g in RG_V:
-                s["grn"] = regroup(s["xnt"][:])
-            cn = p2.tile([P, N], U32, name="cn", tag="cn", align_bytes=64)
-            pn = p2.tile([P, N], U8, name="pn", tag="pn", align_bytes=64)
-            quant(cn[:], pn[:], s["grn"][:].rearrange("p c j -> p (c j)"))
-            s["cn"], s["pn"] = cn, pn
+        def regroup_on_vector(planes):
+            grouped, dst, src = regrouped_views(planes)
+            nc.vector.tensor_copy(out=dst, in_=src)
+            return grouped
 
-        def mxp(g, t):
-            s = tiles(g)
-            bank = ps_v.tile([P, N], F32, name="preb", tag="vps")
+        def regroup_on_scalar(g):
+            grouped, dst, src = regrouped_views(of(g)["xn_planes"][:])
+            nc.scalar.copy(out=dst, in_=src)
+            of(g)["grouped"] = grouped
+
+        def quantise_xn(g):
+            s = of(g)
+            if g in ON_VECTOR:
+                s["grouped"] = regroup_on_vector(s["xn_planes"][:])
+            xn_codes = two.tile([P, D], U32, name="xn_codes", tag="xn_codes", align_bytes=64)
+            xn_scales = two.tile([P, D], U8, name="xn_scales", tag="xn_scales", align_bytes=64)
+            quantise(xn_codes[:], xn_scales[:], s["grouped"][:].rearrange("p n j -> p (n j)"))
+            s["xn_codes"], s["xn_scales"] = xn_codes, xn_scales
+
+        def pre_pass(g, t):
+            s = of(g)
+            bank = for_vector.tile([P, D], F32, name="pre_bank", tag="bank")
             nc.tensor.matmul_mx(
                 out=bank[:],
-                lhsT=s["cn"][:, t * P : (t + 1) * P].bitcast(FP8X4),
-                lhsT_scale=s["pn"][:, t * P : (t + 1) * P],
-                rhs=ws_c[:].bitcast(FP8X4),
-                rhs_scale=ws_p[:],
+                lhsT=s["xn_codes"][:, t * P : (t + 1) * P].bitcast(FP8X4),
+                lhsT_scale=s["xn_scales"][:, t * P : (t + 1) * P],
+                rhs=syn_codes[:].bitcast(FP8X4),
+                rhs_scale=syn_scales[:],
                 start=True,
                 stop=True,
             )
-            s["pre%d" % t] = bank
+            s["pre_bank%d" % t] = bank
 
-        def mxg(g, c):
-            s = tiles(g)
-            bank = ps_s.tile([P, N], F32, name="gtb", tag="sps")
+        def gate_pass(g, c):
+            s = of(g)
+            bank = for_scalar.tile([P, D], F32, name="gate_t_bank", tag="bank")
             nc.tensor.matmul_mx(
                 out=bank[:],
-                lhsT=wg_c[:, c * P : (c + 1) * P].bitcast(FP8X4),
-                lhsT_scale=wg_p[:, c * P : (c + 1) * P],
-                rhs=s["cx"][:].bitcast(FP8X4),
-                rhs_scale=s["px"][:],
+                lhsT=gate_codes[:, c * P : (c + 1) * P].bitcast(FP8X4),
+                lhsT_scale=gate_scales[:, c * P : (c + 1) * P],
+                rhs=s["x_codes"][:].bitcast(FP8X4),
+                rhs_scale=s["x_scales"][:],
                 start=True,
                 stop=True,
             )
-            s["gT%d" % c] = bank
+            s["gate_t_bank%d" % c] = bank
 
-        def sig(g, c):
-            s = tiles(g)
+        def sigmoid(g, c):
+            s = of(g)
             if c == 0:
-                gate_t = p2.tile([P, 4, N], F32, name="gate_t", tag="gate_t")
+                gate_t = two.tile([P, CHUNKS, D], F32, name="gate_t", tag="gate_t")
                 s["gate_t"] = gate_t
             nc.scalar.activation(
-                out=s["gate_t"][:, c, :], in_=s["gT%d" % c][:], func=ACT.Sigmoid, bias=cols[:, 8 + c : 9 + c]
+                out=s["gate_t"][:, c, :], in_=s["gate_t_bank%d" % c][:], func=ACT.Sigmoid,
+                bias=vec_cols[:, 2 * CHUNKS + c : 2 * CHUNKS + c + 1],
             )
 
-        def tb(g, t):
-            s = tiles(g)
-            bank = ps_v.tile([P, N], F32, name="gbb", tag="vps")
-            for c in range(4):
+        def gate_to_rows(g, t):
+            s = of(g)
+            bank = for_vector.tile([P, D], F32, name="gate_bank", tag="bank")
+            for c in range(CHUNKS):
                 nc.tensor.transpose(bank[:, c * P : (c + 1) * P], s["gate_t"][:, c, t * P : (t + 1) * P], ident[:])
-            s["gb%d" % t] = bank
+            s["gate_bank%d" % t] = bank
 
-        def pot_op(g, t):
-            s = tiles(g)
+        def potential(g, t):
+            s = of(g)
             if t == 0:
-                pot = p2.tile([P, GT, N], F32, name="pot", tag="pot")
+                pot = two.tile([P, GT, D], F32, name="pot", tag="pot")
                 s["pot"] = pot
             nc.vector.scalar_tensor_tensor(
-                out=s["pot"][:, t, :], in0=prev_all[:, g * GT + t, :], scalar=DECAY, in1=s["pre%d" % t][:],
+                out=s["pot"][:, t, :], in0=prev_all[:, g * GT + t, :], scalar=DECAY, in1=s["pre_bank%d" % t][:],
                 op0=ALU.mult, op1=ALU.add,
             )
 
-        def pld_tail(g):
-            s = tiles(g)
-            nc.sync.dma_start(out=pot_v[:, gsl(g), :], in_=s["pot"][:])
-            wk = p4.tile([P, GT, N], F32, name="wk", tag="wk")
-            s["wk"] = wk
+        def store_potential_and_start_blend(g):
+            s = of(g)
+            nc.sync.dma_start(out=pot_dram[:, tiles_of(g), :], in_=s["pot"][:])
+            res = four.tile([P, GT, D], F32, name="res", tag="res")
+            s["res"] = res
             for h in range(2):
-                ph = s["pot"][:, 2 * h : 2 * h + 2, :].rearrange("p t n -> p (t n)")
-                wh = wk[:, 2 * h : 2 * h + 2, :].rearrange("p t n -> p (t n)")
-                nc.vector.scalar_tensor_tensor(out=wh, in0=ph, scalar=SLOPE, in1=ph, op0=ALU.mult, op1=ALU.max)
+                pot_half = s["pot"][:, 2 * h : 2 * h + 2, :].rearrange("p t n -> p (t n)")
+                res_half = res[:, 2 * h : 2 * h + 2, :].rearrange("p t n -> p (t n)")
+                nc.vector.scalar_tensor_tensor(
+                    out=res_half, in0=pot_half, scalar=SLOPE, in1=pot_half, op0=ALU.mult, op1=ALU.max
+                )
             for h in range(2):
                 i0 = g * GT + 2 * h
                 nc.vector.tensor_tensor(
-                    out=wk[:, 2 * h : 2 * h + 2, :], in0=wk[:, 2 * h : 2 * h + 2, :], in1=x_all[:, i0 : i0 + 2, :],
+                    out=res[:, 2 * h : 2 * h + 2, :], in0=res[:, 2 * h : 2 * h + 2, :], in1=x_all[:, i0 : i0 + 2, :],
                     op=ALU.subtract,
                 )
 
-        def m_op(g, t):
-            s = tiles(g)
-            nc.vector.tensor_tensor(out=s["wk"][:, t, :], in0=s["wk"][:, t, :], in1=s["gb%d" % t][:], op=ALU.mult)
+        def times_gate(g, t):
+            s = of(g)
+            nc.vector.tensor_tensor(
+                out=s["res"][:, t, :], in0=s["res"][:, t, :], in1=s["gate_bank%d" % t][:], op=ALU.mult
+            )
 
-        def res(g):
-            s = tiles(g)
+        def plus_x(g):
+            s = of(g)
             for t in range(GT):
                 i = g * GT + t
                 nc.vector.scalar_tensor_tensor(
-                    out=s["wk"][:, t, :], in0=s["wk"][:, t, :], scalar=1.0, in1=x_all[:, i, :],
-                    op0=ALU.mult, op1=ALU.add, accum_out=sres[:, i : i + 1],
+                    out=s["res"][:, t, :], in0=s["res"][:, t, :], scalar=1.0, in1=x_all[:, i, :],
+                    op0=ALU.mult, op1=ALU.add, accum_out=sum2[:, i : i + 1],
                 )
 
-        def nmu2_op(g):
-            nc.scalar.mul(out=nmu2[:, gsl(g)], in_=sres[:, gsl(g)], mul=-1.0 / N)
+        def squared_deviations2(g):
+            nc.scalar.mul(out=neg_mean2[:, tiles_of(g)], in_=sum2[:, tiles_of(g)], mul=-1.0 / D)
+            for t in range(GT):
+                i = g * GT + t
+                nc.scalar.activation(
+                    out=junk_out(), in_=of(g)["res"][:, t, :], func=ACT.Square, bias=neg_mean2[:, i : i + 1],
+                    accum_out=sq_dev2[:, i : i + 1],
+                )
 
-        def square2(g, t):
-            i = g * GT + t
+        def rstd2_by_pow(g):
             nc.scalar.activation(
-                out=junk_ap(), in_=tiles(g)["wk"][:, t, :], func=ACT.Square, bias=nmu2[:, i : i + 1],
-                accum_out=ss2[:, i : i + 1],
+                out=var_eps2[:, tiles_of(g)], in_=sq_dev2[:, tiles_of(g)], func=ACT.Identity, scale=1.0 / D,
+                bias=eps_col[:, 0:1],
+            )
+            nc.gpsimd.tensor_tensor(
+                out=rstd2[:, tiles_of(g)], in0=var_eps2[:, tiles_of(g)], in1=minus_half[:, 0:GT], op=ALU.pow
             )
 
-        def ve2_op(lo, hi):
+        def std2_of_last_group():
             nc.scalar.activation(
-                out=ve2[:, lo:hi], in_=ss2[:, lo:hi], func=ACT.Identity, scale=1.0 / N, bias=epst[:, 0:1]
-            )
-            nc.gpsimd.tensor_tensor(out=rstd2[:, lo:hi], in0=ve2[:, lo:hi], in1=mhalf[:, 0 : hi - lo], op=ALU.pow)
-
-        def sqrt2_last(lo, hi):
-            base = (NG - 1) * GT
-            nc.scalar.activation(
-                out=sd2[:, lo:hi], in_=ss2[:, base + lo : base + hi], func=ACT.Sqrt, scale=1.0 / N, bias=epst[:, 0:1]
+                out=std2_last[:, 0:GT], in_=sq_dev2[:, tiles_of(LAST)], func=ACT.Sqrt, scale=1.0 / D,
+                bias=eps_col[:, 0:1],
             )
 
-        def o_op(g):
-            s = tiles(g)
+        def finish(g):
+            s = of(g)
             for t in range(GT):
                 i = g * GT + t
                 nc.vector.scalar_tensor_tensor(
-                    out=s["wk"][:, t, :], in0=s["wk"][:, t, :], scalar=nmu2[:, i : i + 1], in1=g_b[:],
+                    out=s["res"][:, t, :], in0=s["res"][:, t, :], scalar=neg_mean2[:, i : i + 1], in1=gamma2[:],
                     op0=ALU.add, op1=ALU.mult,
                 )
-            if g == NG - 1:
-                nc.vector.reciprocal(out=rstd2b[:], in_=sd2[:])
+            if g == LAST:
+                nc.vector.reciprocal(out=rstd2_last[:], in_=std2_last[:])
             for t in range(GT):
                 i = g * GT + t
                 nc.vector.scalar_tensor_tensor(
-                    out=s["wk"][:, t, :], in0=s["wk"][:, t, :],
-                    scalar=(rstd2b[:, t : t + 1] if g == NG - 1 else rstd2[:, i : i + 1]), in1=b_b[:],
+                    out=s["res"][:, t, :], in0=s["res"][:, t, :],
+                    scalar=(rstd2_last[:, t : t + 1] if g == LAST else rstd2[:, i : i + 1]), in1=beta2[:],
                     op0=ALU.mult, op1=ALU.add,
                 )
-                if g == NG - 1:
-                    nc.sync.dma_start(out=out_v[:, i, :], in_=s["wk"][:, t, :])
-            if g < NG - 1:
-                nc.sync.dma_start(out=out_v[:, gsl(g), :], in_=s["wk"][:])
+                if g == LAST:
+                    nc.sync.dma_start(out=out_dram[:, i, :], in_=s["res"][:, t, :])
+            if g < LAST:
+                nc.sync.dma_start(out=out_dram[:, tiles_of(g), :], in_=s["res"][:])
 
-        RG_V = (0, 1)
-
-        st_v(0)
-        pv = ps_s.tile([P, P], BF16, name="pv", tag="sps")
-        nc.tensor.transpose(pv[:], vt[:], identb[:])
-        nc.vector.tensor_copy(out=cols[:], in_=pv[:, 0:12])
-        wtx(0, 0)
-        wtx(0, 1)
-        xw_out(0, 0)
-        xw_out(0, 1)
-        sqrt1(0)
-        grs = regroup(ws_raw[:])
-        quant(ws_c[:], ws_p[:], grs[:].rearrange("p c j -> p (c j)"))
-        xh_v(0)
-        for b in range(3):
-            tx(0, b)
-        st_sum(2)
-        st_v(1)
-        qx(0)
-        grw = p4.tile([P, 4 * N], BF16, name="grw", tag="grx", align_bytes=64)
-        wbs = []
-        for b in range(4):
-            gbn(0, b)
-            if b == 0:
-                tx(0, 3)
-            elif b < 3:
-                wbs.append(words_tx(wg_raw[:], b - 1))
-            else:
-                wtx(1, 0)
-        sqrt1(1)
-        qn(0)
+        stats1_on_vector(0)
+        vec_bank = for_scalar.tile([P, P], BF16, name="vec_bank", tag="bank")
+        nc.tensor.transpose(vec_bank[:], vec_rows[:], ident_bf[:])
+        nc.vector.tensor_copy(out=vec_cols[:], in_=vec_bank[:, 0 : 3 * CHUNKS])
+        transpose_x(0, 0)
+        transpose_x(0, 1)
+        copy_x(0, 0)
+        copy_x(0, 1)
+        std1_on_scalar(0)
+        syn_grouped = regroup_on_vector(syn_rows[:])
+        quantise(syn_codes[:], syn_scales[:], syn_grouped[:].rearrange("p n j -> p (n j)"))
+        xhat_on_vector(0)
+        for j in range(SCALAR_BANKS):
+            transpose_xhat(0, j)
+        row_sums_on_scalar(SUMS_ON_SCALAR)
+        stats1_on_vector(1)
+        quantise_x(0)
+        gate_w_t = four.tile([P, PACK * D], BF16, name="gate_w_t", tag="x_t", align_bytes=64)
+        gain_and_shift1(0, 0)
+        transpose_xhat(0, 3)
+        gain_and_shift1(0, 1)
+        gate_w_bank0 = transpose_words(gate_w_rows[:], 0)
+        gain_and_shift1(0, 2)
+        gate_w_bank1 = transpose_words(gate_w_rows[:], 1)
+        gain_and_shift1(0, 3)
+        transpose_x(1, 0)
+        std1_on_scalar(1)
+        quantise_xn(0)
         for t in range(GT):
-            mxp(0, t)
-        words_out(wbs[0], grw, 0, False)
-        wtx(1, 1)
-        words_out(wbs[1], grw, 1, False)
-        wtx(2, 0)
-        quant(wg_c[:], wg_p[:], grw[:])
-        xw_out(1, 0)
-        wtx(2, 1)
-        xw_out(1, 1)
-        wtx(3, 0)
-        xw_out(2, 0)
-        wtx(3, 1)
-        xw_out(2, 1)
-        mxg(0, 0)
-        nm1_op(2)
-        st_sq(2)
+            pre_pass(0, t)
+        copy_words(gate_w_bank0, gate_w_t, 0)
+        transpose_x(1, 1)
+        copy_words(gate_w_bank1, gate_w_t, 1)
+        transpose_x(2, 0)
+        quantise(gate_codes[:], gate_scales[:], gate_w_t[:])
+        copy_x(1, 0)
+        transpose_x(2, 1)
+        copy_x(1, 1)
+        transpose_x(3, 0)
+        copy_x(2, 0)
+        transpose_x(3, 1)
+        copy_x(2, 1)
+        gate_pass(0, 0)
+        neg_mean1_from_scalar_sums(SUMS_ON_SCALAR)
+        squared_deviations1(SUMS_ON_SCALAR)
 
-        def iteration(g):
-            if ok(g):
+        def round_of_pipeline(g):
+            if exists(g):
                 for t in range(GT):
-                    m_op(g, t)
-            if ok(g + 1) and g >= 0:
-                qn(g + 1)
+                    times_gate(g, t)
+            if g >= 0 and exists(g + 1):
+                quantise_xn(g + 1)
                 for t in range(GT):
-                    mxp(g + 1, t)
-            if ok(g + 2) and g >= 0:
-                xh_s(g + 2)
-            if ok(g + 3):
-                ve1_op(g + 3)
+                    pre_pass(g + 1, t)
+            if g >= 0 and exists(g + 2):
+                xhat_on_scalar(g + 2)
+            if exists(g + 3):
+                rstd1_by_pow(g + 3)
             for h in range(2):
-                if ok(g + 4):
-                    xw_out(g + 4, h)
-                if ok(g + 1):
-                    mxg(g + 1, h + 1)
-            for c in range(4):
-                if ok(g + 1):
-                    sig(g + 1, c)
+                if exists(g + 4):
+                    copy_x(g + 4, h)
+                if exists(g + 1):
+                    gate_pass(g + 1, h + 1)
+            for c in range(CHUNKS):
+                if exists(g + 1):
+                    sigmoid(g + 1, c)
                     if c == 0:
-                        mxg(g + 1, 3)
+                        gate_pass(g + 1, CHUNKS - 1)
                 if g == -1 and c == 0:
-                    xh_v(1)
-                if ok(g + 2) and c > 0:
-                    tx(g + 2, c - 1)
-            if ok(g + 1):
-                tb(g + 1, 0)
-            if g + 1 == NG - 1:
-                nc.scalar.activation(out=dummy[:, 1:2], in_=epst[:, 0:1], func=ACT.Sqrt)
-            if ok(g):
-                res(g)
-                nmu2_op(g)
+                    xhat_on_vector(1)
+                if exists(g + 2) and c > 0:
+                    transpose_xhat(g + 2, c - 1)
+            if exists(g + 1):
+                gate_to_rows(g + 1, 0)
+            if g + 1 == LAST:
+                nc.scalar.activation(out=table_warmer[:, 1:2], in_=eps_col[:, 0:1], func=ACT.Sqrt)
+            if exists(g):
+                plus_x(g)
+                squared_deviations2(g)
+                if g == LAST:
+                    std2_of_last_group()
+            if exists(g + 1):
                 for t in range(GT):
-                    square2(g, t)
-                if g == NG - 1:
-                    sqrt2_last(0, GT)
-            if ok(g + 1):
-                for t in range(GT):
-                    pot_op(g + 1, t)
+                    potential(g + 1, t)
                     if t + 1 < GT:
-                        tb(g + 1, t + 1)
-                pld_tail(g + 1)
-            if ok(g + 3):
-                nmr1_v(g + 3)
+                        gate_to_rows(g + 1, t + 1)
+                store_potential_and_start_blend(g + 1)
+            if exists(g + 3):
+                neg_mean_times_rstd1(g + 3)
             if g == -1:
-                qx(1)
-                qx(2)
-            if ok(g + 4):
-                qx(g + 4)
-            for b in range(4):
-                if ok(g + 2):
-                    gbn(g + 2, b)
-                if b == 0 and ok(g + 2):
-                    tx(g + 2, 3)
-                if b == 1:
-                    if ok(g + 4):
-                        sumx(g + 4)
-                    if ok(g) and g < NG - 1:
-                        ve2_op(g * GT, g * GT + GT)
-                if b >= 2 and ok(g + 5):
-                    wtx(g + 5, b - 2)
-            if ok(g + 2) and g + 2 not in RG_V:
-                regroup_s(g + 2)
-            if ok(g + 4):
-                nm1_pe(g + 4)
-            if ok(g + 2):
-                mxg(g + 2, 0)
-            if ok(g + 4):
-                st_sq(g + 4)
-            if ok(g - 1):
-                o_op(g - 1)
+                quantise_x(1)
+                quantise_x(2)
+            if exists(g + 4):
+                quantise_x(g + 4)
+            for j in range(PACK):
+                if exists(g + 2):
+                    gain_and_shift1(g + 2, j)
+                if j == 0 and exists(g + 2):
+                    transpose_xhat(g + 2, PACK - 1)
+                if j == 1:
+                    if exists(g + 4):
+                        row_sums_on_tensor(g + 4)
+                    if exists(g) and g < LAST:
+                        rstd2_by_pow(g)
+                if j >= 2 and exists(g + 5):
+                    transpose_x(g + 5, j - 2)
+            if exists(g + 2) and g + 2 not in ON_VECTOR:
+                regroup_on_scalar(g + 2)
+            if exists(g + 4):
+                neg_mean1_from_tensor_sums(g + 4)
+            if exists(g + 2):
+                gate_pass(g + 2, 0)
+            if exists(g + 4):
+                squared_deviations1(g + 4)
+            if exists(g - 1):
+                finish(g - 1)
 
-        for g in range(-1, NG + 1):
-            iteration(g)
+        for g in range(-1, GROUPS + 1):
+            round_of_pipeline(g)

@@ -26,9 +26,10 @@ SLOPE = 0.01
 SUM_COLS = 32
 JUNK_BUFS = 8
 SCALAR_BANKS = 3
-VECTOR_BANKS = 5
+VECTOR_BANKS = 4
 ON_VECTOR = (0, 1)
 SUMS_ON_SCALAR = 2
+SCALAR_RUNS = 96
 
 FLOPS = 2 * 2 * ROWS * D * D
 
@@ -45,6 +46,7 @@ def tile_mnelayer_pa_t_kernel(
         five = ctx.enter_context(tc.tile_pool(name="five", bufs=5))
         for_scalar = ctx.enter_context(tc.psum_pool(name="for_scalar", bufs=SCALAR_BANKS))
         for_vector = ctx.enter_context(tc.psum_pool(name="for_vector", bufs=VECTOR_BANKS))
+        constants = ctx.enter_context(tc.psum_pool(name="constants", bufs=1))
 
         x_dram = inputs.rearrange("(p i) k -> p i k", i=TILES)
         prev_dram = prev_potential.rearrange("(p i) k -> p i k", i=TILES)
@@ -56,12 +58,11 @@ def tile_mnelayer_pa_t_kernel(
         gate_w_rows = const.tile([P, CHUNKS, D], BF16, name="gate_w_rows")
         syn_rows = const.tile([P, PACK, D], BF16, name="syn_rows")
         vec_rows = const.tile([P, P], BF16, name="vec_rows")
-        gamma2 = const.tile([P, D], BF16, name="gamma2")
-        beta2 = const.tile([P, D], BF16, name="beta2")
+        ln_rows = const.tile([P, 2, D], BF16, name="ln_rows")
         vec_cols = const.tile([P, 3 * CHUNKS], F32, name="vec_cols")
-        minus_half = const.tile([P, GT], F32, name="minus_half")
+        minus_half = const.tile([P, 2 * GT], F32, name="minus_half")
         eps_col = const.tile([P, 1], F32, name="eps_col")
-        ones = const.tile([P, SUM_COLS], BF16, name="ones")
+        ones = const.tile([P, P], BF16, name="ones")
         ident = const.tile([P, P], F32, name="ident")
         ident_bf = const.tile([P, P], BF16, name="ident_bf")
         junk = const.tile([P, JUNK_BUFS, D], BF16, name="junk")
@@ -75,14 +76,14 @@ def tile_mnelayer_pa_t_kernel(
         sum1 = const.tile([P, GT], F32, name="sum1")
         neg_mean1 = const.tile([P, TILES], F32, name="neg_mean1")
         sq_dev1 = const.tile([P, TILES], F32, name="sq_dev1")
-        var_eps1 = const.tile([P, TILES], F32, name="var_eps1")
-        rstd1 = const.tile([P, TILES], F32, name="rstd1")
+        var_eps_all = const.tile([P, GROUPS + GT, 2 * GT], F32, name="var_eps_all")
+        rstd_all = const.tile([P, GROUPS + GT, 2 * GT], F32, name="rstd_all")
+        rstd1_of, rstd2_of = {}, {}
+        rstd1 = const.tile([P, len(ON_VECTOR) * GT], F32, name="rstd1")
         neg_mean_rstd1 = const.tile([P, TILES], F32, name="neg_mean_rstd1")
         sum2 = const.tile([P, TILES], F32, name="sum2")
         neg_mean2 = const.tile([P, TILES], F32, name="neg_mean2")
         sq_dev2 = const.tile([P, TILES], F32, name="sq_dev2")
-        var_eps2 = const.tile([P, TILES], F32, name="var_eps2")
-        rstd2 = const.tile([P, TILES], F32, name="rstd2")
         std1 = const.tile([P, len(ON_VECTOR) * GT], F32, name="std1")
         std2_last = const.tile([P, GT], F32, name="std2_last")
         rstd2_last = const.tile([P, GT], F32, name="rstd2_last")
@@ -94,6 +95,7 @@ def tile_mnelayer_pa_t_kernel(
         def exists(g):
             return 0 <= g < GROUPS
 
+        nc.gpsimd.memset(ln_rows[:], 0.0)
         nc.vector.memset(vec_rows[:], 0.0)
         nc.vector.memset(minus_half[:], -0.5)
         nc.vector.memset(eps_col[:], EPS)
@@ -112,8 +114,8 @@ def tile_mnelayer_pa_t_kernel(
         nc.sync.dma_start(out=x_all[:, 2:4, :], in_=x_dram[:, 2:4, :])
         for a, vec in enumerate((pre_gamma, pre_beta, gate_b)):
             nc.sync.dma_start(out=vec_rows[a * CHUNKS : (a + 1) * CHUNKS, :], in_=vec.rearrange("(j p) -> j p", p=P))
-        nc.sync.dma_start(out=syn_rows[:], in_=syn_weights.rearrange("(j p) n -> p j n", p=P))
         load_x(1)
+        nc.sync.dma_start(out=syn_rows[:], in_=syn_weights.rearrange("(j p) n -> p j n", p=P))
         load_x(2)
         nc.sync.dma_start(out=gate_w_rows[:], in_=gate_W.rearrange("(c m) k -> m c k", m=P))
         load_prev(0)
@@ -121,8 +123,8 @@ def tile_mnelayer_pa_t_kernel(
         load_x(4)
         load_prev(1)
         load_x(5)
-        nc.sync.dma_start(out=gamma2[:], in_=ln_gamma.partition_broadcast(P))
-        nc.sync.dma_start(out=beta2[:], in_=ln_beta.partition_broadcast(P))
+        for a, vec in enumerate((ln_gamma, ln_beta)):
+            nc.sync.dma_start(out=ln_rows[0:1, a, :], in_=vec.rearrange("(a n) -> a n", a=1))
         load_prev(2)
         load_x(6)
         load_prev(3)
@@ -177,7 +179,7 @@ def tile_mnelayer_pa_t_kernel(
             for t in range(GT):
                 for v in range(PACK):
                     nc.tensor.matmul(
-                        out=sums[:, t, :], lhsT=x_t[:, t * P : (t + 1) * P, v], rhs=ones[:],
+                        out=sums[:, t, :], lhsT=x_t[:, t * P : (t + 1) * P, v], rhs=ones[:, 0:SUM_COLS],
                         start=(v == 0), stop=(v == PACK - 1),
                     )
             of(g)["sums"] = sums
@@ -185,27 +187,36 @@ def tile_mnelayer_pa_t_kernel(
         def neg_mean1_from_tensor_sums(g):
             nc.scalar.mul(out=neg_mean1[:, tiles_of(g)], in_=of(g)["sums"][:, :, 0], mul=-1.0 / D)
 
-        def squared_deviations1(g):
-            for i in range(g * GT, (g + 1) * GT):
+        def squared_deviations1(g, tiles=range(GT)):
+            for t in tiles:
+                i = g * GT + t
                 nc.scalar.activation(
                     out=junk_out(), in_=x_all[:, i, :], func=ACT.Square, bias=neg_mean1[:, i : i + 1],
                     accum_out=sq_dev1[:, i : i + 1],
                 )
 
-        def rstd1_by_pow(g):
-            nc.scalar.activation(
-                out=var_eps1[:, tiles_of(g)], in_=sq_dev1[:, tiles_of(g)], func=ACT.Identity, scale=1.0 / D,
-                bias=eps_col[:, 0:1],
-            )
+        def norm_scales(g1, g2):
+            turn = g1 - SUMS_ON_SCALAR if exists(g1) else g2 + GT
+            var_eps, rstd = var_eps_all[:, turn, :], rstd_all[:, turn, :]
+            parts = []
+            if exists(g1):
+                parts.append((0, sq_dev1[:, tiles_of(g1)], 1.0 / D))
+                rstd1_of[g1] = rstd[:, 0:GT]
+            if exists(g2):
+                parts.append((GT, sq_dev2[:, tiles_of(g2)], 1.0 / D**3))
+                rstd2_of[g2] = rstd[:, GT : 2 * GT]
+            for col, sq_dev, factor in parts:
+                nc.gpsimd.tensor_scalar(
+                    out=var_eps[:, col : col + GT], in0=sq_dev, scalar1=factor, scalar2=EPS, op0=ALU.mult, op1=ALU.add
+                )
+            cols = slice(parts[0][0], parts[-1][0] + GT)
             nc.gpsimd.tensor_tensor(
-                out=rstd1[:, tiles_of(g)], in0=var_eps1[:, tiles_of(g)], in1=minus_half[:], op=ALU.pow
+                out=rstd[:, cols], in0=var_eps[:, cols], in1=minus_half[:, 0 : len(parts) * GT], op=ALU.pow
             )
-
-        def neg_mean_times_rstd1(g):
-            nc.vector.tensor_tensor(
-                out=neg_mean_rstd1[:, tiles_of(g)], in0=neg_mean1[:, tiles_of(g)], in1=rstd1[:, tiles_of(g)],
-                op=ALU.mult,
-            )
+            if exists(g1):
+                nc.gpsimd.tensor_tensor(
+                    out=neg_mean_rstd1[:, tiles_of(g1)], in0=neg_mean1[:, tiles_of(g1)], in1=rstd1_of[g1], op=ALU.mult
+                )
 
         def xhat_on_scalar(g):
             xhat = two.tile([P, GT, D], F32, name="xhat", tag="xhat")
@@ -214,7 +225,7 @@ def tile_mnelayer_pa_t_kernel(
                 i = g * GT + t
                 nc.scalar.activation(
                     out=xhat[:, t, :], in_=x_all[:, i, :], func=ACT.Identity,
-                    scale=rstd1[:, i : i + 1], bias=neg_mean_rstd1[:, i : i + 1],
+                    scale=rstd1_of[g][:, t : t + 1], bias=neg_mean_rstd1[:, i : i + 1],
                 )
 
         def transpose_words(rows, h):
@@ -281,15 +292,22 @@ def tile_mnelayer_pa_t_kernel(
             nc.vector.tensor_copy(out=dst, in_=src)
             return grouped
 
+        def regroup_on_gpsimd(planes):
+            grouped, dst, src = regrouped_views(planes)
+            nc.gpsimd.tensor_scalar(out=dst, in0=src, scalar1=1.0, scalar2=0.0, op0=ALU.mult, op1=ALU.add)
+            return grouped
+
         def regroup_on_scalar(g):
-            grouped, dst, src = regrouped_views(of(g)["xn_planes"][:])
-            nc.scalar.copy(out=dst, in_=src)
-            of(g)["grouped"] = grouped
+            s = of(g)
+            s["grouped"], s["regroup_to"], s["regroup_from"] = regrouped_views(s["xn_planes"][:])
+            nc.scalar.copy(out=s["regroup_to"][:, 0:SCALAR_RUNS], in_=s["regroup_from"][:, 0:SCALAR_RUNS])
 
         def quantise_xn(g):
             s = of(g)
             if g in ON_VECTOR:
                 s["grouped"] = regroup_on_vector(s["xn_planes"][:])
+            elif SCALAR_RUNS < D // 4:
+                nc.vector.tensor_copy(out=s["regroup_to"][:, SCALAR_RUNS:], in_=s["regroup_from"][:, SCALAR_RUNS:])
             xn_codes = two.tile([P, D], U32, name="xn_codes", tag="xn_codes", align_bytes=64)
             xn_scales = two.tile([P, D], U8, name="xn_scales", tag="xn_scales", align_bytes=64)
             quantise(xn_codes[:], xn_scales[:], s["grouped"][:].rearrange("p n j -> p (n j)"))
@@ -350,9 +368,11 @@ def tile_mnelayer_pa_t_kernel(
                 op0=ALU.mult, op1=ALU.add,
             )
 
-        def store_potential_and_start_blend(g):
+        def store_potential(g):
+            nc.sync.dma_start(out=pot_dram[:, tiles_of(g), :], in_=of(g)["pot"][:])
+
+        def leaky_relu(g):
             s = of(g)
-            nc.sync.dma_start(out=pot_dram[:, tiles_of(g), :], in_=s["pot"][:])
             res = four.tile([P, GT, D], F32, name="res", tag="res")
             s["res"] = res
             for h in range(2):
@@ -361,11 +381,12 @@ def tile_mnelayer_pa_t_kernel(
                 nc.vector.scalar_tensor_tensor(
                     out=res_half, in0=pot_half, scalar=SLOPE, in1=pot_half, op0=ALU.mult, op1=ALU.max
                 )
-            for h in range(2):
-                i0 = g * GT + 2 * h
-                nc.vector.tensor_tensor(
-                    out=res[:, 2 * h : 2 * h + 2, :], in0=res[:, 2 * h : 2 * h + 2, :], in1=x_all[:, i0 : i0 + 2, :],
-                    op=ALU.subtract,
+
+        def minus_x(g):
+            for t in range(GT):
+                engine = nc.vector if g * GT + t < 6 else nc.gpsimd
+                engine.tensor_tensor(
+                    out=of(g)["res"][:, t, :], in0=of(g)["res"][:, t, :], in1=x_all[:, g * GT + t, :], op=ALU.subtract
                 )
 
         def times_gate(g, t):
@@ -384,26 +405,17 @@ def tile_mnelayer_pa_t_kernel(
                 )
 
         def squared_deviations2(g):
-            nc.scalar.mul(out=neg_mean2[:, tiles_of(g)], in_=sum2[:, tiles_of(g)], mul=-1.0 / D)
             for t in range(GT):
                 i = g * GT + t
                 nc.scalar.activation(
-                    out=junk_out(), in_=of(g)["res"][:, t, :], func=ACT.Square, bias=neg_mean2[:, i : i + 1],
+                    out=junk_out(), in_=of(g)["res"][:, t, :], func=ACT.Square, scale=-float(D), bias=sum2[:, i : i + 1],
                     accum_out=sq_dev2[:, i : i + 1],
                 )
-
-        def rstd2_by_pow(g):
-            nc.scalar.activation(
-                out=var_eps2[:, tiles_of(g)], in_=sq_dev2[:, tiles_of(g)], func=ACT.Identity, scale=1.0 / D,
-                bias=eps_col[:, 0:1],
-            )
-            nc.gpsimd.tensor_tensor(
-                out=rstd2[:, tiles_of(g)], in0=var_eps2[:, tiles_of(g)], in1=minus_half[:, 0:GT], op=ALU.pow
-            )
+            nc.scalar.mul(out=neg_mean2[:, tiles_of(g)], in_=sum2[:, tiles_of(g)], mul=-1.0 / D)
 
         def std2_of_last_group():
             nc.scalar.activation(
-                out=std2_last[:, 0:GT], in_=sq_dev2[:, tiles_of(LAST)], func=ACT.Sqrt, scale=1.0 / D,
+                out=std2_last[:, 0:GT], in_=sq_dev2[:, tiles_of(LAST)], func=ACT.Sqrt, scale=1.0 / D**3,
                 bias=eps_col[:, 0:1],
             )
 
@@ -412,7 +424,7 @@ def tile_mnelayer_pa_t_kernel(
             for t in range(GT):
                 i = g * GT + t
                 nc.vector.scalar_tensor_tensor(
-                    out=s["res"][:, t, :], in0=s["res"][:, t, :], scalar=neg_mean2[:, i : i + 1], in1=gamma2[:],
+                    out=s["res"][:, t, :], in0=s["res"][:, t, :], scalar=neg_mean2[:, i : i + 1], in1=gain_shift2[:, 0, :],
                     op0=ALU.add, op1=ALU.mult,
                 )
             if g == LAST:
@@ -421,7 +433,7 @@ def tile_mnelayer_pa_t_kernel(
                 i = g * GT + t
                 nc.vector.scalar_tensor_tensor(
                     out=s["res"][:, t, :], in0=s["res"][:, t, :],
-                    scalar=(rstd2_last[:, t : t + 1] if g == LAST else rstd2[:, i : i + 1]), in1=beta2[:],
+                    scalar=(rstd2_last[:, t : t + 1] if g == LAST else rstd2_of[g][:, t : t + 1]), in1=gain_shift2[:, 1, :],
                     op0=ALU.mult, op1=ALU.add,
                 )
                 if g == LAST:
@@ -429,122 +441,141 @@ def tile_mnelayer_pa_t_kernel(
             if g < LAST:
                 nc.sync.dma_start(out=out_dram[:, tiles_of(g), :], in_=s["res"][:])
 
-        stats1_on_vector(0)
-        vec_bank = for_scalar.tile([P, P], BF16, name="vec_bank", tag="bank")
-        nc.tensor.transpose(vec_bank[:], vec_rows[:], ident_bf[:])
-        nc.vector.tensor_copy(out=vec_cols[:], in_=vec_bank[:, 0 : 3 * CHUNKS])
+        syn_grouped = regroup_on_gpsimd(syn_rows[:])
         transpose_x(0, 0)
         transpose_x(0, 1)
+        vec_bank = for_scalar.tile([P, P], BF16, name="vec_bank", tag="bank")
+        nc.tensor.transpose(vec_bank[:], vec_rows[:], ident_bf[:])
+        stats1_on_vector(0)
+        std1_on_scalar(0)
         copy_x(0, 0)
         copy_x(0, 1)
-        std1_on_scalar(0)
-        syn_grouped = regroup_on_vector(syn_rows[:])
-        quantise(syn_codes[:], syn_scales[:], syn_grouped[:].rearrange("p n j -> p (n j)"))
+        nc.scalar.copy(out=vec_cols[:], in_=vec_bank[:, 0 : 3 * CHUNKS])
         xhat_on_vector(0)
         for j in range(SCALAR_BANKS):
             transpose_xhat(0, j)
-        row_sums_on_scalar(SUMS_ON_SCALAR)
         stats1_on_vector(1)
-        quantise_x(0)
-        gate_w_t = four.tile([P, PACK * D], BF16, name="gate_w_t", tag="x_t", align_bytes=64)
         gain_and_shift1(0, 0)
         transpose_xhat(0, 3)
         gain_and_shift1(0, 1)
+        gate_w_t = four.tile([P, PACK * D], BF16, name="gate_w_t", tag="x_t", align_bytes=64)
         gate_w_bank0 = transpose_words(gate_w_rows[:], 0)
         gain_and_shift1(0, 2)
         gate_w_bank1 = transpose_words(gate_w_rows[:], 1)
         gain_and_shift1(0, 3)
-        transpose_x(1, 0)
+        transpose_x(2, 0)
         std1_on_scalar(1)
         quantise_xn(0)
+        quantise(syn_codes[:], syn_scales[:], syn_grouped[:].rearrange("p n j -> p (n j)"))
+        xhat_on_vector(1)
+        copy_words(gate_w_bank0, gate_w_t, 0)
+        transpose_x(2, 1)
+        copy_words(gate_w_bank1, gate_w_t, 1)
+        nc.scalar.activation(out=table_warmer[:, 1:2], in_=eps_col[:, 0:1], func=ACT.Sigmoid)
+        transpose_x(1, 0)
         for t in range(GT):
             pre_pass(0, t)
-        copy_words(gate_w_bank0, gate_w_t, 0)
-        transpose_x(1, 1)
-        copy_words(gate_w_bank1, gate_w_t, 1)
-        transpose_x(2, 0)
-        quantise(gate_codes[:], gate_scales[:], gate_w_t[:])
-        copy_x(1, 0)
-        transpose_x(2, 1)
-        copy_x(1, 1)
-        transpose_x(3, 0)
         copy_x(2, 0)
-        transpose_x(3, 1)
+        transpose_x(1, 1)
         copy_x(2, 1)
-        gate_pass(0, 0)
-        neg_mean1_from_scalar_sums(SUMS_ON_SCALAR)
-        squared_deviations1(SUMS_ON_SCALAR)
+        row_sums_on_tensor(2)
+        copy_x(1, 0)
+        transpose_xhat(1, 0)
+        copy_x(1, 1)
+        transpose_xhat(1, 1)
+        quantise(gate_codes[:], gate_scales[:], gate_w_t[:])
+        for t in range(GT):
+            potential(0, t)
+        store_potential(0)
+        neg_mean1_from_tensor_sums(2)
+        transpose_xhat(1, 2)
+        squared_deviations1(2)
+        quantise_x(0)
+        for j in range(PACK):
+            gain_and_shift1(1, j)
+            if j == 0:
+                transpose_xhat(1, 3)
+            else:
+                gate_pass(0, j - 1)
+        quantise_x(1)
 
-        def round_of_pipeline(g):
-            if exists(g):
-                for t in range(GT):
-                    times_gate(g, t)
-            if g >= 0 and exists(g + 1):
-                quantise_xn(g + 1)
-                for t in range(GT):
-                    pre_pass(g + 1, t)
-            if g >= 0 and exists(g + 2):
-                xhat_on_scalar(g + 2)
-            if exists(g + 3):
-                rstd1_by_pow(g + 3)
-            for h in range(2):
-                if exists(g + 4):
-                    copy_x(g + 4, h)
-                if exists(g + 1):
-                    gate_pass(g + 1, h + 1)
+        gain_shift2 = constants.tile([P, 2, D], BF16, name="gain_shift2")
+        for a in range(2):
+            nc.tensor.matmul(out=gain_shift2[:, a, :], lhsT=ones[:], rhs=ln_rows[:, a, :], start=True, stop=True)
+
+        def round_of_pipeline(r):
             for c in range(CHUNKS):
-                if exists(g + 1):
-                    sigmoid(g + 1, c)
-                    if c == 0:
-                        gate_pass(g + 1, CHUNKS - 1)
-                if g == -1 and c == 0:
-                    xhat_on_vector(1)
-                if exists(g + 2) and c > 0:
-                    transpose_xhat(g + 2, c - 1)
-            if exists(g + 1):
-                gate_to_rows(g + 1, 0)
-            if g + 1 == LAST:
-                nc.scalar.activation(out=table_warmer[:, 1:2], in_=eps_col[:, 0:1], func=ACT.Sqrt)
-            if exists(g):
-                plus_x(g)
-                squared_deviations2(g)
-                if g == LAST:
-                    std2_of_last_group()
-            if exists(g + 1):
+                if exists(r + 1):
+                    sigmoid(r + 1, c)
+                if c == 0 and exists(r + 1):
+                    gate_pass(r + 1, CHUNKS - 1)
+                if c in (1, 2) and exists(r + 4):
+                    transpose_x(r + 4, c - 1)
+            if r == -1:
                 for t in range(GT):
-                    potential(g + 1, t)
-                    if t + 1 < GT:
-                        gate_to_rows(g + 1, t + 1)
-                store_potential_and_start_blend(g + 1)
-            if exists(g + 3):
-                neg_mean_times_rstd1(g + 3)
-            if g == -1:
-                quantise_x(1)
-                quantise_x(2)
-            if exists(g + 4):
-                quantise_x(g + 4)
-            for j in range(PACK):
-                if exists(g + 2):
-                    gain_and_shift1(g + 2, j)
-                if j == 0 and exists(g + 2):
-                    transpose_xhat(g + 2, PACK - 1)
-                if j == 1:
-                    if exists(g + 4):
-                        row_sums_on_tensor(g + 4)
-                    if exists(g) and g < LAST:
-                        rstd2_by_pow(g)
-                if j >= 2 and exists(g + 5):
-                    transpose_x(g + 5, j - 2)
-            if exists(g + 2) and g + 2 not in ON_VECTOR:
-                regroup_on_scalar(g + 2)
-            if exists(g + 4):
-                neg_mean1_from_tensor_sums(g + 4)
-            if exists(g + 2):
-                gate_pass(g + 2, 0)
-            if exists(g + 4):
-                squared_deviations1(g + 4)
-            if exists(g - 1):
-                finish(g - 1)
+                    gate_to_rows(0, t)
+            if r + 1 == LAST:
+                nc.scalar.activation(out=table_warmer[:, 1:2], in_=eps_col[:, 0:1], func=ACT.Sqrt)
+            if exists(r + 4):
+                copy_x(r + 4, 0)
+                copy_x(r + 4, 1)
+                row_sums_on_tensor(r + 4)
+            if exists(r):
+                plus_x(r)
+                squared_deviations2(r)
+                if r == LAST:
+                    std2_of_last_group()
+            if exists(r + 3):
+                quantise_x(r + 3)
+            if exists(r + 2) and r >= 0:
+                quantise_xn(r + 2)
+                for t in range(GT):
+                    pre_pass(r + 2, t)
+            if exists(r + 1):
+                leaky_relu(r + 1)
+            if exists(r + 3) or (exists(r) and r < LAST):
+                norm_scales(r + 3, r if r < LAST else GROUPS)
+            if exists(r + 1):
+                minus_x(r + 1)
+            if r == -1:
+                quantise_xn(1)
+                for t in range(GT):
+                    times_gate(0, t)
+                    pre_pass(1, t)
+            if exists(r + 4):
+                neg_mean1_from_tensor_sums(r + 4)
+                squared_deviations1(r + 4, range(3))
+            if exists(r + 3):
+                xhat_on_scalar(r + 3)
+                if r != 0:
+                    for j in range(SCALAR_BANKS):
+                        transpose_xhat(r + 3, j)
+            if exists(r + 4):
+                squared_deviations1(r + 4, range(3, GT))
+            if exists(r - 1):
+                finish(r - 1)
+            for t in range(GT):
+                if exists(r + 2):
+                    potential(r + 2, t)
+                if exists(r + 1) and r >= 0:
+                    gate_to_rows(r + 1, t)
+            for t in range(GT):
+                if r == 0 and t == 0:
+                    for j in range(SCALAR_BANKS):
+                        transpose_xhat(r + 3, j)
+                if exists(r + 3):
+                    gain_and_shift1(r + 3, t)
+                    if t == 0:
+                        transpose_xhat(r + 3, 3)
+                if t > 0 and exists(r + 2):
+                    gate_pass(r + 2, t - 1)
+            if exists(r + 2):
+                store_potential(r + 2)
+            if exists(r + 3):
+                regroup_on_scalar(r + 3)
+            if exists(r + 1) and r >= 0:
+                for t in range(GT):
+                    times_gate(r + 1, t)
 
-        for g in range(-1, GROUPS + 1):
-            round_of_pipeline(g)
+        for r in range(-1, GROUPS + 1):
+            round_of_pipeline(r)

@@ -60,7 +60,7 @@ def tile_mnelayer_pa_t_kernel(
         vec_rows = const.tile([P, P], BF16, name="vec_rows")
         ln_rows = const.tile([P, 2, D], BF16, name="ln_rows")
         vec_cols = const.tile([P, 3 * CHUNKS], F32, name="vec_cols")
-        minus_half = const.tile([P, 2 * GT], F32, name="minus_half")
+        minus_half = const.tile([P, GT], F32, name="minus_half")
         eps_col = const.tile([P, 1], F32, name="eps_col")
         ones = const.tile([P, P], BF16, name="ones")
         ident = const.tile([P, P], F32, name="ident")
@@ -76,10 +76,10 @@ def tile_mnelayer_pa_t_kernel(
         sum1 = const.tile([P, GT], F32, name="sum1")
         neg_mean1 = const.tile([P, TILES], F32, name="neg_mean1")
         sq_dev1 = const.tile([P, TILES], F32, name="sq_dev1")
-        var_eps_all = const.tile([P, GROUPS + GT, 2 * GT], F32, name="var_eps_all")
-        rstd_all = const.tile([P, GROUPS + GT, 2 * GT], F32, name="rstd_all")
-        rstd1_of, rstd2_of = {}, {}
-        rstd1 = const.tile([P, len(ON_VECTOR) * GT], F32, name="rstd1")
+        var_eps1 = const.tile([P, TILES], F32, name="var_eps1")
+        rstd1 = const.tile([P, TILES], F32, name="rstd1")
+        var_eps2 = const.tile([P, TILES], F32, name="var_eps2")
+        rstd2 = const.tile([P, TILES], F32, name="rstd2")
         neg_mean_rstd1 = const.tile([P, TILES], F32, name="neg_mean_rstd1")
         sum2 = const.tile([P, TILES], F32, name="sum2")
         neg_mean2 = const.tile([P, TILES], F32, name="neg_mean2")
@@ -195,28 +195,27 @@ def tile_mnelayer_pa_t_kernel(
                     accum_out=sq_dev1[:, i : i + 1],
                 )
 
-        def norm_scales(g1, g2):
-            turn = g1 - SUMS_ON_SCALAR if exists(g1) else g2 + GT
-            var_eps, rstd = var_eps_all[:, turn, :], rstd_all[:, turn, :]
-            parts = []
-            if exists(g1):
-                parts.append((0, sq_dev1[:, tiles_of(g1)], 1.0 / D))
-                rstd1_of[g1] = rstd[:, 0:GT]
-            if exists(g2):
-                parts.append((GT, sq_dev2[:, tiles_of(g2)], 1.0 / D**3))
-                rstd2_of[g2] = rstd[:, GT : 2 * GT]
-            for col, sq_dev, factor in parts:
-                nc.gpsimd.tensor_scalar(
-                    out=var_eps[:, col : col + GT], in0=sq_dev, scalar1=factor, scalar2=EPS, op0=ALU.mult, op1=ALU.add
-                )
-            cols = slice(parts[0][0], parts[-1][0] + GT)
-            nc.gpsimd.tensor_tensor(
-                out=rstd[:, cols], in0=var_eps[:, cols], in1=minus_half[:, 0 : len(parts) * GT], op=ALU.pow
+        def scales1(g):
+            nc.gpsimd.tensor_scalar(
+                out=var_eps1[:, tiles_of(g)], in0=sq_dev1[:, tiles_of(g)], scalar1=1.0 / D, scalar2=EPS,
+                op0=ALU.mult, op1=ALU.add,
             )
-            if exists(g1):
-                nc.gpsimd.tensor_tensor(
-                    out=neg_mean_rstd1[:, tiles_of(g1)], in0=neg_mean1[:, tiles_of(g1)], in1=rstd1_of[g1], op=ALU.mult
-                )
+            nc.gpsimd.tensor_tensor(
+                out=rstd1[:, tiles_of(g)], in0=var_eps1[:, tiles_of(g)], in1=minus_half[:], op=ALU.pow
+            )
+            nc.gpsimd.tensor_tensor(
+                out=neg_mean_rstd1[:, tiles_of(g)], in0=neg_mean1[:, tiles_of(g)], in1=rstd1[:, tiles_of(g)],
+                op=ALU.mult,
+            )
+
+        def scales2(g):
+            nc.gpsimd.tensor_scalar(
+                out=var_eps2[:, tiles_of(g)], in0=sq_dev2[:, tiles_of(g)], scalar1=1.0 / D**3, scalar2=EPS,
+                op0=ALU.mult, op1=ALU.add,
+            )
+            nc.gpsimd.tensor_tensor(
+                out=rstd2[:, tiles_of(g)], in0=var_eps2[:, tiles_of(g)], in1=minus_half[:], op=ALU.pow
+            )
 
         def xhat_on_scalar(g):
             xhat = two.tile([P, GT, D], F32, name="xhat", tag="xhat")
@@ -225,7 +224,7 @@ def tile_mnelayer_pa_t_kernel(
                 i = g * GT + t
                 nc.scalar.activation(
                     out=xhat[:, t, :], in_=x_all[:, i, :], func=ACT.Identity,
-                    scale=rstd1_of[g][:, t : t + 1], bias=neg_mean_rstd1[:, i : i + 1],
+                    scale=rstd1[:, i : i + 1], bias=neg_mean_rstd1[:, i : i + 1],
                 )
 
         def transpose_words(rows, h):
@@ -302,12 +301,15 @@ def tile_mnelayer_pa_t_kernel(
             s["grouped"], s["regroup_to"], s["regroup_from"] = regrouped_views(s["xn_planes"][:])
             nc.scalar.copy(out=s["regroup_to"][:, 0:SCALAR_RUNS], in_=s["regroup_from"][:, 0:SCALAR_RUNS])
 
-        def quantise_xn(g):
+        def regroup_on_vector_of(g):
             s = of(g)
             if g in ON_VECTOR:
                 s["grouped"] = regroup_on_vector(s["xn_planes"][:])
             elif SCALAR_RUNS < D // 4:
                 nc.vector.tensor_copy(out=s["regroup_to"][:, SCALAR_RUNS:], in_=s["regroup_from"][:, SCALAR_RUNS:])
+
+        def quantise_xn(g):
+            s = of(g)
             xn_codes = two.tile([P, D], U32, name="xn_codes", tag="xn_codes", align_bytes=64)
             xn_scales = two.tile([P, D], U8, name="xn_scales", tag="xn_scales", align_bytes=64)
             quantise(xn_codes[:], xn_scales[:], s["grouped"][:].rearrange("p n j -> p (n j)"))
@@ -375,12 +377,8 @@ def tile_mnelayer_pa_t_kernel(
             s = of(g)
             res = four.tile([P, GT, D], F32, name="res", tag="res")
             s["res"] = res
-            for h in range(2):
-                pot_half = s["pot"][:, 2 * h : 2 * h + 2, :].rearrange("p t n -> p (t n)")
-                res_half = res[:, 2 * h : 2 * h + 2, :].rearrange("p t n -> p (t n)")
-                nc.vector.scalar_tensor_tensor(
-                    out=res_half, in0=pot_half, scalar=SLOPE, in1=pot_half, op0=ALU.mult, op1=ALU.max
-                )
+            pot, res = s["pot"][:].rearrange("p t n -> p (t n)"), s["res"][:].rearrange("p t n -> p (t n)")
+            nc.vector.scalar_tensor_tensor(out=res, in0=pot, scalar=SLOPE, in1=pot, op0=ALU.mult, op1=ALU.max)
 
         def minus_x(g):
             for t in range(GT):
@@ -433,7 +431,7 @@ def tile_mnelayer_pa_t_kernel(
                 i = g * GT + t
                 nc.vector.scalar_tensor_tensor(
                     out=s["res"][:, t, :], in0=s["res"][:, t, :],
-                    scalar=(rstd2_last[:, t : t + 1] if g == LAST else rstd2_of[g][:, t : t + 1]), in1=gain_shift2[:, 1, :],
+                    scalar=(rstd2_last[:, t : t + 1] if g == LAST else rstd2[:, i : i + 1]), in1=gain_shift2[:, 1, :],
                     op0=ALU.mult, op1=ALU.add,
                 )
                 if g == LAST:
@@ -465,6 +463,7 @@ def tile_mnelayer_pa_t_kernel(
         gain_and_shift1(0, 3)
         transpose_x(2, 0)
         std1_on_scalar(1)
+        regroup_on_vector_of(0)
         quantise_xn(0)
         quantise(syn_codes[:], syn_scales[:], syn_grouped[:].rearrange("p n j -> p (n j)"))
         xhat_on_vector(1)
@@ -498,28 +497,27 @@ def tile_mnelayer_pa_t_kernel(
             else:
                 gate_pass(0, j - 1)
         quantise_x(1)
+        for c in range(CHUNKS):
+            sigmoid(0, c)
+            if c == 0:
+                gate_pass(0, 3)
+            if c in (1, 2):
+                transpose_x(3, c - 1)
+        for t in range(GT):
+            gate_to_rows(0, t)
 
         gain_shift2 = constants.tile([P, 2, D], BF16, name="gain_shift2")
         for a in range(2):
             nc.tensor.matmul(out=gain_shift2[:, a, :], lhsT=ones[:], rhs=ln_rows[:, a, :], start=True, stop=True)
 
         def round_of_pipeline(r):
-            for c in range(CHUNKS):
-                if exists(r + 1):
-                    sigmoid(r + 1, c)
-                if c == 0 and exists(r + 1):
-                    gate_pass(r + 1, CHUNKS - 1)
-                if c in (1, 2) and exists(r + 4):
-                    transpose_x(r + 4, c - 1)
-            if r == -1:
-                for t in range(GT):
-                    gate_to_rows(0, t)
-            if r + 1 == LAST:
-                nc.scalar.activation(out=table_warmer[:, 1:2], in_=eps_col[:, 0:1], func=ACT.Sqrt)
             if exists(r + 4):
                 copy_x(r + 4, 0)
                 copy_x(r + 4, 1)
                 row_sums_on_tensor(r + 4)
+            if exists(r + 2):
+                gate_pass(r + 2, 0)
+                gate_pass(r + 2, 1)
             if exists(r):
                 plus_x(r)
                 squared_deviations2(r)
@@ -528,30 +526,35 @@ def tile_mnelayer_pa_t_kernel(
             if exists(r + 3):
                 quantise_x(r + 3)
             if exists(r + 2) and r >= 0:
-                quantise_xn(r + 2)
-                for t in range(GT):
-                    pre_pass(r + 2, t)
+                regroup_on_vector_of(r + 2)
             if exists(r + 1):
                 leaky_relu(r + 1)
-            if exists(r + 3) or (exists(r) and r < LAST):
-                norm_scales(r + 3, r if r < LAST else GROUPS)
+            if exists(r + 2) and r >= 0:
+                quantise_xn(r + 2)
+            if exists(r + 3):
+                scales1(r + 3)
             if exists(r + 1):
                 minus_x(r + 1)
+            if exists(r) and r < LAST:
+                scales2(r)
             if r == -1:
+                regroup_on_vector_of(1)
                 quantise_xn(1)
                 for t in range(GT):
                     times_gate(0, t)
                     pre_pass(1, t)
             if exists(r + 4):
                 neg_mean1_from_tensor_sums(r + 4)
-                squared_deviations1(r + 4, range(3))
+                squared_deviations1(r + 4, range(2))
+            if exists(r + 2):
+                gate_pass(r + 2, 2)
+                if r >= 0:
+                    for t in range(GT):
+                        pre_pass(r + 2, t)
             if exists(r + 3):
                 xhat_on_scalar(r + 3)
-                if r != 0:
-                    for j in range(SCALAR_BANKS):
-                        transpose_xhat(r + 3, j)
             if exists(r + 4):
-                squared_deviations1(r + 4, range(3, GT))
+                squared_deviations1(r + 4, range(2, GT))
             if exists(r - 1):
                 finish(r - 1)
             for t in range(GT):
@@ -559,20 +562,26 @@ def tile_mnelayer_pa_t_kernel(
                     potential(r + 2, t)
                 if exists(r + 1) and r >= 0:
                     gate_to_rows(r + 1, t)
-            for t in range(GT):
-                if r == 0 and t == 0:
-                    for j in range(SCALAR_BANKS):
-                        transpose_xhat(r + 3, j)
+                if exists(r + 2):
+                    sigmoid(r + 2, t)
+                    if t == 2:
+                        gate_pass(r + 2, 3)
+            if exists(r + 3):
+                for j in range(SCALAR_BANKS):
+                    transpose_xhat(r + 3, j)
+            for j in range(PACK):
                 if exists(r + 3):
-                    gain_and_shift1(r + 3, t)
-                    if t == 0:
+                    gain_and_shift1(r + 3, j)
+                    if j == 0:
                         transpose_xhat(r + 3, 3)
-                if t > 0 and exists(r + 2):
-                    gate_pass(r + 2, t - 1)
+                if j > 0 and j < 3 and exists(r + 5):
+                    transpose_x(r + 5, j - 1)
             if exists(r + 2):
                 store_potential(r + 2)
             if exists(r + 3):
                 regroup_on_scalar(r + 3)
+            if r + 2 == LAST:
+                nc.scalar.activation(out=table_warmer[:, 1:2], in_=eps_col[:, 0:1], func=ACT.Sqrt)
             if exists(r + 1) and r >= 0:
                 for t in range(GT):
                     times_gate(r + 1, t)

@@ -28,7 +28,8 @@ JUNK_BUFS = 8
 SCALAR_BANKS = 3
 VECTOR_BANKS = 4
 ON_VECTOR = (0, 1)
-SUMS_ON_SCALAR = 2
+SUMS_ON_SCALAR = 3
+FIRST_FIN = 2
 SCALAR_RUNS = 96
 
 FLOPS = 2 * 2 * ROWS * D * D
@@ -119,12 +120,12 @@ def tile_mnelayer_pa_t_kernel(
         load_x(2)
         nc.sync.dma_start(out=gate_w_rows[:], in_=gate_W.rearrange("(c m) k -> m c k", m=P))
         load_prev(0)
+        for a, vec in enumerate((ln_gamma, ln_beta)):
+            nc.sync.dma_start(out=ln_rows[0:1, a, :], in_=vec.rearrange("(a n) -> a n", a=1))
         load_x(3)
         load_x(4)
         load_prev(1)
         load_x(5)
-        for a, vec in enumerate((ln_gamma, ln_beta)):
-            nc.sync.dma_start(out=ln_rows[0:1, a, :], in_=vec.rearrange("(a n) -> a n", a=1))
         load_prev(2)
         load_x(6)
         load_prev(3)
@@ -381,10 +382,17 @@ def tile_mnelayer_pa_t_kernel(
             nc.vector.scalar_tensor_tensor(out=res, in0=pot, scalar=SLOPE, in1=pot, op0=ALU.mult, op1=ALU.max)
 
         def minus_x(g):
-            for t in range(GT):
-                engine = nc.vector if g * GT + t < 6 else nc.gpsimd
-                engine.tensor_tensor(
-                    out=of(g)["res"][:, t, :], in0=of(g)["res"][:, t, :], in1=x_all[:, g * GT + t, :], op=ALU.subtract
+            res = of(g)["res"]
+            if g < 2:
+                for t in range(GT):
+                    nc.vector.tensor_tensor(
+                        out=res[:, t, :], in0=res[:, t, :], in1=x_all[:, g * GT + t, :], op=ALU.subtract
+                    )
+                return
+            for t in range(0, GT, 2):
+                i = g * GT + t
+                nc.gpsimd.tensor_tensor(
+                    out=res[:, t : t + 2, :], in0=res[:, t : t + 2, :], in1=x_all[:, i : i + 2, :], op=ALU.subtract
                 )
 
         def times_gate(g, t):
@@ -417,9 +425,9 @@ def tile_mnelayer_pa_t_kernel(
                 bias=eps_col[:, 0:1],
             )
 
-        def finish(g):
+        def finish(g, tiles=range(GT)):
             s = of(g)
-            for t in range(GT):
+            for t in tiles:
                 i = g * GT + t
                 nc.vector.scalar_tensor_tensor(
                     out=s["res"][:, t, :], in0=s["res"][:, t, :], scalar=neg_mean2[:, i : i + 1], in1=gain_shift2[:, 0, :],
@@ -427,7 +435,7 @@ def tile_mnelayer_pa_t_kernel(
                 )
             if g == LAST:
                 nc.vector.reciprocal(out=rstd2_last[:], in_=std2_last[:])
-            for t in range(GT):
+            for t in tiles:
                 i = g * GT + t
                 nc.vector.scalar_tensor_tensor(
                     out=s["res"][:, t, :], in0=s["res"][:, t, :],
@@ -437,7 +445,16 @@ def tile_mnelayer_pa_t_kernel(
                 if g == LAST:
                     nc.sync.dma_start(out=out_dram[:, i, :], in_=s["res"][:, t, :])
             if g < LAST:
-                nc.sync.dma_start(out=out_dram[:, tiles_of(g), :], in_=s["res"][:])
+                i0 = g * GT
+                nc.sync.dma_start(
+                    out=out_dram[:, i0 + tiles[0] : i0 + tiles[-1] + 1, :], in_=s["res"][:, tiles[0] : tiles[-1] + 1, :]
+                )
+
+        gain_shift2 = constants.tile([P, 2, D], BF16, name="gain_shift2")
+
+        def second_norm_constants():
+            for a in range(2):
+                nc.tensor.matmul(out=gain_shift2[:, a, :], lhsT=ones[:], rhs=ln_rows[:, a, :], start=True, stop=True)
 
         syn_grouped = regroup_on_gpsimd(syn_rows[:])
         transpose_x(0, 0)
@@ -452,6 +469,7 @@ def tile_mnelayer_pa_t_kernel(
         xhat_on_vector(0)
         for j in range(SCALAR_BANKS):
             transpose_xhat(0, j)
+        quantise_x(0)
         stats1_on_vector(1)
         gain_and_shift1(0, 0)
         transpose_xhat(0, 3)
@@ -489,7 +507,6 @@ def tile_mnelayer_pa_t_kernel(
         neg_mean1_from_tensor_sums(2)
         transpose_xhat(1, 2)
         squared_deviations1(2)
-        quantise_x(0)
         for j in range(PACK):
             gain_and_shift1(1, j)
             if j == 0:
@@ -505,17 +522,15 @@ def tile_mnelayer_pa_t_kernel(
                 transpose_x(3, c - 1)
         for t in range(GT):
             gate_to_rows(0, t)
-
-        gain_shift2 = constants.tile([P, 2, D], BF16, name="gain_shift2")
-        for a in range(2):
-            nc.tensor.matmul(out=gain_shift2[:, a, :], lhsT=ones[:], rhs=ln_rows[:, a, :], start=True, stop=True)
-
         def round_of_pipeline(r):
             if exists(r + 4):
                 copy_x(r + 4, 0)
                 copy_x(r + 4, 1)
-                row_sums_on_tensor(r + 4)
-            if exists(r + 2):
+                if r + 4 == SUMS_ON_SCALAR:
+                    row_sums_on_scalar(r + 4)
+                else:
+                    row_sums_on_tensor(r + 4)
+            if exists(r + 2) and r >= 0:
                 gate_pass(r + 2, 0)
                 gate_pass(r + 2, 1)
             if exists(r):
@@ -543,8 +558,14 @@ def tile_mnelayer_pa_t_kernel(
                 for t in range(GT):
                     times_gate(0, t)
                     pre_pass(1, t)
+                gate_pass(1, 0)
+                gate_pass(1, 1)
+                second_norm_constants()
             if exists(r + 4):
-                neg_mean1_from_tensor_sums(r + 4)
+                if r + 4 == SUMS_ON_SCALAR:
+                    neg_mean1_from_scalar_sums(r + 4)
+                else:
+                    neg_mean1_from_tensor_sums(r + 4)
                 squared_deviations1(r + 4, range(2))
             if exists(r + 2):
                 gate_pass(r + 2, 2)
@@ -553,19 +574,21 @@ def tile_mnelayer_pa_t_kernel(
                         pre_pass(r + 2, t)
             if exists(r + 3):
                 xhat_on_scalar(r + 3)
-            if exists(r + 4):
-                squared_deviations1(r + 4, range(2, GT))
             if exists(r - 1):
-                finish(r - 1)
+                finish(r - 1, range(FIRST_FIN) if r + 1 <= GROUPS else range(GT))
             for t in range(GT):
                 if exists(r + 2):
                     potential(r + 2, t)
                 if exists(r + 1) and r >= 0:
                     gate_to_rows(r + 1, t)
+                if exists(r - 1) and t == GT - 1 and r + 1 <= GROUPS:
+                    finish(r - 1, range(FIRST_FIN, GT))
                 if exists(r + 2):
                     sigmoid(r + 2, t)
                     if t == 2:
                         gate_pass(r + 2, 3)
+            if exists(r + 4):
+                squared_deviations1(r + 4, range(2, GT))
             if exists(r + 3):
                 for j in range(SCALAR_BANKS):
                     transpose_xhat(r + 3, j)

@@ -25,12 +25,13 @@ DECAY = 0.9
 SLOPE = 0.01
 SUM_COLS = 32
 JUNK_BUFS = 8
-SCALAR_BANKS = 3
-VECTOR_BANKS = 4
+SCALAR_BANKS = 4
+VECTOR_BANKS = 3
 ON_VECTOR = (0, 1)
 SUMS_ON_SCALAR = 3
+XH_FIRST = 3
 FIRST_FIN = 2
-SCALAR_RUNS = 96
+SCALAR_RUNS = 112
 
 FLOPS = 2 * 2 * ROWS * D * D
 
@@ -60,7 +61,7 @@ def tile_mnelayer_pa_t_kernel(
         syn_rows = const.tile([P, PACK, D], BF16, name="syn_rows")
         vec_rows = const.tile([P, P], BF16, name="vec_rows")
         ln_rows = const.tile([P, 2, D], BF16, name="ln_rows")
-        vec_cols = const.tile([P, 3 * CHUNKS], F32, name="vec_cols")
+        vec_cols = const.tile([P, 5 * CHUNKS], F32, name="vec_cols")
         minus_half = const.tile([P, GT], F32, name="minus_half")
         eps_col = const.tile([P, 1], F32, name="eps_col")
         ones = const.tile([P, P], BF16, name="ones")
@@ -88,6 +89,7 @@ def tile_mnelayer_pa_t_kernel(
         std1 = const.tile([P, len(ON_VECTOR) * GT], F32, name="std1")
         std2_last = const.tile([P, GT], F32, name="std2_last")
         rstd2_last = const.tile([P, GT], F32, name="rstd2_last")
+        neg_mean_rstd2 = const.tile([P, GT], F32, name="neg_mean_rstd2")
         table_warmer = const.tile([P, 2], F32, name="table_warmer")
 
         def tiles_of(g):
@@ -113,13 +115,13 @@ def tile_mnelayer_pa_t_kernel(
 
         nc.sync.dma_start(out=x_all[:, 0:2, :], in_=x_dram[:, 0:2, :])
         nc.sync.dma_start(out=x_all[:, 2:4, :], in_=x_dram[:, 2:4, :])
-        for a, vec in enumerate((pre_gamma, pre_beta, gate_b)):
+        for a, vec in enumerate((pre_gamma, pre_beta, gate_b, ln_gamma, ln_beta)):
             nc.sync.dma_start(out=vec_rows[a * CHUNKS : (a + 1) * CHUNKS, :], in_=vec.rearrange("(j p) -> j p", p=P))
         load_x(1)
-        nc.sync.dma_start(out=syn_rows[:], in_=syn_weights.rearrange("(j p) n -> p j n", p=P))
         load_x(2)
         nc.sync.dma_start(out=gate_w_rows[:], in_=gate_W.rearrange("(c m) k -> m c k", m=P))
         load_prev(0)
+        nc.sync.dma_start(out=syn_rows[:], in_=syn_weights.rearrange("(j p) n -> p j n", p=P))
         for a, vec in enumerate((ln_gamma, ln_beta)):
             nc.sync.dma_start(out=ln_rows[0:1, a, :], in_=vec.rearrange("(a n) -> a n", a=1))
         load_x(3)
@@ -450,6 +452,35 @@ def tile_mnelayer_pa_t_kernel(
                     out=out_dram[:, i0 + tiles[0] : i0 + tiles[-1] + 1, :], in_=s["res"][:, tiles[0] : tiles[-1] + 1, :]
                 )
 
+        def finish_on_scalar(g, tiles):
+            s = of(g)
+            res, n = s["res"], len(tiles) * P
+            for t in tiles:
+                i = g * GT + t
+                nc.scalar.activation(
+                    out=res[:, t, :], in_=res[:, t, :], func=ACT.Identity,
+                    scale=rstd2[:, i : i + 1], bias=neg_mean_rstd2[:, t : t + 1],
+                )
+            out_t = two.tile([P, CHUNKS, D], F32, name="out_t", tag="gate_t")
+            banks = []
+            for c in range(CHUNKS):
+                bank = for_scalar.tile([P, D], F32, name="res_bank", tag="bank")
+                for k, t in enumerate(tiles):
+                    nc.tensor.transpose(bank[:, k * P : (k + 1) * P], res[:, t, c * P : (c + 1) * P], ident[:])
+                banks.append(bank)
+            for c in range(CHUNKS):
+                nc.scalar.activation(
+                    out=out_t[:, c, 0:n], in_=banks[c][:, 0:n], func=ACT.Identity,
+                    scale=vec_cols[:, 3 * CHUNKS + c : 3 * CHUNKS + c + 1],
+                    bias=vec_cols[:, 4 * CHUNKS + c : 4 * CHUNKS + c + 1],
+                )
+            for k, t in enumerate(tiles):
+                bank = for_scalar.tile([P, D], F32, name="out_bank", tag="bank")
+                for c in range(CHUNKS):
+                    nc.tensor.transpose(bank[:, c * P : (c + 1) * P], out_t[:, c, k * P : (k + 1) * P], ident[:])
+                nc.scalar.copy(out=res[:, t, :], in_=bank[:])
+                nc.sync.dma_start(out=out_dram[:, g * GT + t, :], in_=res[:, t, :])
+
         gain_shift2 = constants.tile([P, 2, D], BF16, name="gain_shift2")
 
         def second_norm_constants():
@@ -465,74 +496,71 @@ def tile_mnelayer_pa_t_kernel(
         std1_on_scalar(0)
         copy_x(0, 0)
         copy_x(0, 1)
-        nc.scalar.copy(out=vec_cols[:], in_=vec_bank[:, 0 : 3 * CHUNKS])
+        nc.scalar.copy(out=vec_cols[:], in_=vec_bank[:, 0 : 5 * CHUNKS])
         xhat_on_vector(0)
-        for j in range(SCALAR_BANKS):
+        for j in range(PACK):
             transpose_xhat(0, j)
         quantise_x(0)
         stats1_on_vector(1)
-        gain_and_shift1(0, 0)
-        transpose_xhat(0, 3)
-        gain_and_shift1(0, 1)
         gate_w_t = four.tile([P, PACK * D], BF16, name="gate_w_t", tag="x_t", align_bytes=64)
+        gain_and_shift1(0, 0)
         gate_w_bank0 = transpose_words(gate_w_rows[:], 0)
-        gain_and_shift1(0, 2)
+        gain_and_shift1(0, 1)
         gate_w_bank1 = transpose_words(gate_w_rows[:], 1)
-        gain_and_shift1(0, 3)
+        gain_and_shift1(0, 2)
         transpose_x(2, 0)
+        gain_and_shift1(0, 3)
+        transpose_x(2, 1)
         std1_on_scalar(1)
         regroup_on_vector_of(0)
         quantise_xn(0)
         quantise(syn_codes[:], syn_scales[:], syn_grouped[:].rearrange("p n j -> p (n j)"))
         xhat_on_vector(1)
         copy_words(gate_w_bank0, gate_w_t, 0)
-        transpose_x(2, 1)
         copy_words(gate_w_bank1, gate_w_t, 1)
         nc.scalar.activation(out=table_warmer[:, 1:2], in_=eps_col[:, 0:1], func=ACT.Sigmoid)
         transpose_x(1, 0)
-        for t in range(GT):
+        transpose_x(1, 1)
+        second_norm_constants()
+        for t in range(VECTOR_BANKS):
             pre_pass(0, t)
         copy_x(2, 0)
-        transpose_x(1, 1)
         copy_x(2, 1)
         row_sums_on_tensor(2)
+        quantise(gate_codes[:], gate_scales[:], gate_w_t[:])
+        potential(0, 0)
+        pre_pass(0, 3)
         copy_x(1, 0)
         transpose_xhat(1, 0)
         copy_x(1, 1)
         transpose_xhat(1, 1)
-        quantise(gate_codes[:], gate_scales[:], gate_w_t[:])
-        for t in range(GT):
+        transpose_xhat(1, 2)
+        for t in range(1, GT):
+            if t == GT - 1:
+                quantise_x(1)
             potential(0, t)
         store_potential(0)
         neg_mean1_from_tensor_sums(2)
-        transpose_xhat(1, 2)
+        transpose_xhat(1, 3)
         squared_deviations1(2)
         for j in range(PACK):
             gain_and_shift1(1, j)
-            if j == 0:
-                transpose_xhat(1, 3)
-            else:
-                gate_pass(0, j - 1)
-        quantise_x(1)
+            gate_pass(0, j)
         for c in range(CHUNKS):
             sigmoid(0, c)
-            if c == 0:
-                gate_pass(0, 3)
-            if c in (1, 2):
-                transpose_x(3, c - 1)
-        for t in range(GT):
+            if c < 2:
+                transpose_x(3, c)
+        for t in range(VECTOR_BANKS):
             gate_to_rows(0, t)
+
         def round_of_pipeline(r):
             if exists(r + 4):
                 copy_x(r + 4, 0)
                 copy_x(r + 4, 1)
-                if r + 4 == SUMS_ON_SCALAR:
-                    row_sums_on_scalar(r + 4)
-                else:
-                    row_sums_on_tensor(r + 4)
+                row_sums_on_tensor(r + 4)
             if exists(r + 2) and r >= 0:
-                gate_pass(r + 2, 0)
-                gate_pass(r + 2, 1)
+                for c in range(3):
+                    gate_pass(r + 2, c)
             if exists(r):
                 plus_x(r)
                 squared_deviations2(r)
@@ -552,62 +580,71 @@ def tile_mnelayer_pa_t_kernel(
                 minus_x(r + 1)
             if exists(r) and r < LAST:
                 scales2(r)
+                if r == LAST - 1:
+                    nc.gpsimd.tensor_tensor(
+                        out=neg_mean_rstd2[:], in0=neg_mean2[:, tiles_of(r)], in1=rstd2[:, tiles_of(r)], op=ALU.mult
+                    )
             if r == -1:
                 regroup_on_vector_of(1)
                 quantise_xn(1)
-                for t in range(GT):
+                times_gate(0, 0)
+                gate_to_rows(0, 3)
+                for t in range(1, GT):
                     times_gate(0, t)
-                    pre_pass(1, t)
+                    pre_pass(1, t - 1)
                 gate_pass(1, 0)
-                gate_pass(1, 1)
-                second_norm_constants()
+            if r == -1:
+                xhat_on_scalar(2)
             if exists(r + 4):
-                if r + 4 == SUMS_ON_SCALAR:
-                    neg_mean1_from_scalar_sums(r + 4)
-                else:
-                    neg_mean1_from_tensor_sums(r + 4)
+                neg_mean1_from_tensor_sums(r + 4)
                 squared_deviations1(r + 4, range(2))
-            if exists(r + 2):
-                gate_pass(r + 2, 2)
-                if r >= 0:
-                    for t in range(GT):
-                        pre_pass(r + 2, t)
-            if exists(r + 3):
+            if exists(r + 2) and r >= 0:
+                for t in range(VECTOR_BANKS):
+                    pre_pass(r + 2, t)
+                gate_pass(r + 2, 3)
+            if exists(r + 3) and r >= 0:
                 xhat_on_scalar(r + 3)
             if exists(r - 1):
                 finish(r - 1, range(FIRST_FIN) if r + 1 <= GROUPS else range(GT))
-            for t in range(GT):
-                if exists(r + 2):
+            if exists(r + 2):
+                potential(r + 2, 0)
+                pre_pass(r + 2, VECTOR_BANKS)
+                if r == -1:
+                    for c in range(1, CHUNKS):
+                        gate_pass(1, c)
+                for t in range(1, GT):
                     potential(r + 2, t)
-                if exists(r + 1) and r >= 0:
+                store_potential(r + 2)
+                for c in range(CHUNKS):
+                    sigmoid(r + 2, c)
+            for t in range(GT):
+                if exists(r + 1) and r >= 0 and t < GT - 1:
                     gate_to_rows(r + 1, t)
-                if exists(r - 1) and t == GT - 1 and r + 1 <= GROUPS:
-                    finish(r - 1, range(FIRST_FIN, GT))
-                if exists(r + 2):
-                    sigmoid(r + 2, t)
-                    if t == 2:
-                        gate_pass(r + 2, 3)
+                if exists(r + 3) and t < XH_FIRST:
+                    transpose_xhat(r + 3, t)
+            if r == LAST:
+                finish_on_scalar(r - 1, range(FIRST_FIN, GT))
+            elif exists(r - 1) and r < LAST:
+                finish(r - 1, range(FIRST_FIN, GT))
             if exists(r + 4):
                 squared_deviations1(r + 4, range(2, GT))
+            if exists(r + 1) and r >= 0:
+                times_gate(r + 1, 0)
+                gate_to_rows(r + 1, GT - 1)
+                for t in range(1, GT):
+                    times_gate(r + 1, t)
             if exists(r + 3):
-                for j in range(SCALAR_BANKS):
+                for j in range(XH_FIRST, PACK):
                     transpose_xhat(r + 3, j)
             for j in range(PACK):
                 if exists(r + 3):
                     gain_and_shift1(r + 3, j)
-                    if j == 0:
-                        transpose_xhat(r + 3, 3)
-                if j > 0 and j < 3 and exists(r + 5):
-                    transpose_x(r + 5, j - 1)
-            if exists(r + 2):
-                store_potential(r + 2)
+                if j < 2 and exists(r + 5):
+                    transpose_x(r + 5, j)
             if exists(r + 3):
                 regroup_on_scalar(r + 3)
             if r + 2 == LAST:
                 nc.scalar.activation(out=table_warmer[:, 1:2], in_=eps_col[:, 0:1], func=ACT.Sqrt)
-            if exists(r + 1) and r >= 0:
-                for t in range(GT):
-                    times_gate(r + 1, t)
 
         for r in range(-1, GROUPS + 1):
             round_of_pipeline(r)

@@ -30,6 +30,8 @@ VECTOR_BANKS = 3
 ON_VECTOR = (0, 1)
 SUMS_ON_SCALAR = 3
 XH_FIRST = 3
+ENDS_ON_SCALAR = (4, 5, 6)
+LAST_MINUS_X = True
 FIRST_FIN = 2
 SCALAR_RUNS = 112
 
@@ -89,7 +91,7 @@ def tile_mnelayer_pa_t_kernel(
         std1 = const.tile([P, len(ON_VECTOR) * GT], F32, name="std1")
         std2_last = const.tile([P, GT], F32, name="std2_last")
         rstd2_last = const.tile([P, GT], F32, name="rstd2_last")
-        neg_mean_rstd2 = const.tile([P, GT], F32, name="neg_mean_rstd2")
+        neg_mean_rstd2 = const.tile([P, TILES], F32, name="neg_mean_rstd2")
         table_warmer = const.tile([P, 2], F32, name="table_warmer")
 
         def tiles_of(g):
@@ -98,14 +100,16 @@ def tile_mnelayer_pa_t_kernel(
         def exists(g):
             return 0 <= g < GROUPS
 
-        nc.gpsimd.memset(ln_rows[:], 0.0)
         nc.vector.memset(vec_rows[:], 0.0)
         nc.vector.memset(minus_half[:], -0.5)
         nc.vector.memset(eps_col[:], EPS)
         nc.vector.memset(ones[:], 1.0)
+        for a, vec in enumerate((pre_gamma, pre_beta, gate_b, ln_gamma, ln_beta)):
+            nc.scalar.dma_start(out=vec_rows[a * CHUNKS : (a + 1) * CHUNKS, :], in_=vec.rearrange("(j p) -> j p", p=P))
         nc.scalar.activation(out=table_warmer[:, 0:1], in_=eps_col[:, 0:1], func=ACT.Sqrt)
         make_identity(nc, ident[:])
         make_identity(nc, ident_bf[:])
+        nc.gpsimd.memset(ln_rows[:], 0.0)
 
         def load_x(g):
             nc.sync.dma_start(out=x_all[:, tiles_of(g), :], in_=x_dram[:, tiles_of(g), :])
@@ -115,13 +119,11 @@ def tile_mnelayer_pa_t_kernel(
 
         nc.sync.dma_start(out=x_all[:, 0:2, :], in_=x_dram[:, 0:2, :])
         nc.sync.dma_start(out=x_all[:, 2:4, :], in_=x_dram[:, 2:4, :])
-        for a, vec in enumerate((pre_gamma, pre_beta, gate_b, ln_gamma, ln_beta)):
-            nc.sync.dma_start(out=vec_rows[a * CHUNKS : (a + 1) * CHUNKS, :], in_=vec.rearrange("(j p) -> j p", p=P))
         load_x(1)
         load_x(2)
         nc.sync.dma_start(out=gate_w_rows[:], in_=gate_W.rearrange("(c m) k -> m c k", m=P))
-        load_prev(0)
         nc.sync.dma_start(out=syn_rows[:], in_=syn_weights.rearrange("(j p) n -> p j n", p=P))
+        load_prev(0)
         for a, vec in enumerate((ln_gamma, ln_beta)):
             nc.sync.dma_start(out=ln_rows[0:1, a, :], in_=vec.rearrange("(a n) -> a n", a=1))
         load_x(3)
@@ -393,8 +395,9 @@ def tile_mnelayer_pa_t_kernel(
                 return
             for t in range(0, GT, 2):
                 i = g * GT + t
+                n = 1 if g == LAST and t == 2 and LAST_MINUS_X else 2
                 nc.gpsimd.tensor_tensor(
-                    out=res[:, t : t + 2, :], in0=res[:, t : t + 2, :], in1=x_all[:, i : i + 2, :], op=ALU.subtract
+                    out=res[:, t : t + n, :], in0=res[:, t : t + n, :], in1=x_all[:, i : i + n, :], op=ALU.subtract
                 )
 
         def times_gate(g, t):
@@ -459,7 +462,7 @@ def tile_mnelayer_pa_t_kernel(
                 i = g * GT + t
                 nc.scalar.activation(
                     out=res[:, t, :], in_=res[:, t, :], func=ACT.Identity,
-                    scale=rstd2[:, i : i + 1], bias=neg_mean_rstd2[:, t : t + 1],
+                    scale=rstd2[:, i : i + 1], bias=neg_mean_rstd2[:, i : i + 1],
                 )
             out_t = two.tile([P, CHUNKS, D], F32, name="out_t", tag="gate_t")
             banks = []
@@ -580,9 +583,9 @@ def tile_mnelayer_pa_t_kernel(
                 minus_x(r + 1)
             if exists(r) and r < LAST:
                 scales2(r)
-                if r == LAST - 1:
+                if r in ENDS_ON_SCALAR:
                     nc.gpsimd.tensor_tensor(
-                        out=neg_mean_rstd2[:], in0=neg_mean2[:, tiles_of(r)], in1=rstd2[:, tiles_of(r)], op=ALU.mult
+                        out=neg_mean_rstd2[:, tiles_of(r)], in0=neg_mean2[:, tiles_of(r)], in1=rstd2[:, tiles_of(r)], op=ALU.mult
                     )
             if r == -1:
                 regroup_on_vector_of(1)
@@ -622,10 +625,12 @@ def tile_mnelayer_pa_t_kernel(
                     gate_to_rows(r + 1, t)
                 if exists(r + 3) and t < XH_FIRST:
                     transpose_xhat(r + 3, t)
-            if r == LAST:
-                finish_on_scalar(r - 1, range(FIRST_FIN, GT))
-            elif exists(r - 1) and r < LAST:
+            if exists(r - 1) and r < LAST and r - 1 not in ENDS_ON_SCALAR:
                 finish(r - 1, range(FIRST_FIN, GT))
+            if r + 1 == LAST and LAST_MINUS_X:
+                nc.vector.tensor_tensor(
+                    out=of(LAST)["res"][:, 3, :], in0=of(LAST)["res"][:, 3, :], in1=x_all[:, TILES - 1, :], op=ALU.subtract
+                )
             if exists(r + 4):
                 squared_deviations1(r + 4, range(2, GT))
             if exists(r + 1) and r >= 0:
@@ -633,6 +638,8 @@ def tile_mnelayer_pa_t_kernel(
                 gate_to_rows(r + 1, GT - 1)
                 for t in range(1, GT):
                     times_gate(r + 1, t)
+            if r - 1 in ENDS_ON_SCALAR:
+                finish_on_scalar(r - 1, range(FIRST_FIN, GT))
             if exists(r + 3):
                 for j in range(XH_FIRST, PACK):
                     transpose_xhat(r + 3, j)

@@ -62,8 +62,10 @@ def tile_mnelayer_pa_t_kernel(
         gate_w_rows = const.tile([P, CHUNKS, D], BF16, name="gate_w_rows")
         syn_rows = const.tile([P, PACK, D], BF16, name="syn_rows")
         vec_rows = const.tile([P, P], BF16, name="vec_rows")
+        vec2_rows = const.tile([P, P], BF16, name="vec2_rows")
         ln_rows = const.tile([P, 2, D], BF16, name="ln_rows")
-        vec_cols = const.tile([P, 5 * CHUNKS], F32, name="vec_cols")
+        vec_cols = const.tile([P, 2 * CHUNKS], F32, name="vec_cols")
+        vec2_cols = const.tile([P, 3 * CHUNKS], F32, name="vec2_cols")
         minus_half = const.tile([P, GT], F32, name="minus_half")
         eps_col = const.tile([P, 1], F32, name="eps_col")
         ones = const.tile([P, P], BF16, name="ones")
@@ -101,10 +103,11 @@ def tile_mnelayer_pa_t_kernel(
             return 0 <= g < GROUPS
 
         nc.vector.memset(vec_rows[:], 0.0)
+        nc.vector.memset(vec2_rows[:], 0.0)
         nc.vector.memset(minus_half[:], -0.5)
         nc.vector.memset(eps_col[:], EPS)
         nc.vector.memset(ones[:], 1.0)
-        for a, vec in enumerate((pre_gamma, pre_beta, gate_b, ln_gamma, ln_beta)):
+        for a, vec in enumerate((pre_gamma, pre_beta)):
             nc.scalar.dma_start(out=vec_rows[a * CHUNKS : (a + 1) * CHUNKS, :], in_=vec.rearrange("(j p) -> j p", p=P))
         nc.scalar.activation(out=table_warmer[:, 0:1], in_=eps_col[:, 0:1], func=ACT.Sqrt)
         make_identity(nc, ident[:])
@@ -119,11 +122,13 @@ def tile_mnelayer_pa_t_kernel(
 
         nc.sync.dma_start(out=x_all[:, 0:2, :], in_=x_dram[:, 0:2, :])
         nc.sync.dma_start(out=x_all[:, 2:4, :], in_=x_dram[:, 2:4, :])
+        nc.sync.dma_start(out=gate_w_rows[:], in_=gate_W.rearrange("(c m) k -> m c k", m=P))
         load_x(1)
         load_x(2)
-        nc.sync.dma_start(out=gate_w_rows[:], in_=gate_W.rearrange("(c m) k -> m c k", m=P))
         nc.sync.dma_start(out=syn_rows[:], in_=syn_weights.rearrange("(j p) n -> p j n", p=P))
         load_prev(0)
+        for a, vec in enumerate((gate_b, ln_gamma, ln_beta)):
+            nc.sync.dma_start(out=vec2_rows[a * CHUNKS : (a + 1) * CHUNKS, :], in_=vec.rearrange("(j p) -> j p", p=P))
         for a, vec in enumerate((ln_gamma, ln_beta)):
             nc.sync.dma_start(out=ln_rows[0:1, a, :], in_=vec.rearrange("(a n) -> a n", a=1))
         load_x(3)
@@ -355,7 +360,7 @@ def tile_mnelayer_pa_t_kernel(
                 s["gate_t"] = gate_t
             nc.scalar.activation(
                 out=s["gate_t"][:, c, :], in_=s["gate_t_bank%d" % c][:], func=ACT.Sigmoid,
-                bias=vec_cols[:, 2 * CHUNKS + c : 2 * CHUNKS + c + 1],
+                bias=vec2_cols[:, c : c + 1],
             )
 
         def gate_to_rows(g, t):
@@ -474,8 +479,8 @@ def tile_mnelayer_pa_t_kernel(
             for c in range(CHUNKS):
                 nc.scalar.activation(
                     out=out_t[:, c, 0:n], in_=banks[c][:, 0:n], func=ACT.Identity,
-                    scale=vec_cols[:, 3 * CHUNKS + c : 3 * CHUNKS + c + 1],
-                    bias=vec_cols[:, 4 * CHUNKS + c : 4 * CHUNKS + c + 1],
+                    scale=vec2_cols[:, CHUNKS + c : CHUNKS + c + 1],
+                    bias=vec2_cols[:, 2 * CHUNKS + c : 2 * CHUNKS + c + 1],
                 )
             for k, t in enumerate(tiles):
                 bank = for_scalar.tile([P, D], F32, name="out_bank", tag="bank")
@@ -493,59 +498,57 @@ def tile_mnelayer_pa_t_kernel(
         syn_grouped = regroup_on_gpsimd(syn_rows[:])
         transpose_x(0, 0)
         transpose_x(0, 1)
-        vec_bank = for_scalar.tile([P, P], BF16, name="vec_bank", tag="bank")
-        nc.tensor.transpose(vec_bank[:], vec_rows[:], ident_bf[:])
+        gate_w_t = four.tile([P, PACK * D], BF16, name="gate_w_t", tag="x_t", align_bytes=64)
+        gate_w_bank0 = transpose_words(gate_w_rows[:], 0)
+        gate_w_bank1 = transpose_words(gate_w_rows[:], 1)
         stats1_on_vector(0)
-        std1_on_scalar(0)
         copy_x(0, 0)
         copy_x(0, 1)
-        nc.scalar.copy(out=vec_cols[:], in_=vec_bank[:, 0 : 5 * CHUNKS])
+        copy_words(gate_w_bank0, gate_w_t, 0)
+        std1_on_scalar(0)
+        copy_words(gate_w_bank1, gate_w_t, 1)
+        vec_bank = for_scalar.tile([P, P], BF16, name="vec_bank", tag="bank")
+        nc.tensor.transpose(vec_bank[:], vec_rows[:], ident_bf[:])
+        transpose_x(1, 0)
+        transpose_x(1, 1)
+        nc.scalar.copy(out=vec_cols[:], in_=vec_bank[:, 0 : 2 * CHUNKS])
+        copy_x(1, 0)
+        copy_x(1, 1)
         xhat_on_vector(0)
         for j in range(PACK):
             transpose_xhat(0, j)
         quantise_x(0)
         stats1_on_vector(1)
-        gate_w_t = four.tile([P, PACK * D], BF16, name="gate_w_t", tag="x_t", align_bytes=64)
-        gain_and_shift1(0, 0)
-        gate_w_bank0 = transpose_words(gate_w_rows[:], 0)
-        gain_and_shift1(0, 1)
-        gate_w_bank1 = transpose_words(gate_w_rows[:], 1)
-        gain_and_shift1(0, 2)
-        transpose_x(2, 0)
-        gain_and_shift1(0, 3)
-        transpose_x(2, 1)
-        std1_on_scalar(1)
+        for j in range(PACK):
+            gain_and_shift1(0, j)
+            if j < 2:
+                transpose_x(2, j)
+        vec2_bank = for_scalar.tile([P, P], BF16, name="vec2_bank", tag="bank")
+        nc.tensor.transpose(vec2_bank[:], vec2_rows[:], ident_bf[:])
         regroup_on_vector_of(0)
         quantise_xn(0)
         quantise(syn_codes[:], syn_scales[:], syn_grouped[:].rearrange("p n j -> p (n j)"))
-        xhat_on_vector(1)
-        copy_words(gate_w_bank0, gate_w_t, 0)
-        copy_words(gate_w_bank1, gate_w_t, 1)
-        nc.scalar.activation(out=table_warmer[:, 1:2], in_=eps_col[:, 0:1], func=ACT.Sigmoid)
-        transpose_x(1, 0)
-        transpose_x(1, 1)
-        second_norm_constants()
+        quantise(gate_codes[:], gate_scales[:], gate_w_t[:])
         for t in range(VECTOR_BANKS):
             pre_pass(0, t)
         copy_x(2, 0)
         copy_x(2, 1)
-        row_sums_on_tensor(2)
-        quantise(gate_codes[:], gate_scales[:], gate_w_t[:])
+        std1_on_scalar(1)
+        nc.scalar.copy(out=vec2_cols[:], in_=vec2_bank[:, 0 : 3 * CHUNKS])
+        xhat_on_vector(1)
+        nc.scalar.activation(out=table_warmer[:, 1:2], in_=eps_col[:, 0:1], func=ACT.Sigmoid)
+        row_sums_on_scalar(2)
+        neg_mean1_from_scalar_sums(2)
+        squared_deviations1(2)
+        for j in range(PACK):
+            transpose_xhat(1, j)
         potential(0, 0)
         pre_pass(0, 3)
-        copy_x(1, 0)
-        transpose_xhat(1, 0)
-        copy_x(1, 1)
-        transpose_xhat(1, 1)
-        transpose_xhat(1, 2)
+        quantise_x(1)
         for t in range(1, GT):
-            if t == GT - 1:
-                quantise_x(1)
             potential(0, t)
         store_potential(0)
-        neg_mean1_from_tensor_sums(2)
-        transpose_xhat(1, 3)
-        squared_deviations1(2)
+        second_norm_constants()
         for j in range(PACK):
             gain_and_shift1(1, j)
             gate_pass(0, j)
@@ -561,6 +564,8 @@ def tile_mnelayer_pa_t_kernel(
                 copy_x(r + 4, 0)
                 copy_x(r + 4, 1)
                 row_sums_on_tensor(r + 4)
+                if r == -1:
+                    gate_pass(1, 0)
             if exists(r + 2) and r >= 0:
                 for c in range(3):
                     gate_pass(r + 2, c)
@@ -595,7 +600,8 @@ def tile_mnelayer_pa_t_kernel(
                 for t in range(1, GT):
                     times_gate(0, t)
                     pre_pass(1, t - 1)
-                gate_pass(1, 0)
+                    if t < GT - 1:
+                        gate_pass(1, t)
             if r == -1:
                 xhat_on_scalar(2)
             if exists(r + 4):
@@ -613,8 +619,7 @@ def tile_mnelayer_pa_t_kernel(
                 potential(r + 2, 0)
                 pre_pass(r + 2, VECTOR_BANKS)
                 if r == -1:
-                    for c in range(1, CHUNKS):
-                        gate_pass(1, c)
+                    gate_pass(1, 3)
                 for t in range(1, GT):
                     potential(r + 2, t)
                 store_potential(r + 2)

@@ -30,9 +30,11 @@ VECTOR_BANKS = 3
 ON_VECTOR = (0, 1)
 SUMS_ON_SCALAR = 3
 XH_FIRST = 3
-ENDS_ON_SCALAR = (4, 5, 6)
-LAST_MINUS_X = True
+ENDS_ON_SCALAR = (4,)
+BY_SQRT = 6
 FIRST_FIN = 2
+FIRST_N = 1
+SCALAR_RUNS_FIRST = 64
 SCALAR_RUNS = 112
 
 FLOPS = 2 * 2 * ROWS * D * D
@@ -91,8 +93,7 @@ def tile_mnelayer_pa_t_kernel(
         neg_mean2 = const.tile([P, TILES], F32, name="neg_mean2")
         sq_dev2 = const.tile([P, TILES], F32, name="sq_dev2")
         std1 = const.tile([P, len(ON_VECTOR) * GT], F32, name="std1")
-        std2_last = const.tile([P, GT], F32, name="std2_last")
-        rstd2_last = const.tile([P, GT], F32, name="rstd2_last")
+        std2 = const.tile([P, 2 * GT], F32, name="std2")
         neg_mean_rstd2 = const.tile([P, TILES], F32, name="neg_mean_rstd2")
         table_warmer = const.tile([P, 2], F32, name="table_warmer")
 
@@ -122,8 +123,8 @@ def tile_mnelayer_pa_t_kernel(
 
         nc.sync.dma_start(out=x_all[:, 0:2, :], in_=x_dram[:, 0:2, :])
         nc.sync.dma_start(out=x_all[:, 2:4, :], in_=x_dram[:, 2:4, :])
-        nc.sync.dma_start(out=gate_w_rows[:], in_=gate_W.rearrange("(c m) k -> m c k", m=P))
         load_x(1)
+        nc.sync.dma_start(out=gate_w_rows[:], in_=gate_W.rearrange("(c m) k -> m c k", m=P))
         load_x(2)
         nc.sync.dma_start(out=syn_rows[:], in_=syn_weights.rearrange("(j p) n -> p j n", p=P))
         load_prev(0)
@@ -154,9 +155,12 @@ def tile_mnelayer_pa_t_kernel(
             return junk[:, junk_turn[0], :]
 
         def stats1_on_vector(g):
-            for i in range(g * GT, (g + 1) * GT):
-                nc.vector.bn_stats(out=bn6[:, i, :], in_=x_all[:, i, :])
-                nc.vector.bn_aggr(out=mean_var1[:, i, :], in_=bn6[:, i, :])
+            for t in range(GT + 1):
+                i = g * GT + t
+                if t < GT:
+                    nc.vector.bn_stats(out=bn6[:, i, :], in_=x_all[:, i, :])
+                if t > 0:
+                    nc.vector.bn_aggr(out=mean_var1[:, i - 1, :], in_=bn6[:, i - 1, :])
 
         def std1_on_scalar(g):
             nc.scalar.activation(
@@ -288,6 +292,9 @@ def tile_mnelayer_pa_t_kernel(
                 scale=vec_cols[:, j : j + 1], bias=vec_cols[:, CHUNKS + j : CHUNKS + j + 1],
             )
 
+        def runs(g):
+            return SCALAR_RUNS_FIRST if g < 2 + FIRST_N else SCALAR_RUNS
+
         def regrouped_views(planes):
             grouped = two.tile([P, D, PACK], BF16, name="grouped", tag="grouped", align_bytes=64)
             return (
@@ -309,14 +316,14 @@ def tile_mnelayer_pa_t_kernel(
         def regroup_on_scalar(g):
             s = of(g)
             s["grouped"], s["regroup_to"], s["regroup_from"] = regrouped_views(s["xn_planes"][:])
-            nc.scalar.copy(out=s["regroup_to"][:, 0:SCALAR_RUNS], in_=s["regroup_from"][:, 0:SCALAR_RUNS])
+            nc.scalar.copy(out=s["regroup_to"][:, 0 : runs(g)], in_=s["regroup_from"][:, 0 : runs(g)])
 
         def regroup_on_vector_of(g):
             s = of(g)
             if g in ON_VECTOR:
                 s["grouped"] = regroup_on_vector(s["xn_planes"][:])
-            elif SCALAR_RUNS < D // 4:
-                nc.vector.tensor_copy(out=s["regroup_to"][:, SCALAR_RUNS:], in_=s["regroup_from"][:, SCALAR_RUNS:])
+            elif runs(g) < D // 4:
+                nc.vector.tensor_copy(out=s["regroup_to"][:, runs(g) :], in_=s["regroup_from"][:, runs(g) :])
 
         def quantise_xn(g):
             s = of(g)
@@ -383,27 +390,19 @@ def tile_mnelayer_pa_t_kernel(
         def store_potential(g):
             nc.sync.dma_start(out=pot_dram[:, tiles_of(g), :], in_=of(g)["pot"][:])
 
-        def leaky_relu(g):
+        def leaky_relu(g, tiles=slice(0, GT)):
             s = of(g)
-            res = four.tile([P, GT, D], F32, name="res", tag="res")
-            s["res"] = res
-            pot, res = s["pot"][:].rearrange("p t n -> p (t n)"), s["res"][:].rearrange("p t n -> p (t n)")
-            nc.vector.scalar_tensor_tensor(out=res, in0=pot, scalar=SLOPE, in1=pot, op0=ALU.mult, op1=ALU.max)
+            if "res" not in s:
+                res = four.tile([P, GT, D], F32, name="res", tag="res")
+                s["res"] = res
+            pot = s["pot"][:, tiles, :].rearrange("p t n -> p (t n)")
+            act = s["res"][:, tiles, :].rearrange("p t n -> p (t n)")
+            nc.vector.scalar_tensor_tensor(out=act, in0=pot, scalar=SLOPE, in1=pot, op0=ALU.mult, op1=ALU.max)
 
-        def minus_x(g):
-            res = of(g)["res"]
-            if g < 2:
-                for t in range(GT):
-                    nc.vector.tensor_tensor(
-                        out=res[:, t, :], in0=res[:, t, :], in1=x_all[:, g * GT + t, :], op=ALU.subtract
-                    )
-                return
-            for t in range(0, GT, 2):
-                i = g * GT + t
-                n = 1 if g == LAST and t == 2 and LAST_MINUS_X else 2
-                nc.gpsimd.tensor_tensor(
-                    out=res[:, t : t + n, :], in0=res[:, t : t + n, :], in1=x_all[:, i : i + n, :], op=ALU.subtract
-                )
+        def minus_x(engine, g, first, count):
+            i = g * GT + first
+            res = of(g)["res"][:, first : first + count, :]
+            engine.tensor_tensor(out=res, in0=res, in1=x_all[:, i : i + count, :], op=ALU.subtract)
 
         def times_gate(g, t):
             s = of(g)
@@ -423,19 +422,30 @@ def tile_mnelayer_pa_t_kernel(
         def squared_deviations2(g):
             for t in range(GT):
                 i = g * GT + t
+                if t == GT - 1:
+                    nc.scalar.mul(out=neg_mean2[:, tiles_of(g)], in_=sum2[:, tiles_of(g)], mul=-1.0 / D)
                 nc.scalar.activation(
                     out=junk_out(), in_=of(g)["res"][:, t, :], func=ACT.Square, scale=-float(D), bias=sum2[:, i : i + 1],
                     accum_out=sq_dev2[:, i : i + 1],
                 )
-            nc.scalar.mul(out=neg_mean2[:, tiles_of(g)], in_=sum2[:, tiles_of(g)], mul=-1.0 / D)
 
-        def std2_of_last_group():
+        def sqrt_cols(g):
+            return slice((g - BY_SQRT) * GT, (g - BY_SQRT + 1) * GT)
+
+        def rstd2_by_sqrt_scalar(g):
             nc.scalar.activation(
-                out=std2_last[:, 0:GT], in_=sq_dev2[:, tiles_of(LAST)], func=ACT.Sqrt, scale=1.0 / D**3,
+                out=std2[:, sqrt_cols(g)], in_=sq_dev2[:, tiles_of(g)], func=ACT.Sqrt, scale=1.0 / D**3,
                 bias=eps_col[:, 0:1],
             )
 
-        def finish(g, tiles=range(GT)):
+        def rstd2_by_sqrt_vector(g):
+            nc.vector.reciprocal(out=rstd2[:, tiles_of(g)], in_=std2[:, sqrt_cols(g)])
+
+        def finish(g, tiles):
+            center_and_gain2(g, tiles)
+            scale_and_shift2(g, tiles)
+
+        def center_and_gain2(g, tiles):
             s = of(g)
             for t in tiles:
                 i = g * GT + t
@@ -443,13 +453,13 @@ def tile_mnelayer_pa_t_kernel(
                     out=s["res"][:, t, :], in0=s["res"][:, t, :], scalar=neg_mean2[:, i : i + 1], in1=gain_shift2[:, 0, :],
                     op0=ALU.add, op1=ALU.mult,
                 )
-            if g == LAST:
-                nc.vector.reciprocal(out=rstd2_last[:], in_=std2_last[:])
+
+        def scale_and_shift2(g, tiles):
+            s = of(g)
             for t in tiles:
                 i = g * GT + t
                 nc.vector.scalar_tensor_tensor(
-                    out=s["res"][:, t, :], in0=s["res"][:, t, :],
-                    scalar=(rstd2_last[:, t : t + 1] if g == LAST else rstd2[:, i : i + 1]), in1=gain_shift2[:, 1, :],
+                    out=s["res"][:, t, :], in0=s["res"][:, t, :], scalar=rstd2[:, i : i + 1], in1=gain_shift2[:, 1, :],
                     op0=ALU.mult, op1=ALU.add,
                 )
                 if g == LAST:
@@ -463,6 +473,12 @@ def tile_mnelayer_pa_t_kernel(
         def finish_on_scalar(g, tiles):
             s = of(g)
             res, n = s["res"], len(tiles) * P
+            for t in tiles:
+                i = g * GT + t
+                nc.scalar.activation(
+                    out=neg_mean_rstd2[:, i : i + 1], in_=neg_mean2[:, i : i + 1], func=ACT.Identity,
+                    scale=rstd2[:, i : i + 1],
+                )
             for t in tiles:
                 i = g * GT + t
                 nc.scalar.activation(
@@ -498,22 +514,22 @@ def tile_mnelayer_pa_t_kernel(
         syn_grouped = regroup_on_gpsimd(syn_rows[:])
         transpose_x(0, 0)
         transpose_x(0, 1)
-        gate_w_t = four.tile([P, PACK * D], BF16, name="gate_w_t", tag="x_t", align_bytes=64)
-        gate_w_bank0 = transpose_words(gate_w_rows[:], 0)
-        gate_w_bank1 = transpose_words(gate_w_rows[:], 1)
+        transpose_x(1, 0)
+        transpose_x(1, 1)
         stats1_on_vector(0)
         copy_x(0, 0)
         copy_x(0, 1)
-        copy_words(gate_w_bank0, gate_w_t, 0)
+        copy_x(1, 0)
         std1_on_scalar(0)
-        copy_words(gate_w_bank1, gate_w_t, 1)
+        copy_x(1, 1)
         vec_bank = for_scalar.tile([P, P], BF16, name="vec_bank", tag="bank")
         nc.tensor.transpose(vec_bank[:], vec_rows[:], ident_bf[:])
-        transpose_x(1, 0)
-        transpose_x(1, 1)
+        gate_w_t = four.tile([P, PACK * D], BF16, name="gate_w_t", tag="x_t", align_bytes=64)
+        gate_w_bank0 = transpose_words(gate_w_rows[:], 0)
+        gate_w_bank1 = transpose_words(gate_w_rows[:], 1)
         nc.scalar.copy(out=vec_cols[:], in_=vec_bank[:, 0 : 2 * CHUNKS])
-        copy_x(1, 0)
-        copy_x(1, 1)
+        copy_words(gate_w_bank0, gate_w_t, 0)
+        copy_words(gate_w_bank1, gate_w_t, 1)
         xhat_on_vector(0)
         for j in range(PACK):
             transpose_xhat(0, j)
@@ -572,8 +588,6 @@ def tile_mnelayer_pa_t_kernel(
             if exists(r):
                 plus_x(r)
                 squared_deviations2(r)
-                if r == LAST:
-                    std2_of_last_group()
             if exists(r + 3):
                 quantise_x(r + 3)
             if exists(r + 2) and r >= 0:
@@ -584,14 +598,14 @@ def tile_mnelayer_pa_t_kernel(
                 quantise_xn(r + 2)
             if exists(r + 3):
                 scales1(r + 3)
-            if exists(r + 1):
-                minus_x(r + 1)
-            if exists(r) and r < LAST:
+            for t in range(0, GT, 2):
+                if r + 1 < 2:
+                    minus_x(nc.vector, r + 1, t, 1)
+                    minus_x(nc.vector, r + 1, t + 1, 1)
+                else:
+                    minus_x(nc.gpsimd, r + 1, t, 2)
+            if exists(r):
                 scales2(r)
-                if r in ENDS_ON_SCALAR:
-                    nc.gpsimd.tensor_tensor(
-                        out=neg_mean_rstd2[:, tiles_of(r)], in0=neg_mean2[:, tiles_of(r)], in1=rstd2[:, tiles_of(r)], op=ALU.mult
-                    )
             if r == -1:
                 regroup_on_vector_of(1)
                 quantise_xn(1)
@@ -614,7 +628,7 @@ def tile_mnelayer_pa_t_kernel(
             if exists(r + 3) and r >= 0:
                 xhat_on_scalar(r + 3)
             if exists(r - 1):
-                finish(r - 1, range(FIRST_FIN) if r + 1 <= GROUPS else range(GT))
+                finish(r - 1, range(FIRST_FIN))
             if exists(r + 2):
                 potential(r + 2, 0)
                 pre_pass(r + 2, VECTOR_BANKS)
@@ -630,12 +644,8 @@ def tile_mnelayer_pa_t_kernel(
                     gate_to_rows(r + 1, t)
                 if exists(r + 3) and t < XH_FIRST:
                     transpose_xhat(r + 3, t)
-            if exists(r - 1) and r < LAST and r - 1 not in ENDS_ON_SCALAR:
+            if exists(r - 1) and r - 1 not in ENDS_ON_SCALAR:
                 finish(r - 1, range(FIRST_FIN, GT))
-            if r + 1 == LAST and LAST_MINUS_X:
-                nc.vector.tensor_tensor(
-                    out=of(LAST)["res"][:, 3, :], in0=of(LAST)["res"][:, 3, :], in1=x_all[:, TILES - 1, :], op=ALU.subtract
-                )
             if exists(r + 4):
                 squared_deviations1(r + 4, range(2, GT))
             if exists(r + 1) and r >= 0:
@@ -658,5 +668,32 @@ def tile_mnelayer_pa_t_kernel(
             if r + 2 == LAST:
                 nc.scalar.activation(out=table_warmer[:, 1:2], in_=eps_col[:, 0:1], func=ACT.Sqrt)
 
-        for r in range(-1, GROUPS + 1):
+        for r in range(-1, LAST - 1):
             round_of_pipeline(r)
+
+        plus_x(6)
+        squared_deviations2(6)
+        rstd2_by_sqrt_scalar(6)
+        leaky_relu(7, slice(3, 4))
+        leaky_relu(7, slice(0, 3))
+        minus_x(nc.gpsimd, 7, 0, 2)
+        minus_x(nc.gpsimd, 7, 2, 1)
+        minus_x(nc.vector, 7, 3, 1)
+        rstd2_by_sqrt_vector(6)
+        finish(5, (0, 1))
+        finish(6, (0,))
+        for t in range(3):
+            gate_to_rows(7, t)
+        finish_on_scalar(5, (2, 3))
+        times_gate(7, 0)
+        gate_to_rows(7, 3)
+        for t in range(1, GT):
+            times_gate(7, t)
+        finish_on_scalar(6, (2, 3))
+        plus_x(7)
+        finish(6, (1,))
+        squared_deviations2(7)
+        rstd2_by_sqrt_scalar(7)
+        center_and_gain2(7, (0, 1, 2, 3))
+        rstd2_by_sqrt_vector(7)
+        scale_and_shift2(7, (0, 1, 2, 3))

@@ -29,7 +29,7 @@ SCALAR_BANKS = 4
 VECTOR_BANKS = 3
 ON_VECTOR = (0, 1)
 SUMS_ON_SCALAR = 3
-XH_FIRST = 3
+XH_FIRST = 2
 ENDS_ON_SCALAR = (4,)
 BY_SQRT = 6
 FIRST_FIN = 2
@@ -470,27 +470,27 @@ def tile_mnelayer_pa_t_kernel(
                     out=out_dram[:, i0 + tiles[0] : i0 + tiles[-1] + 1, :], in_=s["res"][:, tiles[0] : tiles[-1] + 1, :]
                 )
 
-        def finish_on_scalar(g, tiles):
-            s = of(g)
-            res, n = s["res"], len(tiles) * P
-            for t in tiles:
+        def finish_on_scalar(row_tiles):
+            n = len(row_tiles) * P
+            for g, t in row_tiles:
                 i = g * GT + t
                 nc.scalar.activation(
                     out=neg_mean_rstd2[:, i : i + 1], in_=neg_mean2[:, i : i + 1], func=ACT.Identity,
                     scale=rstd2[:, i : i + 1],
                 )
-            for t in tiles:
-                i = g * GT + t
                 nc.scalar.activation(
-                    out=res[:, t, :], in_=res[:, t, :], func=ACT.Identity,
+                    out=of(g)["res"][:, t, :], in_=of(g)["res"][:, t, :], func=ACT.Identity,
                     scale=rstd2[:, i : i + 1], bias=neg_mean_rstd2[:, i : i + 1],
                 )
             out_t = two.tile([P, CHUNKS, D], F32, name="out_t", tag="gate_t")
+            of(row_tiles[0][0])["out_t"] = out_t
             banks = []
             for c in range(CHUNKS):
                 bank = for_scalar.tile([P, D], F32, name="res_bank", tag="bank")
-                for k, t in enumerate(tiles):
-                    nc.tensor.transpose(bank[:, k * P : (k + 1) * P], res[:, t, c * P : (c + 1) * P], ident[:])
+                for k, (g, t) in enumerate(row_tiles):
+                    nc.tensor.transpose(
+                        bank[:, k * P : (k + 1) * P], of(g)["res"][:, t, c * P : (c + 1) * P], ident[:]
+                    )
                 banks.append(bank)
             for c in range(CHUNKS):
                 nc.scalar.activation(
@@ -498,12 +498,15 @@ def tile_mnelayer_pa_t_kernel(
                     scale=vec2_cols[:, CHUNKS + c : CHUNKS + c + 1],
                     bias=vec2_cols[:, 2 * CHUNKS + c : 2 * CHUNKS + c + 1],
                 )
-            for k, t in enumerate(tiles):
+
+        def output_rows_on_scalar(row_tiles):
+            out_t = of(row_tiles[0][0])["out_t"]
+            for k, (g, t) in enumerate(row_tiles):
                 bank = for_scalar.tile([P, D], F32, name="out_bank", tag="bank")
                 for c in range(CHUNKS):
                     nc.tensor.transpose(bank[:, c * P : (c + 1) * P], out_t[:, c, k * P : (k + 1) * P], ident[:])
-                nc.scalar.copy(out=res[:, t, :], in_=bank[:])
-                nc.sync.dma_start(out=out_dram[:, g * GT + t, :], in_=res[:, t, :])
+                nc.scalar.copy(out=of(g)["res"][:, t, :], in_=bank[:])
+                nc.sync.dma_start(out=out_dram[:, g * GT + t, :], in_=of(g)["res"][:, t, :])
 
         gain_shift2 = constants.tile([P, 2, D], BF16, name="gain_shift2")
 
@@ -639,11 +642,12 @@ def tile_mnelayer_pa_t_kernel(
                 store_potential(r + 2)
                 for c in range(CHUNKS):
                     sigmoid(r + 2, c)
-            for t in range(GT):
-                if exists(r + 1) and r >= 0 and t < GT - 1:
+            if exists(r + 1) and r >= 0:
+                for t in range(GT - 1):
                     gate_to_rows(r + 1, t)
-                if exists(r + 3) and t < XH_FIRST:
-                    transpose_xhat(r + 3, t)
+            if exists(r + 3):
+                for j in range(XH_FIRST):
+                    transpose_xhat(r + 3, j)
             if exists(r - 1) and r - 1 not in ENDS_ON_SCALAR:
                 finish(r - 1, range(FIRST_FIN, GT))
             if exists(r + 4):
@@ -654,7 +658,8 @@ def tile_mnelayer_pa_t_kernel(
                 for t in range(1, GT):
                     times_gate(r + 1, t)
             if r - 1 in ENDS_ON_SCALAR:
-                finish_on_scalar(r - 1, range(FIRST_FIN, GT))
+                finish_on_scalar([(r - 1, t) for t in range(FIRST_FIN, GT)])
+                output_rows_on_scalar([(r - 1, t) for t in range(FIRST_FIN, GT)])
             if exists(r + 3):
                 for j in range(XH_FIRST, PACK):
                     transpose_xhat(r + 3, j)
@@ -684,12 +689,12 @@ def tile_mnelayer_pa_t_kernel(
         finish(6, (0,))
         for t in range(3):
             gate_to_rows(7, t)
-        finish_on_scalar(5, (2, 3))
+        finish_on_scalar([(5, 2), (5, 3), (6, 2), (6, 3)])
         times_gate(7, 0)
         gate_to_rows(7, 3)
+        output_rows_on_scalar([(5, 2), (5, 3), (6, 2), (6, 3)])
         for t in range(1, GT):
             times_gate(7, t)
-        finish_on_scalar(6, (2, 3))
         plus_x(7)
         finish(6, (1,))
         squared_deviations2(7)

@@ -585,6 +585,7 @@ def tile_mnelayer_pa_t_kernel(
                 row_sums_on_tensor(r + 4)
                 if r == -1:
                     gate_pass(1, 0)
+                    gate_pass(1, 1)
             if exists(r + 2) and r >= 0:
                 for c in range(3):
                     gate_pass(r + 2, c)
@@ -617,8 +618,8 @@ def tile_mnelayer_pa_t_kernel(
                 for t in range(1, GT):
                     times_gate(0, t)
                     pre_pass(1, t - 1)
-                    if t < GT - 1:
-                        gate_pass(1, t)
+                    if t == 1:
+                        gate_pass(1, 2)
             if r == -1:
                 xhat_on_scalar(2)
             if exists(r + 4):
@@ -684,21 +685,21 @@ def tile_mnelayer_pa_t_kernel(
         minus_x(nc.gpsimd, 7, 0, 2)
         minus_x(nc.gpsimd, 7, 2, 1)
         minus_x(nc.vector, 7, 3, 1)
-        rstd2_by_sqrt_vector(6)
         finish(5, (0, 1))
+        rstd2_by_sqrt_vector(6)
         finish(6, (0,))
         for t in range(3):
             gate_to_rows(7, t)
-        finish_on_scalar([(5, 2), (5, 3), (6, 2), (6, 3)])
         times_gate(7, 0)
         gate_to_rows(7, 3)
-        output_rows_on_scalar([(5, 2), (5, 3), (6, 2), (6, 3)])
+        finish_on_scalar([(5, 2), (5, 3), (6, 2), (6, 3)])
         for t in range(1, GT):
             times_gate(7, t)
         plus_x(7)
         finish(6, (1,))
         squared_deviations2(7)
         rstd2_by_sqrt_scalar(7)
+        output_rows_on_scalar([(5, 2), (5, 3), (6, 2), (6, 3)])
         center_and_gain2(7, (0, 1, 2, 3))
         rstd2_by_sqrt_vector(7)
         scale_and_shift2(7, (0, 1, 2, 3))

@@ -28,14 +28,12 @@ JUNK_BUFS = 8
 SCALAR_BANKS = 4
 VECTOR_BANKS = 3
 ON_VECTOR = (0, 1)
-SUMS_ON_SCALAR = 3
+SUMS_ON_SCALAR = (2, 3)
 XH_FIRST = 2
-ENDS_ON_SCALAR = (4,)
+XHAT_ON_GPSIMD = (2, 3)
+DETOUR = {4: (2, 3)}
 BY_SQRT = 6
 FIRST_FIN = 2
-FIRST_N = 1
-SCALAR_RUNS_FIRST = 64
-SCALAR_RUNS = 112
 
 FLOPS = 2 * 2 * ROWS * D * D
 
@@ -217,7 +215,11 @@ def tile_mnelayer_pa_t_kernel(
             nc.gpsimd.tensor_tensor(
                 out=rstd1[:, tiles_of(g)], in0=var_eps1[:, tiles_of(g)], in1=minus_half[:], op=ALU.pow
             )
-            nc.gpsimd.tensor_tensor(
+            if g not in XHAT_ON_GPSIMD:
+                neg_mean_times_rstd1(nc.gpsimd, g)
+
+        def neg_mean_times_rstd1(engine, g):
+            engine.tensor_tensor(
                 out=neg_mean_rstd1[:, tiles_of(g)], in0=neg_mean1[:, tiles_of(g)], in1=rstd1[:, tiles_of(g)],
                 op=ALU.mult,
             )
@@ -230,6 +232,17 @@ def tile_mnelayer_pa_t_kernel(
             nc.gpsimd.tensor_tensor(
                 out=rstd2[:, tiles_of(g)], in0=var_eps2[:, tiles_of(g)], in1=minus_half[:], op=ALU.pow
             )
+
+        def xhat_on_gpsimd(g):
+            neg_mean_times_rstd1(nc.vector, g)
+            xhat = two.tile([P, GT, D], F32, name="xhat", tag="xhat")
+            of(g)["xhat"] = xhat
+            for t in range(GT):
+                i = g * GT + t
+                nc.gpsimd.tensor_scalar(
+                    out=xhat[:, t, :], in0=x_all[:, i, :], scalar1=rstd1[:, i : i + 1],
+                    scalar2=neg_mean_rstd1[:, i : i + 1], op0=ALU.mult, op1=ALU.add,
+                )
 
         def xhat_on_scalar(g):
             xhat = two.tile([P, GT, D], F32, name="xhat", tag="xhat")
@@ -293,7 +306,7 @@ def tile_mnelayer_pa_t_kernel(
             )
 
         def runs(g):
-            return SCALAR_RUNS_FIRST if g < 2 + FIRST_N else SCALAR_RUNS
+            return D // 4 - (D // 4 >> g - 1 if g < 6 else 0)
 
         def regrouped_views(planes):
             grouped = two.tile([P, D, PACK], BF16, name="grouped", tag="grouped", align_bytes=64)
@@ -582,10 +595,13 @@ def tile_mnelayer_pa_t_kernel(
             if exists(r + 4):
                 copy_x(r + 4, 0)
                 copy_x(r + 4, 1)
-                row_sums_on_tensor(r + 4)
+                if r + 4 in SUMS_ON_SCALAR:
+                    row_sums_on_scalar(r + 4)
+                else:
+                    row_sums_on_tensor(r + 4)
                 if r == -1:
-                    gate_pass(1, 0)
-                    gate_pass(1, 1)
+                    for c in range(CHUNKS):
+                        gate_pass(1, c)
             if exists(r + 2) and r >= 0:
                 for c in range(3):
                     gate_pass(r + 2, c)
@@ -608,36 +624,40 @@ def tile_mnelayer_pa_t_kernel(
                     minus_x(nc.vector, r + 1, t + 1, 1)
                 else:
                     minus_x(nc.gpsimd, r + 1, t, 2)
+            if r == 0 and 3 in XHAT_ON_GPSIMD:
+                xhat_on_gpsimd(3)
             if exists(r):
                 scales2(r)
             if r == -1:
                 regroup_on_vector_of(1)
                 quantise_xn(1)
+                if 2 in XHAT_ON_GPSIMD:
+                    xhat_on_gpsimd(2)
                 times_gate(0, 0)
                 gate_to_rows(0, 3)
                 for t in range(1, GT):
                     times_gate(0, t)
                     pre_pass(1, t - 1)
-                    if t == 1:
-                        gate_pass(1, 2)
-            if r == -1:
+            if r == -1 and 2 not in XHAT_ON_GPSIMD:
                 xhat_on_scalar(2)
             if exists(r + 4):
-                neg_mean1_from_tensor_sums(r + 4)
+                if r + 4 in SUMS_ON_SCALAR:
+                    neg_mean1_from_scalar_sums(r + 4)
+                else:
+                    neg_mean1_from_tensor_sums(r + 4)
                 squared_deviations1(r + 4, range(2))
             if exists(r + 2) and r >= 0:
                 for t in range(VECTOR_BANKS):
                     pre_pass(r + 2, t)
                 gate_pass(r + 2, 3)
-            if exists(r + 3) and r >= 0:
+            if exists(r + 3) and r >= 0 and r + 3 not in XHAT_ON_GPSIMD:
                 xhat_on_scalar(r + 3)
+            on_scalar = DETOUR.get(r - 1, ())
             if exists(r - 1):
                 finish(r - 1, range(FIRST_FIN))
             if exists(r + 2):
                 potential(r + 2, 0)
                 pre_pass(r + 2, VECTOR_BANKS)
-                if r == -1:
-                    gate_pass(1, 3)
                 for t in range(1, GT):
                     potential(r + 2, t)
                 store_potential(r + 2)
@@ -649,8 +669,8 @@ def tile_mnelayer_pa_t_kernel(
             if exists(r + 3):
                 for j in range(XH_FIRST):
                     transpose_xhat(r + 3, j)
-            if exists(r - 1) and r - 1 not in ENDS_ON_SCALAR:
-                finish(r - 1, range(FIRST_FIN, GT))
+            if exists(r - 1) and len(on_scalar) < 2:
+                finish(r - 1, [t for t in range(FIRST_FIN, GT) if t not in on_scalar])
             if exists(r + 4):
                 squared_deviations1(r + 4, range(2, GT))
             if exists(r + 1) and r >= 0:
@@ -658,9 +678,9 @@ def tile_mnelayer_pa_t_kernel(
                 gate_to_rows(r + 1, GT - 1)
                 for t in range(1, GT):
                     times_gate(r + 1, t)
-            if r - 1 in ENDS_ON_SCALAR:
-                finish_on_scalar([(r - 1, t) for t in range(FIRST_FIN, GT)])
-                output_rows_on_scalar([(r - 1, t) for t in range(FIRST_FIN, GT)])
+            if len(on_scalar) == 2:
+                finish_on_scalar([(r - 1, t) for t in on_scalar])
+                output_rows_on_scalar([(r - 1, t) for t in on_scalar])
             if exists(r + 3):
                 for j in range(XH_FIRST, PACK):
                     transpose_xhat(r + 3, j)
@@ -671,6 +691,9 @@ def tile_mnelayer_pa_t_kernel(
                     transpose_x(r + 5, j)
             if exists(r + 3):
                 regroup_on_scalar(r + 3)
+            if len(on_scalar) == 1:
+                finish_on_scalar([(r - 1, t) for t in on_scalar])
+                output_rows_on_scalar([(r - 1, t) for t in on_scalar])
             if r + 2 == LAST:
                 nc.scalar.activation(out=table_warmer[:, 1:2], in_=eps_col[:, 0:1], func=ACT.Sqrt)
 

from contextlib import ExitStack

import concourse.mybir as mybir
from concourse.masks import make_identity

F32 = mybir.dt.float32
BF16 = mybir.dt.bfloat16
U32 = mybir.dt.uint32
U8 = mybir.dt.uint8
FP8X4 = mybir.dt.float8_e4m3fn_x4
ALU = mybir.AluOpType
ACT = mybir.ActivationFunctionType

P = 128
ROWS = 4096
D = 512
TILES = ROWS // P
GT = 4
GROUPS = TILES // GT
LAST = GROUPS - 1
CHUNKS = D // P
PACK = 4
EPS = 1e-5
DECAY = 0.9
SLOPE = 0.01
SUM_COLS = 32
JUNK_BUFS = 8
SCALAR_BANKS = 4
VECTOR_BANKS = 3
ON_VECTOR = (0, 1)
SUMS_ON_SCALAR = (2, 3)
XH_FIRST = 2
XHAT_ON_GPSIMD = (2, 3)
DETOUR = {4: (2, 3)}
BY_SQRT = 6
FIRST_FIN = 2

FLOPS = 2 * 2 * ROWS * D * D


def tile_mnelayer_pa_t_kernel(
    tc, inputs, prev_potential, syn_weights, gate_W, gate_b, pre_gamma, pre_beta, ln_gamma, ln_beta, out_0, out_1
):
    nc = tc.nc
    with ExitStack() as ctx:
        ctx.enter_context(tc.manual_schedule())
        const = ctx.enter_context(tc.tile_pool(name="const", bufs=1))
        two = ctx.enter_context(tc.tile_pool(name="two", bufs=2))
        four = ctx.enter_context(tc.tile_pool(name="four", bufs=4))
        five = ctx.enter_context(tc.tile_pool(name="five", bufs=5))
        for_scalar = ctx.enter_context(tc.psum_pool(name="for_scalar", bufs=SCALAR_BANKS))
        for_vector = ctx.enter_context(tc.psum_pool(name="for_vector", bufs=VECTOR_BANKS))
        constants = ctx.enter_context(tc.psum_pool(name="constants", bufs=1))

        x_dram = inputs.rearrange("(p i) k -> p i k", i=TILES)
        prev_dram = prev_potential.rearrange("(p i) k -> p i k", i=TILES)
        out_dram = out_0.rearrange("(p i) k -> p i k", i=TILES)
        pot_dram = out_1.rearrange("(p i) k -> p i k", i=TILES)

        x_all = const.tile([P, TILES, D], BF16, name="x_all")
        prev_all = const.tile([P, TILES, D], BF16, name="prev_all")
        gate_w_rows = const.tile([P, CHUNKS, D], BF16, name="gate_w_rows")
        syn_rows = const.tile([P, PACK, D], BF16, name="syn_rows")
        vec_rows = const.tile([P, P], BF16, name="vec_rows")
        vec2_rows = const.tile([P, P], BF16, name="vec2_rows")
        ln_rows = const.tile([P, 2, D], BF16, name="ln_rows")
        vec_cols = const.tile([P, 2 * CHUNKS], F32, name="vec_cols")
        vec2_cols = const.tile([P, 3 * CHUNKS], F32, name="vec2_cols")
        minus_half = const.tile([P, GT], F32, name="minus_half")
        eps_col = const.tile([P, 1], F32, name="eps_col")
        ones = const.tile([P, P], BF16, name="ones")
        ident = const.tile([P, P], F32, name="ident")
        ident_bf = const.tile([P, P], BF16, name="ident_bf")
        junk = const.tile([P, JUNK_BUFS, D], BF16, name="junk")
        junk_turn = [0]
        syn_codes = const.tile([P, D], U32, name="syn_codes", align_bytes=64)
        syn_scales = const.tile([P, D], U8, name="syn_scales", align_bytes=64)
        gate_codes = const.tile([P, D], U32, name="gate_codes", align_bytes=64)
        gate_scales = const.tile([P, D], U8, name="gate_scales", align_bytes=64)
        bn6 = const.tile([P, len(ON_VECTOR) * GT, 6], F32, name="bn6")
        mean_var1 = const.tile([P, len(ON_VECTOR) * GT, 2], F32, name="mean_var1")
        sum1 = const.tile([P, GT], F32, name="sum1")
        neg_mean1 = const.tile([P, TILES], F32, name="neg_mean1")
        sq_dev1 = const.tile([P, TILES], F32, name="sq_dev1")
        var_eps1 = const.tile([P, TILES], F32, name="var_eps1")
        rstd1 = const.tile([P, TILES], F32, name="rstd1")
        var_eps2 = const.tile([P, TILES], F32, name="var_eps2")
        rstd2 = const.tile([P, TILES], F32, name="rstd2")
        neg_mean_rstd1 = const.tile([P, TILES], F32, name="neg_mean_rstd1")
        sum2 = const.tile([P, TILES], F32, name="sum2")
        neg_mean2 = const.tile([P, TILES], F32, name="neg_mean2")
        sq_dev2 = const.tile([P, TILES], F32, name="sq_dev2")
        std1 = const.tile([P, len(ON_VECTOR) * GT], F32, name="std1")
        std2 = const.tile([P, 2 * GT], F32, name="std2")
        neg_mean_rstd2 = const.tile([P, TILES], F32, name="neg_mean_rstd2")
        table_warmer = const.tile([P, 2], F32, name="table_warmer")

        def tiles_of(g):
            return slice(g * GT, (g + 1) * GT)

        def exists(g):
            return 0 <= g < GROUPS

        nc.vector.memset(vec_rows[:], 0.0)
        nc.vector.memset(vec2_rows[:], 0.0)
        nc.vector.memset(minus_half[:], -0.5)
        nc.vector.memset(eps_col[:], EPS)
        nc.vector.memset(ones[:], 1.0)
        for a, vec in enumerate((pre_gamma, pre_beta)):
            nc.scalar.dma_start(out=vec_rows[a * CHUNKS : (a + 1) * CHUNKS, :], in_=vec.rearrange("(j p) -> j p", p=P))
        nc.scalar.activation(out=table_warmer[:, 0:1], in_=eps_col[:, 0:1], func=ACT.Sqrt)
        make_identity(nc, ident[:])
        make_identity(nc, ident_bf[:])
        nc.gpsimd.memset(ln_rows[:], 0.0)

        def load_x(g):
            nc.sync.dma_start(out=x_all[:, tiles_of(g), :], in_=x_dram[:, tiles_of(g), :])

        def load_prev(g):
            nc.sync.dma_start(out=prev_all[:, tiles_of(g), :], in_=prev_dram[:, tiles_of(g), :])

        nc.sync.dma_start(out=x_all[:, 0:2, :], in_=x_dram[:, 0:2, :])
        nc.sync.dma_start(out=x_all[:, 2:4, :], in_=x_dram[:, 2:4, :])
        load_x(1)
        nc.sync.dma_start(out=gate_w_rows[:], in_=gate_W.rearrange("(c m) k -> m c k", m=P))
        load_x(2)
        nc.sync.dma_start(out=syn_rows[:], in_=syn_weights.rearrange("(j p) n -> p j n", p=P))
        load_prev(0)
        for a, vec in enumerate((gate_b, ln_gamma, ln_beta)):
            nc.sync.dma_start(out=vec2_rows[a * CHUNKS : (a + 1) * CHUNKS, :], in_=vec.rearrange("(j p) -> j p", p=P))
        for a, vec in enumerate((ln_gamma, ln_beta)):
            nc.sync.dma_start(out=ln_rows[0:1, a, :], in_=vec.rearrange("(a n) -> a n", a=1))
        load_x(3)
        load_x(4)
        load_prev(1)
        load_x(5)
        load_prev(2)
        load_x(6)
        load_prev(3)
        load_x(7)
        for g in range(4, GROUPS):
            load_prev(g)

        held = {}

        def of(g):
            if g not in held:
                held[g] = {}
            return held[g]

        def junk_out():
            junk_turn[0] = (junk_turn[0] + 1) % JUNK_BUFS
            return junk[:, junk_turn[0], :]

        def stats1_on_vector(g):
            for t in range(GT + 1):
                i = g * GT + t
                if t < GT:
                    nc.vector.bn_stats(out=bn6[:, i, :], in_=x_all[:, i, :])
                if t > 0:
                    nc.vector.bn_aggr(out=mean_var1[:, i - 1, :], in_=bn6[:, i - 1, :])

        def std1_on_scalar(g):
            nc.scalar.activation(
                out=std1[:, tiles_of(g)], in_=mean_var1[:, tiles_of(g), 1], func=ACT.Sqrt, bias=eps_col[:, 0:1]
            )

        def xhat_on_vector(g):
            nc.vector.reciprocal(out=rstd1[:, tiles_of(g)], in_=std1[:, tiles_of(g)])
            xhat = two.tile([P, GT, D], F32, name="xhat", tag="xhat")
            of(g)["xhat"] = xhat
            for t in range(GT):
                i = g * GT + t
                nc.vector.tensor_scalar(
                    out=xhat[:, t, :], in0=x_all[:, i, :], scalar1=mean_var1[:, i, 0:1], scalar2=rstd1[:, i : i + 1],
                    op0=ALU.subtract, op1=ALU.mult,
                )

        def row_sums_on_scalar(g):
            for t in range(GT):
                nc.scalar.activation(
                    out=junk_out(), in_=x_all[:, g * GT + t, :], func=ACT.Identity, accum_out=sum1[:, t : t + 1]
                )

        def neg_mean1_from_scalar_sums(g):
            nc.scalar.mul(out=neg_mean1[:, tiles_of(g)], in_=sum1[:], mul=-1.0 / D)

        def row_sums_on_tensor(g):
            sums = for_scalar.tile([P, GT, SUM_COLS], F32, name="sums", tag="bank")
            x_t = of(g)["x_t"][:].rearrange("p (n v) -> p n v", v=PACK)
            for t in range(GT):
                for v in range(PACK):
                    nc.tensor.matmul(
                        out=sums[:, t, :], lhsT=x_t[:, t * P : (t + 1) * P, v], rhs=ones[:, 0:SUM_COLS],
                        start=(v == 0), stop=(v == PACK - 1),
                    )
            of(g)["sums"] = sums

        def neg_mean1_from_tensor_sums(g):
            nc.scalar.mul(out=neg_mean1[:, tiles_of(g)], in_=of(g)["sums"][:, :, 0], mul=-1.0 / D)

        def squared_deviations1(g, tiles=range(GT)):
            for t in tiles:
                i = g * GT + t
                nc.scalar.activation(
                    out=junk_out(), in_=x_all[:, i, :], func=ACT.Square, bias=neg_mean1[:, i : i + 1],
                    accum_out=sq_dev1[:, i : i + 1],
                )

        def scales1(g):
            nc.gpsimd.tensor_scalar(
                out=var_eps1[:, tiles_of(g)], in0=sq_dev1[:, tiles_of(g)], scalar1=1.0 / D, scalar2=EPS,
                op0=ALU.mult, op1=ALU.add,
            )
            nc.gpsimd.tensor_tensor(
                out=rstd1[:, tiles_of(g)], in0=var_eps1[:, tiles_of(g)], in1=minus_half[:], op=ALU.pow
            )
            if g not in XHAT_ON_GPSIMD:
                neg_mean_times_rstd1(nc.gpsimd, g)

        def neg_mean_times_rstd1(engine, g):
            engine.tensor_tensor(
                out=neg_mean_rstd1[:, tiles_of(g)], in0=neg_mean1[:, tiles_of(g)], in1=rstd1[:, tiles_of(g)],
                op=ALU.mult,
            )

        def scales2(g):
            nc.gpsimd.tensor_scalar(
                out=var_eps2[:, tiles_of(g)], in0=sq_dev2[:, tiles_of(g)], scalar1=1.0 / D**3, scalar2=EPS,
                op0=ALU.mult, op1=ALU.add,
            )
            nc.gpsimd.tensor_tensor(
                out=rstd2[:, tiles_of(g)], in0=var_eps2[:, tiles_of(g)], in1=minus_half[:], op=ALU.pow
            )

        def xhat_on_gpsimd(g):
            neg_mean_times_rstd1(nc.vector, g)
            xhat = two.tile([P, GT, D], F32, name="xhat", tag="xhat")
            of(g)["xhat"] = xhat
            for t in range(GT):
                i = g * GT + t
                nc.gpsimd.tensor_scalar(
                    out=xhat[:, t, :], in0=x_all[:, i, :], scalar1=rstd1[:, i : i + 1],
                    scalar2=neg_mean_rstd1[:, i : i + 1], op0=ALU.mult, op1=ALU.add,
                )

        def xhat_on_scalar(g):
            xhat = two.tile([P, GT, D], F32, name="xhat", tag="xhat")
            of(g)["xhat"] = xhat
            for t in range(GT):
                i = g * GT + t
                nc.scalar.activation(
                    out=xhat[:, t, :], in_=x_all[:, i, :], func=ACT.Identity,
                    scale=rstd1[:, i : i + 1], bias=neg_mean_rstd1[:, i : i + 1],
                )

        def transpose_words(rows, h):
            bank = for_scalar.tile([P, 2, 2 * P], F32, name="word_bank", tag="bank")
            for t in range(2):
                words = rows[:, 2 * h + t, :].bitcast(F32)
                for u in range(2):
                    nc.tensor.transpose(bank[:, u, t * P : (t + 1) * P], words[:, u * P : (u + 1) * P], ident[:])
            return bank

        def copy_words(bank, dst, h):
            nc.scalar.copy(
                out=dst[:].bitcast(F32).rearrange("p (n u) -> p n u", u=2)[:, h * 2 * P : (h + 1) * 2 * P, :],
                in_=bank[:].rearrange("p u n -> p n u"),
            )

        def transpose_x(g, h):
            of(g)["word_bank%d" % h] = transpose_words(x_all[:, tiles_of(g), :], h)

        def copy_x(g, h):
            s = of(g)
            if h == 0:
                x_t = four.tile([P, PACK * D], BF16, name="x_t", tag="x_t", align_bytes=64)
                s["x_t"] = x_t
            copy_words(s["word_bank%d" % h], s["x_t"], h)

        def quantise(codes, scales, values):
            nc.vector.quantize_mx(out=codes.bitcast(FP8X4), scales=scales, in_=values)

        def quantise_x(g):
            s = of(g)
            x_codes = five.tile([P, D], U32, name="x_codes", tag="x_codes", align_bytes=64)
            x_scales = five.tile([P, D], U8, name="x_scales", tag="x_scales", align_bytes=64)
            quantise(x_codes[:], x_scales[:], s["x_t"][:])
            s["x_codes"], s["x_scales"] = x_codes, x_scales

        def transpose_xhat(g, j):
            s = of(g)
            bank = for_scalar.tile([P, D], F32, name="xhat_bank", tag="bank")
            for t in range(GT):
                nc.tensor.transpose(bank[:, t * P : (t + 1) * P], s["xhat"][:, t, j * P : (j + 1) * P], ident[:])
            s["xhat_bank%d" % j] = bank

        def gain_and_shift1(g, j):
            s = of(g)
            if j == 0:
                xn_planes = two.tile([P, PACK, D], BF16, name="xn_planes", tag="xn_planes")
                s["xn_planes"] = xn_planes
            nc.scalar.activation(
                out=s["xn_planes"][:, j, :], in_=s["xhat_bank%d" % j][:], func=ACT.Identity,
                scale=vec_cols[:, j : j + 1], bias=vec_cols[:, CHUNKS + j : CHUNKS + j + 1],
            )

        def runs(g):
            return D // 4 - (D // 4 >> g - 1 if g < 6 else 0)

        def regrouped_views(planes):
            grouped = two.tile([P, D, PACK], BF16, name="grouped", tag="grouped", align_bytes=64)
            return (
                grouped,
                grouped[:].rearrange("p (n i) j -> p n j i", i=4),
                planes.rearrange("p j (n i) -> p n j i", i=4),
            )

        def regroup_on_vector(planes):
            grouped, dst, src = regrouped_views(planes)
            nc.vector.tensor_copy(out=dst, in_=src)
            return grouped

        def regroup_on_gpsimd(planes):
            grouped, dst, src = regrouped_views(planes)
            nc.gpsimd.tensor_scalar(out=dst, in0=src, scalar1=1.0, scalar2=0.0, op0=ALU.mult, op1=ALU.add)
            return grouped

        def regroup_on_scalar(g):
            s = of(g)
            s["grouped"], s["regroup_to"], s["regroup_from"] = regrouped_views(s["xn_planes"][:])
            nc.scalar.copy(out=s["regroup_to"][:, 0 : runs(g)], in_=s["regroup_from"][:, 0 : runs(g)])

        def regroup_on_vector_of(g):
            s = of(g)
            if g in ON_VECTOR:
                s["grouped"] = regroup_on_vector(s["xn_planes"][:])
            elif runs(g) < D // 4:
                nc.vector.tensor_copy(out=s["regroup_to"][:, runs(g) :], in_=s["regroup_from"][:, runs(g) :])

        def quantise_xn(g):
            s = of(g)
            xn_codes = two.tile([P, D], U32, name="xn_codes", tag="xn_codes", align_bytes=64)
            xn_scales = two.tile([P, D], U8, name="xn_scales", tag="xn_scales", align_bytes=64)
            quantise(xn_codes[:], xn_scales[:], s["grouped"][:].rearrange("p n j -> p (n j)"))
            s["xn_codes"], s["xn_scales"] = xn_codes, xn_scales

        def pre_pass(g, t):
            s = of(g)
            bank = for_vector.tile([P, D], F32, name="pre_bank", tag="bank")
            nc.tensor.matmul_mx(
                out=bank[:],
                lhsT=s["xn_codes"][:, t * P : (t + 1) * P].bitcast(FP8X4),
                lhsT_scale=s["xn_scales"][:, t * P : (t + 1) * P],
                rhs=syn_codes[:].bitcast(FP8X4),
                rhs_scale=syn_scales[:],
                start=True,
                stop=True,
            )
            s["pre_bank%d" % t] = bank

        def gate_pass(g, c):
            s = of(g)
            bank = for_scalar.tile([P, D], F32, name="gate_t_bank", tag="bank")
            nc.tensor.matmul_mx(
                out=bank[:],
                lhsT=gate_codes[:, c * P : (c + 1) * P].bitcast(FP8X4),
                lhsT_scale=gate_scales[:, c * P : (c + 1) * P],
                rhs=s["x_codes"][:].bitcast(FP8X4),
                rhs_scale=s["x_scales"][:],
                start=True,
                stop=True,
            )
            s["gate_t_bank%d" % c] = bank

        def sigmoid(g, c):
            s = of(g)
            if c == 0:
                gate_t = two.tile([P, CHUNKS, D], F32, name="gate_t", tag="gate_t")
                s["gate_t"] = gate_t
            nc.scalar.activation(
                out=s["gate_t"][:, c, :], in_=s["gate_t_bank%d" % c][:], func=ACT.Sigmoid,
                bias=vec2_cols[:, c : c + 1],
            )

        def gate_to_rows(g, t):
            s = of(g)
            bank = for_vector.tile([P, D], F32, name="gate_bank", tag="bank")
            for c in range(CHUNKS):
                nc.tensor.transpose(bank[:, c * P : (c + 1) * P], s["gate_t"][:, c, t * P : (t + 1) * P], ident[:])
            s["gate_bank%d" % t] = bank

        def potential(g, t):
            s = of(g)
            if t == 0:
                pot = two.tile([P, GT, D], F32, name="pot", tag="pot")
                s["pot"] = pot
            nc.vector.scalar_tensor_tensor(
                out=s["pot"][:, t, :], in0=prev_all[:, g * GT + t, :], scalar=DECAY, in1=s["pre_bank%d" % t][:],
                op0=ALU.mult, op1=ALU.add,
            )

        def store_potential(g):
            nc.sync.dma_start(out=pot_dram[:, tiles_of(g), :], in_=of(g)["pot"][:])

        def leaky_relu(g, tiles=slice(0, GT)):
            s = of(g)
            if "res" not in s:
                res = four.tile([P, GT, D], F32, name="res", tag="res")
                s["res"] = res
            pot = s["pot"][:, tiles, :].rearrange("p t n -> p (t n)")
            act = s["res"][:, tiles, :].rearrange("p t n -> p (t n)")
            nc.vector.scalar_tensor_tensor(out=act, in0=pot, scalar=SLOPE, in1=pot, op0=ALU.mult, op1=ALU.max)

        def minus_x(engine, g, first, count):
            i = g * GT + first
            res = of(g)["res"][:, first : first + count, :]
            engine.tensor_tensor(out=res, in0=res, in1=x_all[:, i : i + count, :], op=ALU.subtract)

        def times_gate(g, t):
            s = of(g)
            nc.vector.tensor_tensor(
                out=s["res"][:, t, :], in0=s["res"][:, t, :], in1=s["gate_bank%d" % t][:], op=ALU.mult
            )

        def plus_x(g):
            s = of(g)
            for t in range(GT):
                i = g * GT + t
                nc.vector.scalar_tensor_tensor(
                    out=s["res"][:, t, :], in0=s["res"][:, t, :], scalar=1.0, in1=x_all[:, i, :],
                    op0=ALU.mult, op1=ALU.add, accum_out=sum2[:, i : i + 1],
                )

        def squared_deviations2(g):
            for t in range(GT):
                i = g * GT + t
                if t == GT - 1:
                    nc.scalar.mul(out=neg_mean2[:, tiles_of(g)], in_=sum2[:, tiles_of(g)], mul=-1.0 / D)
                nc.scalar.activation(
                    out=junk_out(), in_=of(g)["res"][:, t, :], func=ACT.Square, scale=-float(D), bias=sum2[:, i : i + 1],
                    accum_out=sq_dev2[:, i : i + 1],
                )

        def sqrt_cols(g):
            return slice((g - BY_SQRT) * GT, (g - BY_SQRT + 1) * GT)

        def rstd2_by_sqrt_scalar(g):
            nc.scalar.activation(
                out=std2[:, sqrt_cols(g)], in_=sq_dev2[:, tiles_of(g)], func=ACT.Sqrt, scale=1.0 / D**3,
                bias=eps_col[:, 0:1],
            )

        def rstd2_by_sqrt_vector(g):
            nc.vector.reciprocal(out=rstd2[:, tiles_of(g)], in_=std2[:, sqrt_cols(g)])

        def finish(g, tiles):
            center_and_gain2(g, tiles)
            scale_and_shift2(g, tiles)

        def center_and_gain2(g, tiles):
            s = of(g)
            for t in tiles:
                i = g * GT + t
                nc.vector.scalar_tensor_tensor(
                    out=s["res"][:, t, :], in0=s["res"][:, t, :], scalar=neg_mean2[:, i : i + 1], in1=gain_shift2[:, 0, :],
                    op0=ALU.add, op1=ALU.mult,
                )

        def scale_and_shift2(g, tiles):
            s = of(g)
            for t in tiles:
                i = g * GT + t
                nc.vector.scalar_tensor_tensor(
                    out=s["res"][:, t, :], in0=s["res"][:, t, :], scalar=rstd2[:, i : i + 1], in1=gain_shift2[:, 1, :],
                    op0=ALU.mult, op1=ALU.add,
                )
                if g == LAST:
                    nc.sync.dma_start(out=out_dram[:, i, :], in_=s["res"][:, t, :])
            if g < LAST:
                i0 = g * GT
                nc.sync.dma_start(
                    out=out_dram[:, i0 + tiles[0] : i0 + tiles[-1] + 1, :], in_=s["res"][:, tiles[0] : tiles[-1] + 1, :]
                )

        def finish_on_scalar(row_tiles):
            n = len(row_tiles) * P
            for g, t in row_tiles:
                i = g * GT + t
                nc.scalar.activation(
                    out=neg_mean_rstd2[:, i : i + 1], in_=neg_mean2[:, i : i + 1], func=ACT.Identity,
                    scale=rstd2[:, i : i + 1],
                )
                nc.scalar.activation(
                    out=of(g)["res"][:, t, :], in_=of(g)["res"][:, t, :], func=ACT.Identity,
                    scale=rstd2[:, i : i + 1], bias=neg_mean_rstd2[:, i : i + 1],
                )
            out_t = two.tile([P, CHUNKS, D], F32, name="out_t", tag="gate_t")
            of(row_tiles[0][0])["out_t"] = out_t
            banks = []
            for c in range(CHUNKS):
                bank = for_scalar.tile([P, D], F32, name="res_bank", tag="bank")
                for k, (g, t) in enumerate(row_tiles):
                    nc.tensor.transpose(
                        bank[:, k * P : (k + 1) * P], of(g)["res"][:, t, c * P : (c + 1) * P], ident[:]
                    )
                banks.append(bank)
            for c in range(CHUNKS):
                nc.scalar.activation(
                    out=out_t[:, c, 0:n], in_=banks[c][:, 0:n], func=ACT.Identity,
                    scale=vec2_cols[:, CHUNKS + c : CHUNKS + c + 1],
                    bias=vec2_cols[:, 2 * CHUNKS + c : 2 * CHUNKS + c + 1],
                )

        def output_rows_on_scalar(row_tiles):
            out_t = of(row_tiles[0][0])["out_t"]
            for k, (g, t) in enumerate(row_tiles):
                bank = for_scalar.tile([P, D], F32, name="out_bank", tag="bank")
                for c in range(CHUNKS):
                    nc.tensor.transpose(bank[:, c * P : (c + 1) * P], out_t[:, c, k * P : (k + 1) * P], ident[:])
                nc.scalar.copy(out=of(g)["res"][:, t, :], in_=bank[:])
                nc.sync.dma_start(out=out_dram[:, g * GT + t, :], in_=of(g)["res"][:, t, :])

        gain_shift2 = constants.tile([P, 2, D], BF16, name="gain_shift2")

        def second_norm_constants():
            for a in range(2):
                nc.tensor.matmul(out=gain_shift2[:, a, :], lhsT=ones[:], rhs=ln_rows[:, a, :], start=True, stop=True)

        syn_grouped = regroup_on_gpsimd(syn_rows[:])
        transpose_x(0, 0)
        transpose_x(0, 1)
        transpose_x(1, 0)
        transpose_x(1, 1)
        stats1_on_vector(0)
        copy_x(0, 0)
        copy_x(0, 1)
        copy_x(1, 0)
        std1_on_scalar(0)
        copy_x(1, 1)
        vec_bank = for_scalar.tile([P, P], BF16, name="vec_bank", tag="bank")
        nc.tensor.transpose(vec_bank[:], vec_rows[:], ident_bf[:])
        gate_w_t = four.tile([P, PACK * D], BF16, name="gate_w_t", tag="x_t", align_bytes=64)
        gate_w_bank0 = transpose_words(gate_w_rows[:], 0)
        gate_w_bank1 = transpose_words(gate_w_rows[:], 1)
        nc.scalar.copy(out=vec_cols[:], in_=vec_bank[:, 0 : 2 * CHUNKS])
        copy_words(gate_w_bank0, gate_w_t, 0)
        copy_words(gate_w_bank1, gate_w_t, 1)
        xhat_on_vector(0)
        for j in range(PACK):
            transpose_xhat(0, j)
        quantise_x(0)
        stats1_on_vector(1)
        for j in range(PACK):
            gain_and_shift1(0, j)
            if j < 2:
                transpose_x(2, j)
        vec2_bank = for_scalar.tile([P, P], BF16, name="vec2_bank", tag="bank")
        nc.tensor.transpose(vec2_bank[:], vec2_rows[:], ident_bf[:])
        regroup_on_vector_of(0)
        quantise_xn(0)
        quantise(syn_codes[:], syn_scales[:], syn_grouped[:].rearrange("p n j -> p (n j)"))
        quantise(gate_codes[:], gate_scales[:], gate_w_t[:])
        for t in range(VECTOR_BANKS):
            pre_pass(0, t)
        copy_x(2, 0)
        copy_x(2, 1)
        std1_on_scalar(1)
        nc.scalar.copy(out=vec2_cols[:], in_=vec2_bank[:, 0 : 3 * CHUNKS])
        xhat_on_vector(1)
        nc.scalar.activation(out=table_warmer[:, 1:2], in_=eps_col[:, 0:1], func=ACT.Sigmoid)
        row_sums_on_scalar(2)
        neg_mean1_from_scalar_sums(2)
        squared_deviations1(2)
        for j in range(PACK):
            transpose_xhat(1, j)
        potential(0, 0)
        pre_pass(0, 3)
        quantise_x(1)
        for t in range(1, GT):
            potential(0, t)
        store_potential(0)
        second_norm_constants()
        for j in range(PACK):
            gain_and_shift1(1, j)
            gate_pass(0, j)
        for c in range(CHUNKS):
            sigmoid(0, c)
            if c < 2:
                transpose_x(3, c)
        for t in range(VECTOR_BANKS):
            gate_to_rows(0, t)

        def round_of_pipeline(r):
            if exists(r + 4):
                copy_x(r + 4, 0)
                copy_x(r + 4, 1)
                if r + 4 in SUMS_ON_SCALAR:
                    row_sums_on_scalar(r + 4)
                else:
                    row_sums_on_tensor(r + 4)
                if r == -1:
                    for c in range(CHUNKS):
                        gate_pass(1, c)
            if exists(r + 2) and r >= 0:
                for c in range(3):
                    gate_pass(r + 2, c)
            if exists(r):
                plus_x(r)
                squared_deviations2(r)
            if exists(r + 3):
                quantise_x(r + 3)
            if exists(r + 2) and r >= 0:
                regroup_on_vector_of(r + 2)
            if exists(r + 1):
                leaky_relu(r + 1)
            if exists(r + 2) and r >= 0:
                quantise_xn(r + 2)
            if exists(r + 3):
                scales1(r + 3)
            for t in range(0, GT, 2):
                if r + 1 < 2:
                    minus_x(nc.vector, r + 1, t, 1)
                    minus_x(nc.vector, r + 1, t + 1, 1)
                else:
                    minus_x(nc.gpsimd, r + 1, t, 2)
            if r == 0 and 3 in XHAT_ON_GPSIMD:
                xhat_on_gpsimd(3)
            if exists(r):
                scales2(r)
            if r == -1:
                regroup_on_vector_of(1)
                quantise_xn(1)
                if 2 in XHAT_ON_GPSIMD:
                    xhat_on_gpsimd(2)
                times_gate(0, 0)
                gate_to_rows(0, 3)
                for t in range(1, GT):
                    times_gate(0, t)
                    pre_pass(1, t - 1)
            if r == -1 and 2 not in XHAT_ON_GPSIMD:
                xhat_on_scalar(2)
            if exists(r + 4):
                if r + 4 in SUMS_ON_SCALAR:
                    neg_mean1_from_scalar_sums(r + 4)
                else:
                    neg_mean1_from_tensor_sums(r + 4)
                squared_deviations1(r + 4, range(2))
            if exists(r + 2) and r >= 0:
                for t in range(VECTOR_BANKS):
                    pre_pass(r + 2, t)
                gate_pass(r + 2, 3)
            if exists(r + 3) and r >= 0 and r + 3 not in XHAT_ON_GPSIMD:
                xhat_on_scalar(r + 3)
            on_scalar = DETOUR.get(r - 1, ())
            if exists(r - 1):
                finish(r - 1, range(FIRST_FIN))
            if exists(r + 2):
                potential(r + 2, 0)
                pre_pass(r + 2, VECTOR_BANKS)
                for t in range(1, GT):
                    potential(r + 2, t)
                store_potential(r + 2)
                for c in range(CHUNKS):
                    sigmoid(r + 2, c)
            if exists(r + 1) and r >= 0:
                for t in range(GT - 1):
                    gate_to_rows(r + 1, t)
            if exists(r + 3):
                for j in range(XH_FIRST):
                    transpose_xhat(r + 3, j)
            if exists(r - 1) and len(on_scalar) < 2:
                finish(r - 1, [t for t in range(FIRST_FIN, GT) if t not in on_scalar])
            if exists(r + 4):
                squared_deviations1(r + 4, range(2, GT))
            if exists(r + 1) and r >= 0:
                times_gate(r + 1, 0)
                gate_to_rows(r + 1, GT - 1)
                for t in range(1, GT):
                    times_gate(r + 1, t)
            if len(on_scalar) == 2:
                finish_on_scalar([(r - 1, t) for t in on_scalar])
                output_rows_on_scalar([(r - 1, t) for t in on_scalar])
            if exists(r + 3):
                for j in range(XH_FIRST, PACK):
                    transpose_xhat(r + 3, j)
            for j in range(PACK):
                if exists(r + 3):
                    gain_and_shift1(r + 3, j)
                if j < 2 and exists(r + 5):
                    transpose_x(r + 5, j)
            if exists(r + 3):
                regroup_on_scalar(r + 3)
            if len(on_scalar) == 1:
                finish_on_scalar([(r - 1, t) for t in on_scalar])
                output_rows_on_scalar([(r - 1, t) for t in on_scalar])
            if r + 2 == LAST:
                nc.scalar.activation(out=table_warmer[:, 1:2], in_=eps_col[:, 0:1], func=ACT.Sqrt)

        for r in range(-1, LAST - 1):
            round_of_pipeline(r)

        plus_x(6)
        squared_deviations2(6)
        rstd2_by_sqrt_scalar(6)
        leaky_relu(7, slice(3, 4))
        leaky_relu(7, slice(0, 3))
        minus_x(nc.gpsimd, 7, 0, 2)
        minus_x(nc.gpsimd, 7, 2, 1)
        minus_x(nc.vector, 7, 3, 1)
        finish(5, (0, 1))
        rstd2_by_sqrt_vector(6)
        finish(6, (0,))
        for t in range(3):
            gate_to_rows(7, t)
        times_gate(7, 0)
        gate_to_rows(7, 3)
        finish_on_scalar([(5, 2), (5, 3), (6, 2), (6, 3)])
        for t in range(1, GT):
            times_gate(7, t)
        plus_x(7)
        finish(6, (1,))
        squared_deviations2(7)
        rstd2_by_sqrt_scalar(7)
        output_rows_on_scalar([(5, 2), (5, 3), (6, 2), (6, 3)])
        center_and_gain2(7, (0, 1, 2, 3))
        rstd2_by_sqrt_vector(7)
        scale_and_shift2(7, (0, 1, 2, 3))
